import numpy as np
import ml_dtypes


def mxq(x, axis, fmt="e4m3"):
    dtype, down = {"e4m3": (ml_dtypes.float8_e4m3fn, 7), "e5m2": (ml_dtypes.float8_e5m2, 14)}[fmt]
    v = np.moveaxis(np.asarray(x, np.float32).astype(ml_dtypes.bfloat16).astype(np.float64), axis, -1)
    blocks = v.reshape(v.shape[:-1] + (-1, 32))
    amax = np.abs(blocks).max(-1, keepdims=True)
    byte = np.maximum(np.where(amax > 0, np.frexp(amax)[1] - 1 + 127, 0) - down, 1)
    scale = np.exp2(byte - 127.0)
    codes = (blocks / scale).astype(np.float32).astype(dtype).astype(np.float64)
    return np.moveaxis((codes * scale).reshape(v.shape), -1, axis)


WIDE = False


def mx_kscale(k):
    if not WIDE:
        return np.ones(k)
    levels = np.array([10, -10, 5, -5, 0])
    a = np.random.permutation(np.resize(levels, k // 512 * 4)).reshape(k // 512, 4)
    idx = np.arange(k)
    return np.exp2(a[idx // 512, idx % 128 // 32])


BF16 = ml_dtypes.bfloat16


def bf(x):
    return np.asarray(x, np.float32).astype(BF16)


def f64(x):
    return np.asarray(x).astype(np.float64)


B, N, D, F, L = 32, 16, 512, 1024, 2
EPS = 1e-5


def layer_norm(x, gamma, beta):
    mu = x.mean(-1, keepdims=True)
    var = np.square(x - mu).mean(-1, keepdims=True)
    return (x - mu) / np.sqrt(var + EPS) * gamma + beta


def setup_inputs():
    t = mx_kscale(F)
    return {
        "h": bf(np.random.standard_normal((B, N, D))),
        "adj_mask": bf(np.random.random((B, N, N)) < 0.5),
        "w1a": bf(np.random.standard_normal((D, F)) * 0.7 / np.sqrt(D) * t),
        "w1b": bf(np.random.standard_normal((D, F)) * 0.7 / np.sqrt(D) * t),
        "b1": bf(np.random.standard_normal(F) * 0.3 * t),
        "w2": bf(np.random.standard_normal((F, D)) * 1.5 / np.sqrt(F) / t[:, None]),
        "b2": bf(np.random.standard_normal(D) * 0.3),
        "gamma": bf(1.0 + 0.1 * np.random.standard_normal(D)),
        "beta": bf(0.1 * np.random.standard_normal(D)),
    }


def reference(h, adj_mask, w1a, w1b, b1, w2, b2, gamma, beta):
    h = f64(h)
    hq = mxq(h.reshape(B * N, D), 1, "e4m3")
    a = (hq @ mxq(f64(w1a), 0, "e4m3")).reshape(B, N, 1, F)
    b = (hq @ mxq(f64(w1b), 0, "e4m3")).reshape(B, 1, N, F)
    z = np.maximum(a + b + f64(b1), 0.0)
    m = (mxq(z, 3, "e4m3") @ mxq(f64(w2), 0, "e4m3")) + f64(b2)
    m = m * f64(adj_mask)[..., None]
    msg = m.reshape(B * N, N, D).sum(axis=1).reshape(B, N, D) * (1.0 / N)
    return layer_norm(h + msg, f64(gamma), f64(beta))

@@ -1,0 +1,316 @@
+from contextlib import ExitStack
+
+import concourse.mybir as mybir
+from concourse.masks import make_identity
+
+F32 = mybir.dt.float32
+BF16 = mybir.dt.bfloat16
+U32 = mybir.dt.uint32
+U8 = mybir.dt.uint8
+FP8X4 = mybir.dt.float8_e4m3fn_x4
+ALU = mybir.AluOpType
+ACT = mybir.ActivationFunctionType
+AX = mybir.AxisListType
+
+P = 128
+NODES = 16
+D = 512
+F = 1024
+ROWS = 512
+CHUNKS = 4
+EPS = 1e-5
+FLOPS = 2 * ROWS * D * F * 2 + 2 * ROWS * NODES * F * D
+
+T_CHUNKS = ()
+A_CHUNKS = tuple(r for r in range(CHUNKS) if r not in T_CHUNKS)
+PRE_BUFS = 3
+M_BUFS = 5
+
+
+def tile_simplegnn_pa_t_kernel(tc, h, adj_mask, w1a, w1b, b1, w2, b2, gamma, beta, out):
+    nc = tc.nc
+    h_flat = h.flatten_outer_dims()
+    adj_flat = adj_mask.flatten_outer_dims()
+    out_flat = out.flatten_outer_dims()
+    n_a = len(A_CHUNKS) * P
+
+    with ExitStack() as ctx:
+        const = ctx.enter_context(tc.tile_pool(name="const", bufs=1))
+        stage = ctx.enter_context(tc.tile_pool(name="stage", bufs=2))
+        zpool = ctx.enter_context(tc.tile_pool(name="zpool", bufs=4))
+        small = ctx.enter_context(tc.tile_pool(name="small", bufs=4))
+        pre_pool = ctx.enter_context(tc.psum_pool(name="pre", bufs=PRE_BUFS))
+        m_pool = ctx.enter_context(tc.psum_pool(name="m", bufs=M_BUFS))
+
+        h_sb = const.tile([P, CHUNKS, D], BF16)
+        nc.sync.dma_start(out=h_sb[:], in_=h_flat.rearrange("(r p) d -> p r d", p=P))
+        raw1 = {}
+        for o, w in (("a", w1a), ("b", w1b)):
+            raw1[o] = const.tile([P, 4, F], BF16, name="raw1" + o)
+            for u in range(2):
+                nc.sync.dma_start(
+                    out=raw1[o][:, 2 * u : 2 * u + 2, :],
+                    in_=w[256 * u : 256 * u + 256, :].rearrange("(q e) c -> q e c", e=2),
+                )
+        b1_sb = const.tile([P, 2, 4], BF16)
+        mask_sb = const.tile([P, CHUNKS, NODES], BF16)
+        with nc.allow_non_contiguous_dma(reason="small bias and mask tables"):
+            nc.sync.dma_start(out=b1_sb[:], in_=b1.rearrange("(c p t) -> p c t", c=2, p=P, t=4))
+            nc.sync.dma_start(out=mask_sb[:], in_=adj_flat.rearrange("(r p) j -> p r j", p=P))
+        raw2 = const.tile([P, 2, 4, D], BF16)
+        nc.sync.dma_start(out=raw2[:], in_=w2.rearrange("(c p t) n -> p c t n", c=2, p=P, t=4))
+        b2_bc = const.tile([P, D], BF16)
+        gamma_bc = const.tile([P, D], BF16)
+        beta_bc = const.tile([P, D], BF16)
+        nc.sync.dma_start(out=b2_bc[:], in_=b2.partition_broadcast(P))
+        if T_CHUNKS:
+            b1_bc = const.tile([P, F], BF16)
+            nc.sync.dma_start(out=b1_bc[:], in_=b1.partition_broadcast(P))
+        nc.sync.dma_start(out=gamma_bc[:], in_=gamma.partition_broadcast(P))
+        nc.sync.dma_start(out=beta_bc[:], in_=beta.partition_broadcast(P))
+
+        warm = const.tile([P, 1], F32)
+        nc.vector.memset(warm[:], 1.0)
+        warm2 = const.tile([P, 1], F32)
+        nc.scalar.sqrt(out=warm2[:], in_=warm[:])
+        ident = const.tile([P, P], F32)
+        make_identity(nc, ident[:])
+
+        gh = const.tile([P, 4 * ROWS], BF16, align_bytes=64)
+        ghw = gh[:].bitcast(F32).rearrange("p (r u) -> p r u", u=2)
+        for half in range(2):
+            ps_h = pre_pool.tile([P, 2, 2, P], F32, tag="pre")
+            for l in range(2):
+                r = 2 * half + l
+                for u in range(2):
+                    nc.tensor.transpose(
+                        ps_h[:, l, u, :], h_sb[:, r, :].bitcast(F32)[:, u * P : (u + 1) * P], ident[:]
+                    )
+            for l in range(2):
+                r = 2 * half + l
+                nc.vector.tensor_copy(
+                    out=ghw[:, r * P : (r + 1) * P, :], in_=ps_h[:, l, :, :].rearrange("p u r -> p r u")
+                )
+        hq = const.tile([P, ROWS], U32, align_bytes=64)
+        hs = const.tile([P, ROWS], U8, align_bytes=64)
+
+        w1q = {}
+        w1s = {}
+        for o in ("a", "b"):
+            w1q[o] = const.tile([P, F], U32, name="w1q" + o, align_bytes=64)
+            w1s[o] = const.tile([P, F], U8, name="w1s" + o, align_bytes=64)
+        g1 = {}
+        for c in range(2):
+            for o in ("a", "b"):
+                g1[(o, c)] = const.tile([P, 2048], BF16, name="g1%s%d" % (o, c), align_bytes=64)
+                dst = g1[(o, c)][:].rearrange("q (t p k) -> q p k t", t=4, p=P, k=4)
+                src = raw1[o][:, :, 512 * c : 512 * c + 512].rearrange("q k (p t) -> q p k t", t=4)
+                if o == "a":
+                    nc.vector.tensor_copy(out=dst, in_=src)
+                else:
+                    nc.scalar.copy(out=dst, in_=src)
+        nc.vector.quantize_mx(out=hq[:].bitcast(FP8X4), scales=hs[:], in_=gh[:])
+        for c in range(2):
+            for o in ("a", "b"):
+                cols = slice(512 * c, 512 * c + 512)
+                nc.vector.quantize_mx(
+                    out=w1q[o][:, cols].bitcast(FP8X4), scales=w1s[o][:, cols], in_=g1[(o, c)][:]
+                )
+
+        b1f = const.tile([P, 2, 4], F32)
+        nc.vector.tensor_copy(out=b1f[:], in_=b1_sb[:])
+        maskf = const.tile([P, CHUNKS, NODES], F32)
+        nc.vector.tensor_copy(out=maskf[:], in_=mask_sb[:])
+        deg = const.tile([P, CHUNKS], F32)
+        nc.vector.tensor_reduce(out=deg[:], in_=maskf[:], axis=AX.X, op=ALU.add)
+        masku = const.tile([P, CHUNKS, NODES], F32)
+        for r in A_CHUNKS:
+            nc.vector.tensor_copy(out=masku[:, r, :], in_=maskf[:, r, :])
+
+        a_sb = const.tile([P, 2, max(n_a, P), 4], F32)
+        b_sb = const.tile([P, 2, max(n_a, P), 4], F32)
+
+        def first_layer_pass(dst, o, c, t, r):
+            wcols = slice(512 * c + P * t, 512 * c + P * t + P)
+            hcols = slice(P * r, P * r + P)
+            nc.tensor.matmul_mx(
+                out=dst,
+                lhsT=w1q[o][:, wcols].bitcast(FP8X4),
+                lhsT_scale=w1s[o][:, wcols],
+                rhs=hq[:, hcols].bitcast(FP8X4),
+                rhs_scale=hs[:, hcols],
+                start=True,
+                stop=True,
+            )
+
+        for c in range(2):
+            for r in A_CHUNKS:
+                rows = slice(P * r, P * r + P)
+                pa = pre_pool.tile([P, 4, P], F32, tag="pre")
+                for t in range(4):
+                    first_layer_pass(pa[:, t, :], "a", c, t, r)
+                nc.scalar.copy(out=a_sb[:, c, rows, :], in_=pa[:].rearrange("p t r -> p r t"))
+                pb = pre_pool.tile([P, 4, P], F32, tag="pre")
+                for t in range(4):
+                    first_layer_pass(pb[:, t, :], "b", c, t, r)
+                nc.vector.tensor_tensor(
+                    out=b_sb[:, c, rows, :],
+                    in0=pb[:].rearrange("p t r -> p r t"),
+                    in1=b1f[:, c, :].unsqueeze(1).to_broadcast([P, P, 4]),
+                    op=ALU.add,
+                )
+
+        xa = {}
+        xb = {}
+        if T_CHUNKS:
+            for r in T_CHUNKS:
+                xa[r] = const.tile([P, 2, 4, P], F32, name="xa%d" % r)
+                xb[r] = const.tile([P, 2, 4, P], F32, name="xb%d" % r)
+                hcols = slice(P * r, P * r + P)
+                for c in range(2):
+                    wcols = slice(512 * c, 512 * c + 512)
+                    for o in ("a", "b"):
+                        px = m_pool.tile([P, 4, P], F32, tag="m")
+                        nc.tensor.matmul_mx(
+                            out=px[:].rearrange("p t f -> p (t f)"),
+                            lhsT=hq[:, hcols].bitcast(FP8X4),
+                            lhsT_scale=hs[:, hcols],
+                            rhs=w1q[o][:, wcols].bitcast(FP8X4),
+                            rhs_scale=w1s[o][:, wcols],
+                            start=True,
+                            stop=True,
+                        )
+                        if o == "a":
+                            nc.vector.tensor_tensor(
+                                out=xa[r][:, c, :, :],
+                                in0=px[:],
+                                in1=b1_bc[:, wcols].rearrange("q (p t) -> q t p", t=4),
+                                op=ALU.add,
+                            )
+                        else:
+                            nc.scalar.copy(out=xb[r][:, c, :, :], in_=px[:])
+            ident_d = const.tile([P, 8, 2 * NODES], F32)
+            ident_v = ident[:].rearrange("p (g i) -> p g i", i=NODES)
+            nc.gpsimd.tensor_copy(out=ident_d[:, :, 0:NODES], in_=ident_v)
+            nc.gpsimd.tensor_copy(out=ident_d[:, :, NODES : 2 * NODES], in_=ident_v)
+            prot = const.tile([P, NODES, P], F32)
+            for u in range(NODES):
+                nc.gpsimd.tensor_copy(
+                    out=prot[:, u, :].rearrange("p (g i) -> p g i", i=NODES), in_=ident_d[:, :, u : u + NODES]
+                )
+            i16d = const.tile([P, 2 * NODES], F32)
+            nc.vector.tensor_reduce(
+                out=i16d[:, 0:NODES], in_=ident[:].rearrange("p (g i) -> p i g", i=NODES), axis=AX.X, op=ALU.add
+            )
+            nc.vector.tensor_copy(out=i16d[:, NODES : 2 * NODES], in_=i16d[:, 0:NODES])
+            sel = const.tile([P, NODES, NODES], F32)
+            for u in range(NODES):
+                nc.gpsimd.tensor_copy(out=sel[:, u, :], in_=i16d[:, NODES - u : 2 * NODES - u])
+            for r in T_CHUNKS:
+                prod = small.tile([P, NODES, NODES], F32, tag="prod")
+                nc.vector.tensor_tensor(
+                    out=prod[:],
+                    in0=sel[:],
+                    in1=maskf[:, r, :].unsqueeze(1).to_broadcast([P, NODES, NODES]),
+                    op=ALU.mult,
+                )
+                nc.vector.tensor_reduce(out=masku[:, r, :], in_=prod[:], axis=AX.X, op=ALU.add)
+
+        w2q = const.tile([P, 2, D], U32, align_bytes=64)
+        w2s = const.tile([P, 2, D], U8, align_bytes=64)
+        g2 = {}
+        for c in range(2):
+            g2[c] = const.tile([P, 2048], BF16, name="g2%d" % c, align_bytes=64)
+            dst = g2[c][:].rearrange("p (m i t) -> p m t i", i=4, t=4)
+            src = raw2[:, c, :, :].rearrange("p t (m i) -> p m t i", i=4)
+            nc.scalar.copy(out=dst, in_=src)
+        for c in range(2):
+            nc.vector.quantize_mx(out=w2q[:, c, :].bitcast(FP8X4), scales=w2s[:, c, :], in_=g2[c][:])
+
+        acc = const.tile([P, CHUNKS, D], F32)
+        for r in range(CHUNKS):
+            t1 = stage.tile([P, D], F32, tag="t1")
+            nc.gpsimd.tensor_scalar(
+                out=t1[:], in0=b2_bc[:], scalar1=deg[:, r : r + 1], scalar2=0.0, op0=ALU.mult, op1=ALU.add
+            )
+            h16 = stage.tile([P, D], F32, tag="h16")
+            nc.gpsimd.tensor_scalar(
+                out=h16[:], in0=h_sb[:, r, :], scalar1=16.0, scalar2=0.0, op0=ALU.mult, op1=ALU.add
+            )
+            nc.gpsimd.tensor_tensor(out=acc[:, r, :], in0=t1[:], in1=h16[:], op=ALU.add)
+
+        for u in range(NODES):
+            zq = {}
+            zs = {}
+            for c in range(2):
+                z = zpool.tile([P, 4 * ROWS], BF16, tag="z", align_bytes=64)
+                if n_a:
+                    nc.vector.tensor_tensor(
+                        out=z[:, 0 : 4 * n_a].rearrange("p (g i t) -> p g i t", i=NODES, t=4),
+                        in0=a_sb[:, c, 0:n_a, :].rearrange("p (g i) t -> p g i t", i=NODES),
+                        in1=b_sb[:, c, 0:n_a, :]
+                        .rearrange("p (g j) t -> p g j t", j=NODES)[:, :, u, :]
+                        .unsqueeze(2)
+                        .to_broadcast([P, n_a // NODES, NODES, 4]),
+                        op=ALU.add,
+                    )
+                    nc.scalar.activation(out=z[:, 0 : 4 * n_a], in_=z[:, 0 : 4 * n_a], func=ACT.Relu)
+                for r in T_CHUNKS:
+                    pre = pre_pool.tile([P, 4, P], F32, tag="pre")
+                    for t in range(4):
+                        nc.tensor.matmul(
+                            out=pre[:, t, :], lhsT=xa[r][:, c, t, :], rhs=ident[:],
+                            is_transpose=True, start=True, stop=False,
+                        )
+                        nc.tensor.matmul(
+                            out=pre[:, t, :], lhsT=xb[r][:, c, t, :], rhs=prot[:, u, :],
+                            is_transpose=True, start=False, stop=True,
+                        )
+                    nc.scalar.activation(
+                        out=z[:, 4 * P * r : 4 * P * (r + 1)].rearrange("p (r t) -> p r t", t=4),
+                        in_=pre[:].rearrange("p t r -> p r t"),
+                        func=ACT.Relu,
+                    )
+                zq[c] = zpool.tile([P, ROWS], U32, tag="zq", name="zq%d" % c, align_bytes=64)
+                zs[c] = zpool.tile([P, ROWS], U8, tag="zs", name="zs%d" % c, align_bytes=64)
+                nc.vector.quantize_mx(out=zq[c][:].bitcast(FP8X4), scales=zs[c][:], in_=z[:])
+            for r in range(CHUNKS):
+                cols = slice(P * r, P * r + P)
+                m = m_pool.tile([P, D], F32, tag="m")
+                for c in range(2):
+                    nc.tensor.matmul_mx(
+                        out=m[:],
+                        lhsT=zq[c][:, cols].bitcast(FP8X4),
+                        lhsT_scale=zs[c][:, cols],
+                        rhs=w2q[:, c, :].bitcast(FP8X4),
+                        rhs_scale=w2s[:, c, :],
+                        start=(c == 0),
+                        stop=(c == 1),
+                    )
+                nc.vector.scalar_tensor_tensor(
+                    out=acc[:, r, :],
+                    in0=m[:],
+                    scalar=masku[:, r, u : u + 1],
+                    in1=acc[:, r, :],
+                    op0=ALU.mult,
+                    op1=ALU.add,
+                )
+
+        for r in range(CHUNKS):
+            stats = small.tile([P, 6], F32, tag="stats")
+            nc.vector.bn_stats(out=stats[:], in_=acc[:, r, :])
+            mv = small.tile([P, 2], F32, tag="mv")
+            nc.vector.bn_aggr(out=mv[:], in_=stats[:])
+            ve = small.tile([P, 1], F32, tag="ve")
+            nc.vector.tensor_scalar_add(out=ve[:], in0=mv[:, 1:2], scalar1=256.0 * EPS)
+            sd = small.tile([P, 1], F32, tag="sd")
+            nc.scalar.sqrt(out=sd[:], in_=ve[:])
+            rstd = small.tile([P, 1], F32, tag="rstd")
+            nc.vector.reciprocal(out=rstd[:], in_=sd[:])
+            y = stage.tile([P, D], F32, tag="y")
+            nc.vector.tensor_scalar(
+                out=y[:], in0=acc[:, r, :], scalar1=mv[:, 0:1], scalar2=rstd[:], op0=ALU.subtract, op1=ALU.mult
+            )
+            nc.vector.tensor_tensor(out=y[:], in0=y[:], in1=gamma_bc[:], op=ALU.mult)
+            nc.vector.tensor_tensor(out=y[:], in0=y[:], in1=beta_bc[:], op=ALU.add)
+            nc.sync.dma_start(out=out_flat[P * r : P * r + P, :], in_=y[:])

@@ -21,10 +21,10 @@ CHUNKS = 4
 EPS = 1e-5
 FLOPS = 2 * ROWS * D * F * 2 + 2 * ROWS * NODES * F * D
 
-T_CHUNKS = ()
+T_CHUNKS = (2, 3)
 A_CHUNKS = tuple(r for r in range(CHUNKS) if r not in T_CHUNKS)
-PRE_BUFS = 3
-M_BUFS = 5
+PRE_BUFS = 4
+M_BUFS = 4
 
 
 def tile_simplegnn_pa_t_kernel(tc, h, adj_mask, w1a, w1b, b1, w2, b2, gamma, beta, out):

@@ -20,11 +20,9 @@ ROWS = 512
 CHUNKS = 4
 EPS = 1e-5
 FLOPS = 2 * ROWS * D * F * 2 + 2 * ROWS * NODES * F * D
-
+A_CHUNKS = (0, 1)
 T_CHUNKS = (2, 3)
-A_CHUNKS = tuple(r for r in range(CHUNKS) if r not in T_CHUNKS)
-PRE_BUFS = 4
-M_BUFS = 4
+N_A = 256
 
 
 def tile_simplegnn_pa_t_kernel(tc, h, adj_mask, w1a, w1b, b1, w2, b2, gamma, beta, out):
@@ -32,40 +30,47 @@ def tile_simplegnn_pa_t_kernel(tc, h, adj_mask, w1a, w1b, b1, w2, b2, gamma, bet
     h_flat = h.flatten_outer_dims()
     adj_flat = adj_mask.flatten_outer_dims()
     out_flat = out.flatten_outer_dims()
-    n_a = len(A_CHUNKS) * P
+    w1 = {"a": w1a, "b": w1b}
 
     with ExitStack() as ctx:
         const = ctx.enter_context(tc.tile_pool(name="const", bufs=1))
         stage = ctx.enter_context(tc.tile_pool(name="stage", bufs=2))
         zpool = ctx.enter_context(tc.tile_pool(name="zpool", bufs=4))
         small = ctx.enter_context(tc.tile_pool(name="small", bufs=4))
-        pre_pool = ctx.enter_context(tc.psum_pool(name="pre", bufs=PRE_BUFS))
-        m_pool = ctx.enter_context(tc.psum_pool(name="m", bufs=M_BUFS))
+        pre_pool = ctx.enter_context(tc.psum_pool(name="pre", bufs=4))
+        m_pool = ctx.enter_context(tc.psum_pool(name="m", bufs=4))
+        ctx.enter_context(tc.manual_schedule())
 
+        mask_sb = const.tile([P, CHUNKS, NODES], BF16)
+        b1_sb = const.tile([P, 2, 4], BF16)
+        with nc.allow_non_contiguous_dma(reason="small bias and mask tables"):
+            nc.sync.dma_start(out=mask_sb[:], in_=adj_flat.rearrange("(r p) j -> p r j", p=P))
+            nc.sync.dma_start(out=b1_sb[:], in_=b1.rearrange("(c p t) -> p c t", c=2, p=P, t=4))
         h_sb = const.tile([P, CHUNKS, D], BF16)
         nc.sync.dma_start(out=h_sb[:], in_=h_flat.rearrange("(r p) d -> p r d", p=P))
         raw1 = {}
-        for o, w in (("a", w1a), ("b", w1b)):
+        for o in ("a", "b"):
             raw1[o] = const.tile([P, 4, F], BF16, name="raw1" + o)
+
+        def load_w1(o, c):
             for u in range(2):
                 nc.sync.dma_start(
-                    out=raw1[o][:, 2 * u : 2 * u + 2, :],
-                    in_=w[256 * u : 256 * u + 256, :].rearrange("(q e) c -> q e c", e=2),
+                    out=raw1[o][:, 2 * u : 2 * u + 2, 512 * c : 512 * c + 512],
+                    in_=w1[o][256 * u : 256 * u + 256, 512 * c : 512 * c + 512].rearrange("(q e) f -> q e f", e=2),
                 )
-        b1_sb = const.tile([P, 2, 4], BF16)
-        mask_sb = const.tile([P, CHUNKS, NODES], BF16)
-        with nc.allow_non_contiguous_dma(reason="small bias and mask tables"):
-            nc.sync.dma_start(out=b1_sb[:], in_=b1.rearrange("(c p t) -> p c t", c=2, p=P, t=4))
-            nc.sync.dma_start(out=mask_sb[:], in_=adj_flat.rearrange("(r p) j -> p r j", p=P))
+
+        load_w1("a", 0)
+        load_w1("b", 0)
+        b2_bc = const.tile([P, D], BF16)
+        nc.sync.dma_start(out=b2_bc[:], in_=b2.partition_broadcast(P))
+        b1_bc = const.tile([P, F], BF16)
+        nc.sync.dma_start(out=b1_bc[:], in_=b1.partition_broadcast(P))
+        load_w1("a", 1)
+        load_w1("b", 1)
         raw2 = const.tile([P, 2, 4, D], BF16)
         nc.sync.dma_start(out=raw2[:], in_=w2.rearrange("(c p t) n -> p c t n", c=2, p=P, t=4))
-        b2_bc = const.tile([P, D], BF16)
         gamma_bc = const.tile([P, D], BF16)
         beta_bc = const.tile([P, D], BF16)
-        nc.sync.dma_start(out=b2_bc[:], in_=b2.partition_broadcast(P))
-        if T_CHUNKS:
-            b1_bc = const.tile([P, F], BF16)
-            nc.sync.dma_start(out=b1_bc[:], in_=b1.partition_broadcast(P))
         nc.sync.dma_start(out=gamma_bc[:], in_=gamma.partition_broadcast(P))
         nc.sync.dma_start(out=beta_bc[:], in_=beta.partition_broadcast(P))
 
@@ -75,6 +80,38 @@ def tile_simplegnn_pa_t_kernel(tc, h, adj_mask, w1a, w1b, b1, w2, b2, gamma, bet
         nc.scalar.sqrt(out=warm2[:], in_=warm[:])
         ident = const.tile([P, P], F32)
         make_identity(nc, ident[:])
+        ident_d = const.tile([P, 8, 2 * NODES], F32)
+        ident_v = ident[:].rearrange("p (g i) -> p g i", i=NODES)
+        nc.vector.tensor_copy(out=ident_d[:, :, 0:NODES], in_=ident_v)
+        nc.vector.tensor_copy(out=ident_d[:, :, NODES : 2 * NODES], in_=ident_v)
+        prot = const.tile([P, NODES, P], F32)
+        for u in range(NODES):
+            nc.vector.tensor_copy(
+                out=prot[:, u, :].rearrange("p (g i) -> p g i", i=NODES), in_=ident_d[:, :, u : u + NODES]
+            )
+        i16d = const.tile([P, 2 * NODES], F32)
+        nc.vector.tensor_reduce(
+            out=i16d[:, 0:NODES], in_=ident[:].rearrange("p (g i) -> p i g", i=NODES), axis=AX.X, op=ALU.add
+        )
+        nc.vector.tensor_copy(out=i16d[:, NODES : 2 * NODES], in_=i16d[:, 0:NODES])
+        sel = const.tile([P, NODES, NODES], F32)
+        for u in range(NODES):
+            nc.vector.tensor_copy(out=sel[:, u, :], in_=i16d[:, NODES - u : 2 * NODES - u])
+        mask16 = const.tile([P, CHUNKS, NODES], F32)
+        nc.vector.tensor_scalar_mul(out=mask16[:], in0=mask_sb[:], scalar1=1.0 / NODES)
+        deg16 = const.tile([P, CHUNKS], F32)
+        nc.vector.tensor_reduce(out=deg16[:], in_=mask16[:], axis=AX.X, op=ALU.add)
+        masku = const.tile([P, CHUNKS, NODES], F32)
+        for r in A_CHUNKS:
+            nc.vector.tensor_copy(out=masku[:, r, :], in_=mask16[:, r, :])
+        for r in T_CHUNKS:
+            prod = small.tile([P, NODES, NODES], F32, tag="prod")
+            nc.vector.tensor_tensor(
+                out=prod[:], in0=sel[:], in1=mask16[:, r, :].unsqueeze(1).to_broadcast([P, NODES, NODES]), op=ALU.mult
+            )
+            nc.vector.tensor_reduce(out=masku[:, r, :], in_=prod[:], axis=AX.X, op=ALU.add)
+        b1f = const.tile([P, 2, 4], F32)
+        nc.vector.tensor_copy(out=b1f[:], in_=b1_sb[:])
 
         gh = const.tile([P, 4 * ROWS], BF16, align_bytes=64)
         ghw = gh[:].bitcast(F32).rearrange("p (r u) -> p r u", u=2)
@@ -88,229 +125,248 @@ def tile_simplegnn_pa_t_kernel(tc, h, adj_mask, w1a, w1b, b1, w2, b2, gamma, bet
                     )
             for l in range(2):
                 r = 2 * half + l
-                nc.vector.tensor_copy(
-                    out=ghw[:, r * P : (r + 1) * P, :], in_=ps_h[:, l, :, :].rearrange("p u r -> p r u")
-                )
+                dst = ghw[:, r * P : (r + 1) * P, :]
+                src = ps_h[:, l, :, :].rearrange("p u r -> p r u")
+                if half == 0:
+                    nc.vector.tensor_copy(out=dst, in_=src)
+                else:
+                    nc.scalar.copy(out=dst, in_=src)
         hq = const.tile([P, ROWS], U32, align_bytes=64)
         hs = const.tile([P, ROWS], U8, align_bytes=64)
 
         w1q = {}
         w1s = {}
+        g1 = {}
         for o in ("a", "b"):
             w1q[o] = const.tile([P, F], U32, name="w1q" + o, align_bytes=64)
             w1s[o] = const.tile([P, F], U8, name="w1s" + o, align_bytes=64)
-        g1 = {}
-        for c in range(2):
-            for o in ("a", "b"):
+            for c in range(2):
                 g1[(o, c)] = const.tile([P, 2048], BF16, name="g1%s%d" % (o, c), align_bytes=64)
-                dst = g1[(o, c)][:].rearrange("q (t p k) -> q p k t", t=4, p=P, k=4)
-                src = raw1[o][:, :, 512 * c : 512 * c + 512].rearrange("q k (p t) -> q p k t", t=4)
-                if o == "a":
-                    nc.vector.tensor_copy(out=dst, in_=src)
-                else:
-                    nc.scalar.copy(out=dst, in_=src)
-        nc.vector.quantize_mx(out=hq[:].bitcast(FP8X4), scales=hs[:], in_=gh[:])
-        for c in range(2):
-            for o in ("a", "b"):
-                cols = slice(512 * c, 512 * c + 512)
-                nc.vector.quantize_mx(
-                    out=w1q[o][:, cols].bitcast(FP8X4), scales=w1s[o][:, cols], in_=g1[(o, c)][:]
-                )
 
-        b1f = const.tile([P, 2, 4], F32)
-        nc.vector.tensor_copy(out=b1f[:], in_=b1_sb[:])
-        maskf = const.tile([P, CHUNKS, NODES], F32)
-        nc.vector.tensor_copy(out=maskf[:], in_=mask_sb[:])
-        deg = const.tile([P, CHUNKS], F32)
-        nc.vector.tensor_reduce(out=deg[:], in_=maskf[:], axis=AX.X, op=ALU.add)
-        masku = const.tile([P, CHUNKS, NODES], F32)
-        for r in A_CHUNKS:
-            nc.vector.tensor_copy(out=masku[:, r, :], in_=maskf[:, r, :])
+        def regroup_w1(o, c, eng):
+            dst = g1[(o, c)][:].rearrange("q (t p k) -> q p k t", t=4, p=P, k=4)
+            src = raw1[o][:, :, 512 * c : 512 * c + 512].rearrange("q k (p t) -> q p k t", t=4)
+            if eng == "v":
+                nc.vector.tensor_copy(out=dst, in_=src)
+            else:
+                nc.scalar.copy(out=dst, in_=src)
 
-        a_sb = const.tile([P, 2, max(n_a, P), 4], F32)
-        b_sb = const.tile([P, 2, max(n_a, P), 4], F32)
+        def quantise_w1(o, c):
+            cols = slice(512 * c, 512 * c + 512)
+            nc.vector.quantize_mx(out=w1q[o][:, cols].bitcast(FP8X4), scales=w1s[o][:, cols], in_=g1[(o, c)][:])
 
-        def first_layer_pass(dst, o, c, t, r):
-            wcols = slice(512 * c + P * t, 512 * c + P * t + P)
-            hcols = slice(P * r, P * r + P)
-            nc.tensor.matmul_mx(
-                out=dst,
-                lhsT=w1q[o][:, wcols].bitcast(FP8X4),
-                lhsT_scale=w1s[o][:, wcols],
-                rhs=hq[:, hcols].bitcast(FP8X4),
-                rhs_scale=hs[:, hcols],
-                start=True,
-                stop=True,
-            )
-
-        for c in range(2):
-            for r in A_CHUNKS:
-                rows = slice(P * r, P * r + P)
-                pa = pre_pool.tile([P, 4, P], F32, tag="pre")
-                for t in range(4):
-                    first_layer_pass(pa[:, t, :], "a", c, t, r)
-                nc.scalar.copy(out=a_sb[:, c, rows, :], in_=pa[:].rearrange("p t r -> p r t"))
-                pb = pre_pool.tile([P, 4, P], F32, tag="pre")
-                for t in range(4):
-                    first_layer_pass(pb[:, t, :], "b", c, t, r)
-                nc.vector.tensor_tensor(
-                    out=b_sb[:, c, rows, :],
-                    in0=pb[:].rearrange("p t r -> p r t"),
-                    in1=b1f[:, c, :].unsqueeze(1).to_broadcast([P, P, 4]),
-                    op=ALU.add,
-                )
-
+        a_sb = const.tile([P, 2, N_A, 4], F32)
+        b_sb = const.tile([P, 2, N_A, 4], F32)
         xa = {}
         xb = {}
-        if T_CHUNKS:
-            for r in T_CHUNKS:
-                xa[r] = const.tile([P, 2, 4, P], F32, name="xa%d" % r)
-                xb[r] = const.tile([P, 2, 4, P], F32, name="xb%d" % r)
+        for r in T_CHUNKS:
+            xa[r] = const.tile([P, 2, 4, P], F32, name="xa%d" % r)
+            xb[r] = const.tile([P, 2, 4, P], F32, name="xb%d" % r)
+
+        def first_layer(c):
+            banks = {}
+            for r in A_CHUNKS:
                 hcols = slice(P * r, P * r + P)
-                for c in range(2):
-                    wcols = slice(512 * c, 512 * c + 512)
-                    for o in ("a", "b"):
-                        px = m_pool.tile([P, 4, P], F32, tag="m")
+                for o in ("a", "b"):
+                    banks[(o, r)] = pre_pool.tile([P, 4, P], F32, tag="pre", name="fl%s%d" % (o, r))
+                    for t in range(4):
+                        wcols = slice(512 * c + P * t, 512 * c + P * t + P)
                         nc.tensor.matmul_mx(
-                            out=px[:].rearrange("p t f -> p (t f)"),
-                            lhsT=hq[:, hcols].bitcast(FP8X4),
-                            lhsT_scale=hs[:, hcols],
-                            rhs=w1q[o][:, wcols].bitcast(FP8X4),
-                            rhs_scale=w1s[o][:, wcols],
+                            out=banks[(o, r)][:, t, :],
+                            lhsT=w1q[o][:, wcols].bitcast(FP8X4),
+                            lhsT_scale=w1s[o][:, wcols],
+                            rhs=hq[:, hcols].bitcast(FP8X4),
+                            rhs_scale=hs[:, hcols],
                             start=True,
                             stop=True,
                         )
-                        if o == "a":
-                            nc.vector.tensor_tensor(
-                                out=xa[r][:, c, :, :],
-                                in0=px[:],
-                                in1=b1_bc[:, wcols].rearrange("q (p t) -> q t p", t=4),
-                                op=ALU.add,
-                            )
-                        else:
-                            nc.scalar.copy(out=xb[r][:, c, :, :], in_=px[:])
-            ident_d = const.tile([P, 8, 2 * NODES], F32)
-            ident_v = ident[:].rearrange("p (g i) -> p g i", i=NODES)
-            nc.gpsimd.tensor_copy(out=ident_d[:, :, 0:NODES], in_=ident_v)
-            nc.gpsimd.tensor_copy(out=ident_d[:, :, NODES : 2 * NODES], in_=ident_v)
-            prot = const.tile([P, NODES, P], F32)
-            for u in range(NODES):
-                nc.gpsimd.tensor_copy(
-                    out=prot[:, u, :].rearrange("p (g i) -> p g i", i=NODES), in_=ident_d[:, :, u : u + NODES]
-                )
-            i16d = const.tile([P, 2 * NODES], F32)
-            nc.vector.tensor_reduce(
-                out=i16d[:, 0:NODES], in_=ident[:].rearrange("p (g i) -> p i g", i=NODES), axis=AX.X, op=ALU.add
-            )
-            nc.vector.tensor_copy(out=i16d[:, NODES : 2 * NODES], in_=i16d[:, 0:NODES])
-            sel = const.tile([P, NODES, NODES], F32)
-            for u in range(NODES):
-                nc.gpsimd.tensor_copy(out=sel[:, u, :], in_=i16d[:, NODES - u : 2 * NODES - u])
+            wcols = slice(512 * c, 512 * c + 512)
             for r in T_CHUNKS:
-                prod = small.tile([P, NODES, NODES], F32, tag="prod")
+                hcols = slice(P * r, P * r + P)
+                for o in ("a", "b"):
+                    banks[(o, r)] = m_pool.tile([P, 4, P], F32, tag="m", name="fx%s%d" % (o, r))
+                    nc.tensor.matmul_mx(
+                        out=banks[(o, r)][:].rearrange("p t f -> p (t f)"),
+                        lhsT=hq[:, hcols].bitcast(FP8X4),
+                        lhsT_scale=hs[:, hcols],
+                        rhs=w1q[o][:, wcols].bitcast(FP8X4),
+                        rhs_scale=w1s[o][:, wcols],
+                        start=True,
+                        stop=True,
+                    )
+            return banks
+
+        def first_layer_out(c, banks):
+            wcols = slice(512 * c, 512 * c + 512)
+            for r in A_CHUNKS:
+                rows = slice(P * r, P * r + P)
+                nc.scalar.copy(out=a_sb[:, c, rows, :], in_=banks[("a", r)][:].rearrange("p t r -> p r t"))
                 nc.vector.tensor_tensor(
-                    out=prod[:],
-                    in0=sel[:],
-                    in1=maskf[:, r, :].unsqueeze(1).to_broadcast([P, NODES, NODES]),
-                    op=ALU.mult,
+                    out=b_sb[:, c, rows, :],
+                    in0=banks[("b", r)][:].rearrange("p t r -> p r t"),
+                    in1=b1f[:, c, :].unsqueeze(1).to_broadcast([P, P, 4]),
+                    op=ALU.add,
                 )
-                nc.vector.tensor_reduce(out=masku[:, r, :], in_=prod[:], axis=AX.X, op=ALU.add)
+            for r in T_CHUNKS:
+                nc.scalar.copy(out=xb[r][:, c, :, :], in_=banks[("b", r)][:])
+                nc.vector.tensor_tensor(
+                    out=xa[r][:, c, :, :],
+                    in0=banks[("a", r)][:],
+                    in1=b1_bc[:, wcols].rearrange("q (p t) -> q t p", t=4),
+                    op=ALU.add,
+                )
+
+        regroup_w1("a", 0, "v")
+        regroup_w1("b", 0, "s")
+        nc.vector.quantize_mx(out=hq[:].bitcast(FP8X4), scales=hs[:], in_=gh[:])
+        quantise_w1("a", 0)
+        regroup_w1("a", 1, "v")
+        quantise_w1("b", 0)
+        banks0 = first_layer(0)
+        regroup_w1("b", 1, "v")
+        quantise_w1("a", 1)
+        first_layer_out(0, banks0)
+        quantise_w1("b", 1)
+        banks1 = first_layer(1)
 
         w2q = const.tile([P, 2, D], U32, align_bytes=64)
         w2s = const.tile([P, 2, D], U8, align_bytes=64)
-        g2 = {}
-        for c in range(2):
-            g2[c] = const.tile([P, 2048], BF16, name="g2%d" % c, align_bytes=64)
-            dst = g2[c][:].rearrange("p (m i t) -> p m t i", i=4, t=4)
-            src = raw2[:, c, :, :].rearrange("p t (m i) -> p m t i", i=4)
-            nc.scalar.copy(out=dst, in_=src)
-        for c in range(2):
-            nc.vector.quantize_mx(out=w2q[:, c, :].bitcast(FP8X4), scales=w2s[:, c, :], in_=g2[c][:])
 
         acc = const.tile([P, CHUNKS, D], F32)
         for r in range(CHUNKS):
             t1 = stage.tile([P, D], F32, tag="t1")
             nc.gpsimd.tensor_scalar(
-                out=t1[:], in0=b2_bc[:], scalar1=deg[:, r : r + 1], scalar2=0.0, op0=ALU.mult, op1=ALU.add
+                out=t1[:], in0=b2_bc[:], scalar1=deg16[:, r : r + 1], scalar2=0.0, op0=ALU.mult, op1=ALU.add
             )
-            h16 = stage.tile([P, D], F32, tag="h16")
+            nc.gpsimd.tensor_tensor(out=acc[:, r, :], in0=t1[:], in1=h_sb[:, r, :], op=ALU.add)
+        g2 = {}
+        for c in range(2):
+            g2[c] = const.tile([P, 2048], BF16, name="g2%d" % c, align_bytes=64)
             nc.gpsimd.tensor_scalar(
-                out=h16[:], in0=h_sb[:, r, :], scalar1=16.0, scalar2=0.0, op0=ALU.mult, op1=ALU.add
+                out=g2[c][:].rearrange("p (m i t) -> p m t i", i=4, t=4),
+                in0=raw2[:, c, :, :].rearrange("p t (m i) -> p m t i", i=4),
+                scalar1=1.0, scalar2=0.0, op0=ALU.mult, op1=ALU.add,
             )
-            nc.gpsimd.tensor_tensor(out=acc[:, r, :], in0=t1[:], in1=h16[:], op=ALU.add)
 
-        for u in range(NODES):
-            zq = {}
-            zs = {}
+        z = {}
+        zq = {}
+        zs = {}
+
+        def new_z(u):
             for c in range(2):
-                z = zpool.tile([P, 4 * ROWS], BF16, tag="z", align_bytes=64)
-                if n_a:
-                    nc.vector.tensor_tensor(
-                        out=z[:, 0 : 4 * n_a].rearrange("p (g i t) -> p g i t", i=NODES, t=4),
-                        in0=a_sb[:, c, 0:n_a, :].rearrange("p (g i) t -> p g i t", i=NODES),
-                        in1=b_sb[:, c, 0:n_a, :]
-                        .rearrange("p (g j) t -> p g j t", j=NODES)[:, :, u, :]
-                        .unsqueeze(2)
-                        .to_broadcast([P, n_a // NODES, NODES, 4]),
-                        op=ALU.add,
-                    )
-                    nc.scalar.activation(out=z[:, 0 : 4 * n_a], in_=z[:, 0 : 4 * n_a], func=ACT.Relu)
+                z[(u, c)] = zpool.tile([P, 4 * ROWS], BF16, tag="z", name="z%d" % c, align_bytes=64)
+
+        def sums_on_tensor(u):
+            banks = {}
+            for c in range(2):
                 for r in T_CHUNKS:
-                    pre = pre_pool.tile([P, 4, P], F32, tag="pre")
+                    banks[(c, r)] = pre_pool.tile([P, 4, P], F32, tag="pre", name="pre%d%d" % (c, r))
                     for t in range(4):
                         nc.tensor.matmul(
-                            out=pre[:, t, :], lhsT=xa[r][:, c, t, :], rhs=ident[:],
+                            out=banks[(c, r)][:, t, :], lhsT=xa[r][:, c, t, :], rhs=ident[:],
                             is_transpose=True, start=True, stop=False,
                         )
                         nc.tensor.matmul(
-                            out=pre[:, t, :], lhsT=xb[r][:, c, t, :], rhs=prot[:, u, :],
+                            out=banks[(c, r)][:, t, :], lhsT=xb[r][:, c, t, :], rhs=prot[:, u, :],
                             is_transpose=True, start=False, stop=True,
                         )
-                    nc.scalar.activation(
-                        out=z[:, 4 * P * r : 4 * P * (r + 1)].rearrange("p (r t) -> p r t", t=4),
-                        in_=pre[:].rearrange("p t r -> p r t"),
-                        func=ACT.Relu,
-                    )
-                zq[c] = zpool.tile([P, ROWS], U32, tag="zq", name="zq%d" % c, align_bytes=64)
-                zs[c] = zpool.tile([P, ROWS], U8, tag="zs", name="zs%d" % c, align_bytes=64)
-                nc.vector.quantize_mx(out=zq[c][:].bitcast(FP8X4), scales=zs[c][:], in_=z[:])
+            return banks
+
+        def relu_from_psum(u, c, banks):
+            for r in T_CHUNKS:
+                nc.scalar.activation(
+                    out=z[(u, c)][:, 4 * P * r : 4 * P * (r + 1)].rearrange("p (r t) -> p r t", t=4),
+                    in_=banks[(c, r)][:].rearrange("p t r -> p r t"),
+                    func=ACT.Relu,
+                )
+
+        def sums_on_vector(u, c):
+            nc.vector.tensor_tensor(
+                out=z[(u, c)][:, 0 : 4 * N_A].rearrange("p (g i t) -> p g i t", i=NODES, t=4),
+                in0=a_sb[:, c, :, :].rearrange("p (g i) t -> p g i t", i=NODES),
+                in1=b_sb[:, c, :, :]
+                .rearrange("p (g j) t -> p g j t", j=NODES)[:, :, u, :]
+                .unsqueeze(2)
+                .to_broadcast([P, N_A // NODES, NODES, 4]),
+                op=ALU.add,
+            )
+            nc.scalar.activation(out=z[(u, c)][:, 0 : 4 * N_A], in_=z[(u, c)][:, 0 : 4 * N_A], func=ACT.Relu)
+
+        def quantise_z(u, c):
+            zq[(u, c)] = zpool.tile([P, ROWS], U32, tag="zq", name="zq%d" % c, align_bytes=64)
+            zs[(u, c)] = zpool.tile([P, ROWS], U8, tag="zs", name="zs%d" % c, align_bytes=64)
+            nc.vector.quantize_mx(out=zq[(u, c)][:].bitcast(FP8X4), scales=zs[(u, c)][:], in_=z[(u, c)][:])
+
+        def second_layer(u):
+            ms = {}
             for r in range(CHUNKS):
                 cols = slice(P * r, P * r + P)
-                m = m_pool.tile([P, D], F32, tag="m")
+                ms[r] = m_pool.tile([P, D], F32, tag="m", name="m%d" % r)
                 for c in range(2):
                     nc.tensor.matmul_mx(
-                        out=m[:],
-                        lhsT=zq[c][:, cols].bitcast(FP8X4),
-                        lhsT_scale=zs[c][:, cols],
+                        out=ms[r][:],
+                        lhsT=zq[(u, c)][:, cols].bitcast(FP8X4),
+                        lhsT_scale=zs[(u, c)][:, cols],
                         rhs=w2q[:, c, :].bitcast(FP8X4),
                         rhs_scale=w2s[:, c, :],
                         start=(c == 0),
                         stop=(c == 1),
                     )
-                nc.vector.scalar_tensor_tensor(
-                    out=acc[:, r, :],
-                    in0=m[:],
-                    scalar=masku[:, r, u : u + 1],
-                    in1=acc[:, r, :],
-                    op0=ALU.mult,
-                    op1=ALU.add,
-                )
+            return ms
 
+        def add_masked(u, r, ms):
+            nc.vector.scalar_tensor_tensor(
+                out=acc[:, r, :], in0=ms[r][:], scalar=masku[:, r, u : u + 1], in1=acc[:, r, :],
+                op0=ALU.mult, op1=ALU.add,
+            )
+
+        new_z(0)
+        sums_on_vector(0, 0)
+        first_layer_out(1, banks1)
+        pre0 = sums_on_tensor(0)
+        relu_from_psum(0, 0, pre0)
+        sums_on_vector(0, 1)
+        relu_from_psum(0, 1, pre0)
+
+        for u in range(NODES):
+            more = u + 1 < NODES
+            if more:
+                pre_next = sums_on_tensor(u + 1)
+            quantise_z(u, 0)
+            quantise_z(u, 1)
+            if u == 0:
+                for c in range(2):
+                    nc.vector.quantize_mx(out=w2q[:, c, :].bitcast(FP8X4), scales=w2s[:, c, :], in_=g2[c][:])
+            ms = second_layer(u)
+            if more:
+                new_z(u + 1)
+                relu_from_psum(u + 1, 0, pre_next)
+                sums_on_vector(u + 1, 0)
+                relu_from_psum(u + 1, 1, pre_next)
+                sums_on_vector(u + 1, 1)
+                for r in range(CHUNKS):
+                    add_masked(u, r, ms)
+
+        mv = {}
+        rstd = {}
+        y = {}
         for r in range(CHUNKS):
+            add_masked(NODES - 1, r, ms)
             stats = small.tile([P, 6], F32, tag="stats")
             nc.vector.bn_stats(out=stats[:], in_=acc[:, r, :])
-            mv = small.tile([P, 2], F32, tag="mv")
-            nc.vector.bn_aggr(out=mv[:], in_=stats[:])
+            mv[r] = small.tile([P, 2], F32, tag="mv", name="mv%d" % r)
+            nc.vector.bn_aggr(out=mv[r][:], in_=stats[:])
             ve = small.tile([P, 1], F32, tag="ve")
-            nc.vector.tensor_scalar_add(out=ve[:], in0=mv[:, 1:2], scalar1=256.0 * EPS)
+            nc.vector.tensor_scalar_add(out=ve[:], in0=mv[r][:, 1:2], scalar1=EPS)
             sd = small.tile([P, 1], F32, tag="sd")
             nc.scalar.sqrt(out=sd[:], in_=ve[:])
-            rstd = small.tile([P, 1], F32, tag="rstd")
-            nc.vector.reciprocal(out=rstd[:], in_=sd[:])
-            y = stage.tile([P, D], F32, tag="y")
-            nc.vector.tensor_scalar(
-                out=y[:], in0=acc[:, r, :], scalar1=mv[:, 0:1], scalar2=rstd[:], op0=ALU.subtract, op1=ALU.mult
+            y[r] = small.tile([P, D], F32, tag="y", name="y%d" % r)
+            nc.vector.scalar_tensor_tensor(
+                out=y[r][:], in0=acc[:, r, :], scalar=mv[r][:, 0:1], in1=gamma_bc[:], op0=ALU.subtract, op1=ALU.mult
             )
-            nc.vector.tensor_tensor(out=y[:], in0=y[:], in1=gamma_bc[:], op=ALU.mult)
-            nc.vector.tensor_tensor(out=y[:], in0=y[:], in1=beta_bc[:], op=ALU.add)
-            nc.sync.dma_start(out=out_flat[P * r : P * r + P, :], in_=y[:])
+            rstd[r] = small.tile([P, 1], F32, tag="rstd", name="rstd%d" % r)
+            nc.vector.reciprocal(out=rstd[r][:], in_=sd[:])
+            nc.vector.scalar_tensor_tensor(
+                out=y[r][:], in0=y[r][:], scalar=rstd[r][:], in1=beta_bc[:], op0=ALU.mult, op1=ALU.add
+            )
+            nc.sync.dma_start(out=out_flat[P * r : P * r + P, :], in_=y[r][:])

@@ -38,7 +38,8 @@ def tile_simplegnn_pa_t_kernel(tc, h, adj_mask, w1a, w1b, b1, w2, b2, gamma, bet
         zpool = ctx.enter_context(tc.tile_pool(name="zpool", bufs=4))
         small = ctx.enter_context(tc.tile_pool(name="small", bufs=4))
         pre_pool = ctx.enter_context(tc.psum_pool(name="pre", bufs=4))
-        m_pool = ctx.enter_context(tc.psum_pool(name="m", bufs=4))
+        m_pool = ctx.enter_context(tc.psum_pool(name="m", bufs=2))
+        g_pool = ctx.enter_context(tc.psum_pool(name="g", bufs=2))
         ctx.enter_context(tc.manual_schedule())
 
         mask_sb = const.tile([P, CHUNKS, NODES], BF16)
@@ -94,24 +95,56 @@ def tile_simplegnn_pa_t_kernel(tc, h, adj_mask, w1a, w1b, b1, w2, b2, gamma, bet
             out=i16d[:, 0:NODES], in_=ident[:].rearrange("p (g i) -> p i g", i=NODES), axis=AX.X, op=ALU.add
         )
         nc.vector.tensor_copy(out=i16d[:, NODES : 2 * NODES], in_=i16d[:, 0:NODES])
-        sel = const.tile([P, NODES, NODES], F32)
+        sel2 = const.tile([P, NODES, NODES], F32)
         for u in range(NODES):
-            nc.vector.tensor_copy(out=sel[:, u, :], in_=i16d[:, NODES - u : 2 * NODES - u])
+            nc.vector.tensor_copy(out=sel2[:, u, :], in_=i16d[:, u : u + NODES])
+        bd8 = const.tile([P, 8], F32)
+        nc.vector.tensor_reduce(out=bd8[:], in_=ident_v, axis=AX.X, op=ALU.add)
+        maskf = const.tile([P, CHUNKS, NODES], F32)
+        nc.vector.tensor_copy(out=maskf[:], in_=mask_sb[:])
         mask16 = const.tile([P, CHUNKS, NODES], F32)
         nc.vector.tensor_scalar_mul(out=mask16[:], in0=mask_sb[:], scalar1=1.0 / NODES)
         deg16 = const.tile([P, CHUNKS], F32)
         nc.vector.tensor_reduce(out=deg16[:], in_=mask16[:], axis=AX.X, op=ALU.add)
-        masku = const.tile([P, CHUNKS, NODES], F32)
-        for r in A_CHUNKS:
-            nc.vector.tensor_copy(out=masku[:, r, :], in_=mask16[:, r, :])
-        for r in T_CHUNKS:
-            prod = small.tile([P, NODES, NODES], F32, tag="prod")
-            nc.vector.tensor_tensor(
-                out=prod[:], in0=sel[:], in1=mask16[:, r, :].unsqueeze(1).to_broadcast([P, NODES, NODES]), op=ALU.mult
-            )
-            nc.vector.tensor_reduce(out=masku[:, r, :], in_=prod[:], axis=AX.X, op=ALU.add)
+        degm1 = const.tile([P, CHUNKS], F32)
+        nc.vector.tensor_scalar_add(out=degm1[:], in0=deg16[:], scalar1=-1.0)
         b1f = const.tile([P, 2, 4], F32)
         nc.vector.tensor_copy(out=b1f[:], in_=b1_sb[:])
+        blk = const.tile([P, 2, 8, NODES], F32)
+        ps_e = pre_pool.tile([P, 2, P], F32, tag="pre")
+        adj_t = const.tile([P, 2, NODES], F32)
+        mt = const.tile([P, 2, NODES], F32)
+        for x, r in enumerate(T_CHUNKS):
+            nc.vector.tensor_tensor(
+                out=blk[:, x, :, :],
+                in0=bd8[:].unsqueeze(2).to_broadcast([P, 8, NODES]),
+                in1=maskf[:, r, :].unsqueeze(1).to_broadcast([P, 8, NODES]),
+                op=ALU.mult,
+            )
+            nc.tensor.transpose(ps_e[:, x, :], blk[:, x, :, :].rearrange("p g j -> p (g j)"), ident[:])
+        for x, r in enumerate(T_CHUNKS):
+            nc.vector.tensor_reduce(
+                out=adj_t[:, x, :], in_=ps_e[:, x, :].rearrange("p (g i) -> p i g", i=NODES), axis=AX.X, op=ALU.add
+            )
+            prod = small.tile([P, NODES, NODES], F32, tag="prod")
+            nc.vector.tensor_tensor(
+                out=prod[:], in0=sel2[:], in1=adj_t[:, x, :].unsqueeze(1).to_broadcast([P, NODES, NODES]), op=ALU.mult
+            )
+            nc.vector.tensor_reduce(out=mt[:, x, :], in_=prod[:], axis=AX.X, op=ALU.add)
+        protm = const.tile([P, 2, NODES, P], F32)
+
+        def mask_rotation(x, u, eng):
+            if eng == "v":
+                nc.vector.tensor_scalar_mul(out=protm[:, x, u, :], in0=prot[:, u, :], scalar1=mt[:, x, u : u + 1])
+            else:
+                nc.gpsimd.tensor_scalar(
+                    out=protm[:, x, u, :], in0=prot[:, u, :], scalar1=mt[:, x, u : u + 1], scalar2=0.0,
+                    op0=ALU.mult, op1=ALU.add,
+                )
+
+        for u in range(2):
+            for x in range(2):
+                mask_rotation(x, u, "v")
 
         gh = const.tile([P, 4 * ROWS], BF16, align_bytes=64)
         ghw = gh[:].bitcast(F32).rearrange("p (r u) -> p r u", u=2)
@@ -184,7 +217,10 @@ def tile_simplegnn_pa_t_kernel(tc, h, adj_mask, w1a, w1b, b1, w2, b2, gamma, bet
             for r in T_CHUNKS:
                 hcols = slice(P * r, P * r + P)
                 for o in ("a", "b"):
-                    banks[(o, r)] = m_pool.tile([P, 4, P], F32, tag="m", name="fx%s%d" % (o, r))
+                    if o == "a":
+                        banks[(o, r)] = m_pool.tile([P, 4, P], F32, tag="m", name="fxa%d" % r)
+                    else:
+                        banks[(o, r)] = g_pool.tile([P, 4, P], F32, tag="g", name="fxb%d" % r)
                     nc.tensor.matmul_mx(
                         out=banks[(o, r)][:].rearrange("p t f -> p (t f)"),
                         lhsT=hq[:, hcols].bitcast(FP8X4),
@@ -248,125 +284,157 @@ def tile_simplegnn_pa_t_kernel(tc, h, adj_mask, w1a, w1b, b1, w2, b2, gamma, bet
                 scalar1=1.0, scalar2=0.0, op0=ALU.mult, op1=ALU.add,
             )
 
+        for u in range(2, NODES):
+            for x in range(2):
+                mask_rotation(x, u, "g")
+
+        t_seq = ["za"] + list(range(NODES))
+        rounds = len(t_seq)
         z = {}
         zq = {}
         zs = {}
+        g_t = {}
 
-        def new_z(u):
+        def new_z(k):
             for c in range(2):
-                z[(u, c)] = zpool.tile([P, 4 * ROWS], BF16, tag="z", name="z%d" % c, align_bytes=64)
+                z[(k, c)] = zpool.tile([P, 4 * ROWS], BF16, tag="z", name="z%d" % c, align_bytes=64)
 
-        def sums_on_tensor(u):
+        def sums_on_tensor(k):
+            tu = t_seq[k]
             banks = {}
             for c in range(2):
-                for r in T_CHUNKS:
+                for x, r in enumerate(T_CHUNKS):
                     banks[(c, r)] = pre_pool.tile([P, 4, P], F32, tag="pre", name="pre%d%d" % (c, r))
                     for t in range(4):
-                        nc.tensor.matmul(
-                            out=banks[(c, r)][:, t, :], lhsT=xa[r][:, c, t, :], rhs=ident[:],
-                            is_transpose=True, start=True, stop=False,
-                        )
-                        nc.tensor.matmul(
-                            out=banks[(c, r)][:, t, :], lhsT=xb[r][:, c, t, :], rhs=prot[:, u, :],
-                            is_transpose=True, start=False, stop=True,
-                        )
+                        if tu == "za":
+                            nc.tensor.transpose(banks[(c, r)][:, t, :], xa[r][:, c, t, :], ident[:])
+                        else:
+                            nc.tensor.matmul(
+                                out=banks[(c, r)][:, t, :], lhsT=xb[r][:, c, t, :], rhs=protm[:, x, tu, :],
+                                is_transpose=True, start=True, stop=False,
+                            )
+                            nc.tensor.matmul(
+                                out=banks[(c, r)][:, t, :], lhsT=xa[r][:, c, t, :], rhs=ident[:],
+                                is_transpose=True, start=False, stop=True,
+                            )
             return banks
 
-        def relu_from_psum(u, c, banks):
+        def relu_from_psum(k, c, banks):
             for r in T_CHUNKS:
                 nc.scalar.activation(
-                    out=z[(u, c)][:, 4 * P * r : 4 * P * (r + 1)].rearrange("p (r t) -> p r t", t=4),
+                    out=z[(k, c)][:, 4 * P * r : 4 * P * (r + 1)].rearrange("p (r t) -> p r t", t=4),
                     in_=banks[(c, r)][:].rearrange("p t r -> p r t"),
                     func=ACT.Relu,
                 )
 
-        def sums_on_vector(u, c):
+        def sums_on_vector(k, c):
             nc.vector.tensor_tensor(
-                out=z[(u, c)][:, 0 : 4 * N_A].rearrange("p (g i t) -> p g i t", i=NODES, t=4),
+                out=z[(k, c)][:, 0 : 4 * N_A].rearrange("p (g i t) -> p g i t", i=NODES, t=4),
                 in0=a_sb[:, c, :, :].rearrange("p (g i) t -> p g i t", i=NODES),
                 in1=b_sb[:, c, :, :]
-                .rearrange("p (g j) t -> p g j t", j=NODES)[:, :, u, :]
+                .rearrange("p (g j) t -> p g j t", j=NODES)[:, :, k, :]
                 .unsqueeze(2)
                 .to_broadcast([P, N_A // NODES, NODES, 4]),
                 op=ALU.add,
             )
-            nc.scalar.activation(out=z[(u, c)][:, 0 : 4 * N_A], in_=z[(u, c)][:, 0 : 4 * N_A], func=ACT.Relu)
+            nc.scalar.activation(out=z[(k, c)][:, 0 : 4 * N_A], in_=z[(k, c)][:, 0 : 4 * N_A], func=ACT.Relu)
 
-        def quantise_z(u, c):
-            zq[(u, c)] = zpool.tile([P, ROWS], U32, tag="zq", name="zq%d" % c, align_bytes=64)
-            zs[(u, c)] = zpool.tile([P, ROWS], U8, tag="zs", name="zs%d" % c, align_bytes=64)
-            nc.vector.quantize_mx(out=zq[(u, c)][:].bitcast(FP8X4), scales=zs[(u, c)][:], in_=z[(u, c)][:])
+        def quantise_z(k, c):
+            zq[(k, c)] = zpool.tile([P, ROWS], U32, tag="zq", name="zq%d" % c, align_bytes=64)
+            zs[(k, c)] = zpool.tile([P, ROWS], U8, tag="zs", name="zs%d" % c, align_bytes=64)
+            lo = 0 if k < NODES else N_A
+            nc.vector.quantize_mx(
+                out=zq[(k, c)][:, lo:ROWS].bitcast(FP8X4), scales=zs[(k, c)][:, lo:ROWS], in_=z[(k, c)][:, 4 * lo : 4 * ROWS]
+            )
 
-        def second_layer(u):
+        def mx_pass(dst, k, c, r, start, stop):
+            cols = slice(P * r, P * r + P)
+            nc.tensor.matmul_mx(
+                out=dst,
+                lhsT=zq[(k, c)][:, cols].bitcast(FP8X4),
+                lhsT_scale=zs[(k, c)][:, cols],
+                rhs=w2q[:, c, :].bitcast(FP8X4),
+                rhs_scale=w2s[:, c, :],
+                start=start,
+                stop=stop,
+            )
+
+        def second_layer(k):
+            tu = t_seq[k]
             ms = {}
-            for r in range(CHUNKS):
-                cols = slice(P * r, P * r + P)
-                ms[r] = m_pool.tile([P, D], F32, tag="m", name="m%d" % r)
-                for c in range(2):
-                    nc.tensor.matmul_mx(
-                        out=ms[r][:],
-                        lhsT=zq[(u, c)][:, cols].bitcast(FP8X4),
-                        lhsT_scale=zs[(u, c)][:, cols],
-                        rhs=w2q[:, c, :].bitcast(FP8X4),
-                        rhs_scale=w2s[:, c, :],
-                        start=(c == 0),
-                        stop=(c == 1),
-                    )
+            if k < NODES:
+                for r in A_CHUNKS:
+                    ms[r] = m_pool.tile([P, D], F32, tag="m", name="m%d" % r)
+                    for c in range(2):
+                        mx_pass(ms[r][:], k, c, r, c == 0, c == 1)
+            for r in T_CHUNKS:
+                if tu == "za":
+                    ms[r] = g_pool.tile([P, D], F32, tag="g", name="mz%d" % r)
+                    for c in range(2):
+                        mx_pass(ms[r][:], k, c, r, c == 0, c == 1)
+                else:
+                    if tu == 0:
+                        g_t[r] = g_pool.tile([P, D], F32, tag="g", name="gt%d" % r)
+                    for c in range(2):
+                        mx_pass(g_t[r][:], k, c, r, tu == 0 and c == 0, tu == NODES - 1 and c == 1)
             return ms
 
-        def add_masked(u, r, ms):
+        def add_scaled(r, src, factor):
             nc.vector.scalar_tensor_tensor(
-                out=acc[:, r, :], in0=ms[r][:], scalar=masku[:, r, u : u + 1], in1=acc[:, r, :],
-                op0=ALU.mult, op1=ALU.add,
+                out=acc[:, r, :], in0=src, scalar=factor, in1=acc[:, r, :], op0=ALU.mult, op1=ALU.add
             )
+
+        def layer_norm(r):
+            stats = small.tile([P, 6], F32, tag="stats")
+            nc.vector.bn_stats(out=stats[:], in_=acc[:, r, :])
+            mv = small.tile([P, 2], F32, tag="mv")
+            nc.vector.bn_aggr(out=mv[:], in_=stats[:])
+            ve = small.tile([P, 1], F32, tag="ve")
+            nc.vector.tensor_scalar_add(out=ve[:], in0=mv[:, 1:2], scalar1=EPS)
+            sd = small.tile([P, 1], F32, tag="sd")
+            nc.scalar.sqrt(out=sd[:], in_=ve[:])
+            y = small.tile([P, D], F32, tag="y")
+            nc.vector.scalar_tensor_tensor(
+                out=y[:], in0=acc[:, r, :], scalar=mv[:, 0:1], in1=gamma_bc[:], op0=ALU.subtract, op1=ALU.mult
+            )
+            rstd = small.tile([P, 1], F32, tag="rstd")
+            nc.vector.reciprocal(out=rstd[:], in_=sd[:])
+            nc.vector.scalar_tensor_tensor(
+                out=y[:], in0=y[:], scalar=rstd[:], in1=beta_bc[:], op0=ALU.mult, op1=ALU.add
+            )
+            nc.sync.dma_start(out=out_flat[P * r : P * r + P, :], in_=y[:])
 
         new_z(0)
         sums_on_vector(0, 0)
         first_layer_out(1, banks1)
-        pre0 = sums_on_tensor(0)
-        relu_from_psum(0, 0, pre0)
+        pre_next = sums_on_tensor(0)
+        relu_from_psum(0, 0, pre_next)
         sums_on_vector(0, 1)
-        relu_from_psum(0, 1, pre0)
+        relu_from_psum(0, 1, pre_next)
 
-        for u in range(NODES):
-            more = u + 1 < NODES
-            if more:
-                pre_next = sums_on_tensor(u + 1)
-            quantise_z(u, 0)
-            quantise_z(u, 1)
-            if u == 0:
+        for k in range(rounds):
+            if k + 1 < rounds:
+                pre_next = sums_on_tensor(k + 1)
+            quantise_z(k, 0)
+            quantise_z(k, 1)
+            if k == 0:
                 for c in range(2):
                     nc.vector.quantize_mx(out=w2q[:, c, :].bitcast(FP8X4), scales=w2s[:, c, :], in_=g2[c][:])
-            ms = second_layer(u)
-            if more:
-                new_z(u + 1)
-                relu_from_psum(u + 1, 0, pre_next)
-                sums_on_vector(u + 1, 0)
-                relu_from_psum(u + 1, 1, pre_next)
-                sums_on_vector(u + 1, 1)
-                for r in range(CHUNKS):
-                    add_masked(u, r, ms)
-
-        mv = {}
-        rstd = {}
-        y = {}
-        for r in range(CHUNKS):
-            add_masked(NODES - 1, r, ms)
-            stats = small.tile([P, 6], F32, tag="stats")
-            nc.vector.bn_stats(out=stats[:], in_=acc[:, r, :])
-            mv[r] = small.tile([P, 2], F32, tag="mv", name="mv%d" % r)
-            nc.vector.bn_aggr(out=mv[r][:], in_=stats[:])
-            ve = small.tile([P, 1], F32, tag="ve")
-            nc.vector.tensor_scalar_add(out=ve[:], in0=mv[r][:, 1:2], scalar1=EPS)
-            sd = small.tile([P, 1], F32, tag="sd")
-            nc.scalar.sqrt(out=sd[:], in_=ve[:])
-            y[r] = small.tile([P, D], F32, tag="y", name="y%d" % r)
-            nc.vector.scalar_tensor_tensor(
-                out=y[r][:], in0=acc[:, r, :], scalar=mv[r][:, 0:1], in1=gamma_bc[:], op0=ALU.subtract, op1=ALU.mult
-            )
-            rstd[r] = small.tile([P, 1], F32, tag="rstd", name="rstd%d" % r)
-            nc.vector.reciprocal(out=rstd[r][:], in_=sd[:])
-            nc.vector.scalar_tensor_tensor(
-                out=y[r][:], in0=y[r][:], scalar=rstd[r][:], in1=beta_bc[:], op0=ALU.mult, op1=ALU.add
-            )
-            nc.sync.dma_start(out=out_flat[P * r : P * r + P, :], in_=y[r][:])
+            ms = second_layer(k)
+            if k + 1 < rounds:
+                new_z(k + 1)
+                for c in range(2):
+                    relu_from_psum(k + 1, c, pre_next)
+                    if k + 1 < NODES:
+                        sums_on_vector(k + 1, c)
+            if k < NODES:
+                for r in A_CHUNKS:
+                    add_scaled(r, ms[r][:], mask16[:, r, k : k + 1])
+            if k == 0:
+                for r in T_CHUNKS:
+                    add_scaled(r, ms[r][:], degm1[:, r : r + 1])
+        for r in A_CHUNKS:
+            layer_norm(r)
+        for r in T_CHUNKS:
+            add_scaled(r, g_t[r][:], 1.0 / NODES)
+            layer_norm(r)

@@ -49,6 +49,8 @@ def tile_simplegnn_pa_t_kernel(tc, h, adj_mask, w1a, w1b, b1, w2, b2, gamma, bet
             nc.sync.dma_start(out=b1_sb[:], in_=b1.rearrange("(c p t) -> p c t", c=2, p=P, t=4))
         h_sb = const.tile([P, CHUNKS, D], BF16)
         nc.sync.dma_start(out=h_sb[:], in_=h_flat.rearrange("(r p) d -> p r d", p=P))
+        b2_bc = const.tile([P, D], BF16)
+        nc.sync.dma_start(out=b2_bc[:], in_=b2.partition_broadcast(P))
         raw1 = {}
         for o in ("a", "b"):
             raw1[o] = const.tile([P, 4, F], BF16, name="raw1" + o)
@@ -62,8 +64,6 @@ def tile_simplegnn_pa_t_kernel(tc, h, adj_mask, w1a, w1b, b1, w2, b2, gamma, bet
 
         load_w1("a", 0)
         load_w1("b", 0)
-        b2_bc = const.tile([P, D], BF16)
-        nc.sync.dma_start(out=b2_bc[:], in_=b2.partition_broadcast(P))
         b1_bc = const.tile([P, F], BF16)
         nc.sync.dma_start(out=b1_bc[:], in_=b1.partition_broadcast(P))
         load_w1("a", 1)
@@ -85,11 +85,6 @@ def tile_simplegnn_pa_t_kernel(tc, h, adj_mask, w1a, w1b, b1, w2, b2, gamma, bet
         ident_v = ident[:].rearrange("p (g i) -> p g i", i=NODES)
         nc.vector.tensor_copy(out=ident_d[:, :, 0:NODES], in_=ident_v)
         nc.vector.tensor_copy(out=ident_d[:, :, NODES : 2 * NODES], in_=ident_v)
-        prot = const.tile([P, NODES, P], F32)
-        for u in range(NODES):
-            nc.vector.tensor_copy(
-                out=prot[:, u, :].rearrange("p (g i) -> p g i", i=NODES), in_=ident_d[:, :, u : u + NODES]
-            )
         i16d = const.tile([P, 2 * NODES], F32)
         nc.vector.tensor_reduce(
             out=i16d[:, 0:NODES], in_=ident[:].rearrange("p (g i) -> p i g", i=NODES), axis=AX.X, op=ALU.add
@@ -122,29 +117,6 @@ def tile_simplegnn_pa_t_kernel(tc, h, adj_mask, w1a, w1b, b1, w2, b2, gamma, bet
                 op=ALU.mult,
             )
             nc.tensor.transpose(ps_e[:, x, :], blk[:, x, :, :].rearrange("p g j -> p (g j)"), ident[:])
-        for x, r in enumerate(T_CHUNKS):
-            nc.vector.tensor_reduce(
-                out=adj_t[:, x, :], in_=ps_e[:, x, :].rearrange("p (g i) -> p i g", i=NODES), axis=AX.X, op=ALU.add
-            )
-            prod = small.tile([P, NODES, NODES], F32, tag="prod")
-            nc.vector.tensor_tensor(
-                out=prod[:], in0=sel2[:], in1=adj_t[:, x, :].unsqueeze(1).to_broadcast([P, NODES, NODES]), op=ALU.mult
-            )
-            nc.vector.tensor_reduce(out=mt[:, x, :], in_=prod[:], axis=AX.X, op=ALU.add)
-        protm = const.tile([P, 2, NODES, P], F32)
-
-        def mask_rotation(x, u, eng):
-            if eng == "v":
-                nc.vector.tensor_scalar_mul(out=protm[:, x, u, :], in0=prot[:, u, :], scalar1=mt[:, x, u : u + 1])
-            else:
-                nc.gpsimd.tensor_scalar(
-                    out=protm[:, x, u, :], in0=prot[:, u, :], scalar1=mt[:, x, u : u + 1], scalar2=0.0,
-                    op0=ALU.mult, op1=ALU.add,
-                )
-
-        for u in range(2):
-            for x in range(2):
-                mask_rotation(x, u, "v")
 
         gh = const.tile([P, 4 * ROWS], BF16, align_bytes=64)
         ghw = gh[:].bitcast(F32).rearrange("p (r u) -> p r u", u=2)
@@ -254,6 +226,30 @@ def tile_simplegnn_pa_t_kernel(tc, h, adj_mask, w1a, w1b, b1, w2, b2, gamma, bet
 
         regroup_w1("a", 0, "v")
         regroup_w1("b", 0, "s")
+        for x, r in enumerate(T_CHUNKS):
+            nc.vector.tensor_reduce(
+                out=adj_t[:, x, :], in_=ps_e[:, x, :].rearrange("p (g i) -> p i g", i=NODES), axis=AX.X, op=ALU.add
+            )
+            prod = small.tile([P, NODES, NODES], F32, tag="prod")
+            nc.vector.tensor_tensor(
+                out=prod[:], in0=sel2[:], in1=adj_t[:, x, :].unsqueeze(1).to_broadcast([P, NODES, NODES]), op=ALU.mult
+            )
+            nc.vector.tensor_reduce(out=mt[:, x, :], in_=prod[:], axis=AX.X, op=ALU.add)
+        protm = const.tile([P, 2, NODES, P], F32)
+
+        def mask_rotation(x, u, eng):
+            dst = protm[:, x, u, :].rearrange("p (g i) -> p g i", i=NODES)
+            src = ident_d[:, :, u : u + NODES]
+            if eng == "v":
+                nc.vector.tensor_scalar_mul(out=dst, in0=src, scalar1=mt[:, x, u : u + 1])
+            else:
+                nc.gpsimd.tensor_scalar(
+                    out=dst, in0=src, scalar1=mt[:, x, u : u + 1], scalar2=0.0, op0=ALU.mult, op1=ALU.add
+                )
+
+        for u in range(2):
+            for x in range(2):
+                mask_rotation(x, u, "v")
         nc.vector.quantize_mx(out=hq[:].bitcast(FP8X4), scales=hs[:], in_=gh[:])
         quantise_w1("a", 0)
         regroup_w1("a", 1, "v")
@@ -299,25 +295,22 @@ def tile_simplegnn_pa_t_kernel(tc, h, adj_mask, w1a, w1b, b1, w2, b2, gamma, bet
             for c in range(2):
                 z[(k, c)] = zpool.tile([P, 4 * ROWS], BF16, tag="z", name="z%d" % c, align_bytes=64)
 
-        def sums_on_tensor(k):
+        def sums_on_tensor(k, c, banks):
             tu = t_seq[k]
-            banks = {}
-            for c in range(2):
-                for x, r in enumerate(T_CHUNKS):
-                    banks[(c, r)] = pre_pool.tile([P, 4, P], F32, tag="pre", name="pre%d%d" % (c, r))
-                    for t in range(4):
-                        if tu == "za":
-                            nc.tensor.transpose(banks[(c, r)][:, t, :], xa[r][:, c, t, :], ident[:])
-                        else:
-                            nc.tensor.matmul(
-                                out=banks[(c, r)][:, t, :], lhsT=xb[r][:, c, t, :], rhs=protm[:, x, tu, :],
-                                is_transpose=True, start=True, stop=False,
-                            )
-                            nc.tensor.matmul(
-                                out=banks[(c, r)][:, t, :], lhsT=xa[r][:, c, t, :], rhs=ident[:],
-                                is_transpose=True, start=False, stop=True,
-                            )
-            return banks
+            for x, r in enumerate(T_CHUNKS):
+                banks[(c, r)] = pre_pool.tile([P, 4, P], F32, tag="pre", name="pre%d%d" % (c, r))
+                for t in range(4):
+                    if tu == "za":
+                        nc.tensor.transpose(banks[(c, r)][:, t, :], xa[r][:, c, t, :], ident[:])
+                    else:
+                        nc.tensor.matmul(
+                            out=banks[(c, r)][:, t, :], lhsT=xb[r][:, c, t, :], rhs=protm[:, x, tu, :],
+                            is_transpose=True, start=True, stop=False,
+                        )
+                        nc.tensor.matmul(
+                            out=banks[(c, r)][:, t, :], lhsT=xa[r][:, c, t, :], rhs=ident[:],
+                            is_transpose=True, start=False, stop=True,
+                        )
 
         def relu_from_psum(k, c, banks):
             for r in T_CHUNKS:
@@ -337,7 +330,12 @@ def tile_simplegnn_pa_t_kernel(tc, h, adj_mask, w1a, w1b, b1, w2, b2, gamma, bet
                 .to_broadcast([P, N_A // NODES, NODES, 4]),
                 op=ALU.add,
             )
-            nc.scalar.activation(out=z[(k, c)][:, 0 : 4 * N_A], in_=z[(k, c)][:, 0 : 4 * N_A], func=ACT.Relu)
+
+        def relu_in_place(k, c, eng):
+            if eng == "s":
+                nc.scalar.activation(out=z[(k, c)][:, 0 : 4 * N_A], in_=z[(k, c)][:, 0 : 4 * N_A], func=ACT.Relu)
+            else:
+                nc.vector.tensor_scalar_max(out=z[(k, c)][:, 0 : 4 * N_A], in0=z[(k, c)][:, 0 : 4 * N_A], scalar1=0.0)
 
         def quantise_z(k, c):
             zq[(k, c)] = zpool.tile([P, ROWS], U32, tag="zq", name="zq%d" % c, align_bytes=64)
@@ -359,14 +357,14 @@ def tile_simplegnn_pa_t_kernel(tc, h, adj_mask, w1a, w1b, b1, w2, b2, gamma, bet
                 stop=stop,
             )
 
-        def second_layer(k):
+        def second_layer_a(k, ms):
+            for r in A_CHUNKS:
+                ms[r] = m_pool.tile([P, D], F32, tag="m", name="m%d" % r)
+                for c in range(2):
+                    mx_pass(ms[r][:], k, c, r, c == 0, c == 1)
+
+        def second_layer_t(k, ms):
             tu = t_seq[k]
-            ms = {}
-            if k < NODES:
-                for r in A_CHUNKS:
-                    ms[r] = m_pool.tile([P, D], F32, tag="m", name="m%d" % r)
-                    for c in range(2):
-                        mx_pass(ms[r][:], k, c, r, c == 0, c == 1)
             for r in T_CHUNKS:
                 if tu == "za":
                     ms[r] = g_pool.tile([P, D], F32, tag="g", name="mz%d" % r)
@@ -377,64 +375,105 @@ def tile_simplegnn_pa_t_kernel(tc, h, adj_mask, w1a, w1b, b1, w2, b2, gamma, bet
                         g_t[r] = g_pool.tile([P, D], F32, tag="g", name="gt%d" % r)
                     for c in range(2):
                         mx_pass(g_t[r][:], k, c, r, tu == 0 and c == 0, tu == NODES - 1 and c == 1)
-            return ms
 
         def add_scaled(r, src, factor):
             nc.vector.scalar_tensor_tensor(
                 out=acc[:, r, :], in0=src, scalar=factor, in1=acc[:, r, :], op0=ALU.mult, op1=ALU.add
             )
 
-        def layer_norm(r):
+        mv = {}
+        rstd = {}
+        sd = {}
+        y = {}
+
+        def ln_stats(r):
             stats = small.tile([P, 6], F32, tag="stats")
             nc.vector.bn_stats(out=stats[:], in_=acc[:, r, :])
-            mv = small.tile([P, 2], F32, tag="mv")
-            nc.vector.bn_aggr(out=mv[:], in_=stats[:])
+            mv[r] = small.tile([P, 2], F32, tag="mv", name="mv%d" % r)
+            nc.vector.bn_aggr(out=mv[r][:], in_=stats[:])
             ve = small.tile([P, 1], F32, tag="ve")
-            nc.vector.tensor_scalar_add(out=ve[:], in0=mv[:, 1:2], scalar1=EPS)
-            sd = small.tile([P, 1], F32, tag="sd")
-            nc.scalar.sqrt(out=sd[:], in_=ve[:])
-            y = small.tile([P, D], F32, tag="y")
-            nc.vector.scalar_tensor_tensor(
-                out=y[:], in0=acc[:, r, :], scalar=mv[:, 0:1], in1=gamma_bc[:], op0=ALU.subtract, op1=ALU.mult
+            nc.vector.tensor_scalar_add(out=ve[:], in0=mv[r][:, 1:2], scalar1=EPS)
+            sd[r] = small.tile([P, 1], F32, tag="sd", name="sd%d" % r)
+            nc.scalar.sqrt(out=sd[r][:], in_=ve[:])
+
+        def ln_rstd(r):
+            rstd[r] = small.tile([P, 1], F32, tag="rstd", name="rstd%d" % r)
+            nc.vector.reciprocal(out=rstd[r][:], in_=sd[r][:])
+
+        def ln_apply_gpsimd(r):
+            y[r] = small.tile([P, D], F32, tag="y", name="y%d" % r)
+            nc.gpsimd.tensor_scalar(
+                out=y[r][:], in0=acc[:, r, :], scalar1=mv[r][:, 0:1], scalar2=rstd[r][:], op0=ALU.subtract, op1=ALU.mult
             )
-            rstd = small.tile([P, 1], F32, tag="rstd")
-            nc.vector.reciprocal(out=rstd[:], in_=sd[:])
+            nc.gpsimd.tensor_tensor(out=y[r][:], in0=y[r][:], in1=gamma_bc[:], op=ALU.mult)
+            nc.gpsimd.tensor_tensor(out=y[r][:], in0=y[r][:], in1=beta_bc[:], op=ALU.add)
+            nc.sync.dma_start(out=out_flat[P * r : P * r + P, :], in_=y[r][:])
+
+        def ln_centre_vector(r):
+            y[r] = small.tile([P, D], F32, tag="y", name="y%d" % r)
             nc.vector.scalar_tensor_tensor(
-                out=y[:], in0=y[:], scalar=rstd[:], in1=beta_bc[:], op0=ALU.mult, op1=ALU.add
+                out=y[r][:], in0=acc[:, r, :], scalar=mv[r][:, 0:1], in1=gamma_bc[:], op0=ALU.subtract, op1=ALU.mult
             )
-            nc.sync.dma_start(out=out_flat[P * r : P * r + P, :], in_=y[:])
+
+        def ln_finish_vector(r):
+            nc.vector.scalar_tensor_tensor(
+                out=y[r][:], in0=y[r][:], scalar=rstd[r][:], in1=beta_bc[:], op0=ALU.mult, op1=ALU.add
+            )
+            nc.sync.dma_start(out=out_flat[P * r : P * r + P, :], in_=y[r][:])
 
         new_z(0)
         sums_on_vector(0, 0)
+        relu_in_place(0, 0, "s")
         first_layer_out(1, banks1)
-        pre_next = sums_on_tensor(0)
+        pre_next = {}
+        sums_on_tensor(0, 0, pre_next)
+        sums_on_tensor(0, 1, pre_next)
         relu_from_psum(0, 0, pre_next)
         sums_on_vector(0, 1)
+        relu_in_place(0, 1, "s")
         relu_from_psum(0, 1, pre_next)
 
         for k in range(rounds):
-            if k + 1 < rounds:
-                pre_next = sums_on_tensor(k + 1)
+            more = k + 1 < rounds
+            ms = {}
+            pre_next = {}
+            if more:
+                sums_on_tensor(k + 1, 0, pre_next)
             quantise_z(k, 0)
             quantise_z(k, 1)
             if k == 0:
                 for c in range(2):
                     nc.vector.quantize_mx(out=w2q[:, c, :].bitcast(FP8X4), scales=w2s[:, c, :], in_=g2[c][:])
-            ms = second_layer(k)
-            if k + 1 < rounds:
-                new_z(k + 1)
-                for c in range(2):
-                    relu_from_psum(k + 1, c, pre_next)
-                    if k + 1 < NODES:
-                        sums_on_vector(k + 1, c)
             if k < NODES:
-                for r in A_CHUNKS:
-                    add_scaled(r, ms[r][:], mask16[:, r, k : k + 1])
+                second_layer_a(k, ms)
+            if more:
+                sums_on_tensor(k + 1, 1, pre_next)
+            second_layer_t(k, ms)
+            if more:
+                new_z(k + 1)
+                relu_from_psum(k + 1, 0, pre_next)
+                if k + 1 < NODES:
+                    sums_on_vector(k + 1, 0)
+                    relu_in_place(k + 1, 0, "s")
+                    sums_on_vector(k + 1, 1)
+                relu_from_psum(k + 1, 1, pre_next)
+            if k < NODES:
+                add_scaled(A_CHUNKS[0], ms[A_CHUNKS[0]][:], mask16[:, A_CHUNKS[0], k : k + 1])
+                if k + 1 < NODES:
+                    relu_in_place(k + 1, 1, "v")
+                add_scaled(A_CHUNKS[1], ms[A_CHUNKS[1]][:], mask16[:, A_CHUNKS[1], k : k + 1])
             if k == 0:
                 for r in T_CHUNKS:
                     add_scaled(r, ms[r][:], degm1[:, r : r + 1])
         for r in A_CHUNKS:
-            layer_norm(r)
+            ln_stats(r)
+        for r in A_CHUNKS:
+            ln_rstd(r)
+            ln_apply_gpsimd(r)
         for r in T_CHUNKS:
             add_scaled(r, g_t[r][:], 1.0 / NODES)
-            layer_norm(r)
+            ln_stats(r)
+        for r in T_CHUNKS:
+            ln_centre_vector(r)
+            ln_rstd(r)
+            ln_finish_vector(r)

@@ -23,6 +23,7 @@ FLOPS = 2 * ROWS * D * F * 2 + 2 * ROWS * NODES * F * D
 A_CHUNKS = (0, 1)
 T_CHUNKS = (2, 3)
 N_A = 256
+ZA_AT = 8
 
 
 def tile_simplegnn_pa_t_kernel(tc, h, adj_mask, w1a, w1b, b1, w2, b2, gamma, beta, out):
@@ -162,50 +163,71 @@ def tile_simplegnn_pa_t_kernel(tc, h, adj_mask, w1a, w1b, b1, w2, b2, gamma, bet
 
         a_sb = const.tile([P, 2, N_A, 4], F32)
         b_sb = const.tile([P, 2, N_A, 4], F32)
+        at_sb = const.tile([P, ROWS - N_A, 4], F32)
         xa = {}
         xb = {}
         for r in T_CHUNKS:
             xa[r] = const.tile([P, 2, 4, P], F32, name="xa%d" % r)
             xb[r] = const.tile([P, 2, 4, P], F32, name="xb%d" % r)
 
-        def first_layer(c):
-            banks = {}
-            for r in A_CHUNKS:
+        def mx_lone(dst, lq, ls, lcols, rq, rs, rcols):
+            nc.tensor.matmul_mx(
+                out=dst,
+                lhsT=lq[:, lcols].bitcast(FP8X4),
+                lhsT_scale=ls[:, lcols],
+                rhs=rq[:, rcols].bitcast(FP8X4),
+                rhs_scale=rs[:, rcols],
+                start=True,
+                stop=True,
+            )
+
+        def first_layer_t(c, banks):
+            for r in T_CHUNKS:
                 hcols = slice(P * r, P * r + P)
+                banks[("a", r)] = m_pool.tile([P, 4, P], F32, tag="m", name="fxa%d" % r)
+                banks[("b", r)] = g_pool.tile([P, 4, P], F32, tag="g", name="fxb%d" % r)
+                if c == 0:
+                    for t in range(4):
+                        mx_lone(banks[("a", r)][:, t, :], w1q["a"], w1s["a"], slice(P * t, P * t + P), hq, hs, hcols)
+                else:
+                    mx_lone(
+                        banks[("a", r)][:].rearrange("p t f -> p (t f)"), hq, hs, hcols,
+                        w1q["a"], w1s["a"], slice(512 * c, 512 * c + 512),
+                    )
+                mx_lone(
+                    banks[("b", r)][:].rearrange("p t f -> p (t f)"), hq, hs, hcols,
+                    w1q["b"], w1s["b"], slice(512 * c, 512 * c + 512),
+                )
+
+        def first_layer_a(c, banks):
+            for r in A_CHUNKS:
                 for o in ("a", "b"):
                     banks[(o, r)] = pre_pool.tile([P, 4, P], F32, tag="pre", name="fl%s%d" % (o, r))
                     for t in range(4):
-                        wcols = slice(512 * c + P * t, 512 * c + P * t + P)
-                        nc.tensor.matmul_mx(
-                            out=banks[(o, r)][:, t, :],
-                            lhsT=w1q[o][:, wcols].bitcast(FP8X4),
-                            lhsT_scale=w1s[o][:, wcols],
-                            rhs=hq[:, hcols].bitcast(FP8X4),
-                            rhs_scale=hs[:, hcols],
-                            start=True,
-                            stop=True,
+                        mx_lone(
+                            banks[(o, r)][:, t, :], w1q[o], w1s[o], slice(512 * c + P * t, 512 * c + P * t + P),
+                            hq, hs, slice(P * r, P * r + P),
                         )
-            wcols = slice(512 * c, 512 * c + 512)
-            for r in T_CHUNKS:
-                hcols = slice(P * r, P * r + P)
-                for o in ("a", "b"):
-                    if o == "a":
-                        banks[(o, r)] = m_pool.tile([P, 4, P], F32, tag="m", name="fxa%d" % r)
-                    else:
-                        banks[(o, r)] = g_pool.tile([P, 4, P], F32, tag="g", name="fxb%d" % r)
-                    nc.tensor.matmul_mx(
-                        out=banks[(o, r)][:].rearrange("p t f -> p (t f)"),
-                        lhsT=hq[:, hcols].bitcast(FP8X4),
-                        lhsT_scale=hs[:, hcols],
-                        rhs=w1q[o][:, wcols].bitcast(FP8X4),
-                        rhs_scale=w1s[o][:, wcols],
-                        start=True,
-                        stop=True,
-                    )
-            return banks
 
-        def first_layer_out(c, banks):
-            wcols = slice(512 * c, 512 * c + 512)
+        def first_layer_out_t(c, banks):
+            for r in T_CHUNKS:
+                nc.scalar.copy(out=xb[r][:, c, :, :], in_=banks[("b", r)][:])
+                if c == 0:
+                    nc.vector.tensor_tensor(
+                        out=at_sb[:, P * r - N_A : P * r - N_A + P, :],
+                        in0=banks[("a", r)][:].rearrange("p t r -> p r t"),
+                        in1=b1f[:, c, :].unsqueeze(1).to_broadcast([P, P, 4]),
+                        op=ALU.add,
+                    )
+                else:
+                    nc.vector.tensor_tensor(
+                        out=xa[r][:, c, :, :],
+                        in0=banks[("a", r)][:],
+                        in1=b1_bc[:, 512 * c : 512 * c + 512].rearrange("q (p t) -> q t p", t=4),
+                        op=ALU.add,
+                    )
+
+        def first_layer_out_a(c, banks):
             for r in A_CHUNKS:
                 rows = slice(P * r, P * r + P)
                 nc.scalar.copy(out=a_sb[:, c, rows, :], in_=banks[("a", r)][:].rearrange("p t r -> p r t"))
@@ -215,17 +237,11 @@ def tile_simplegnn_pa_t_kernel(tc, h, adj_mask, w1a, w1b, b1, w2, b2, gamma, bet
                     in1=b1f[:, c, :].unsqueeze(1).to_broadcast([P, P, 4]),
                     op=ALU.add,
                 )
-            for r in T_CHUNKS:
-                nc.scalar.copy(out=xb[r][:, c, :, :], in_=banks[("b", r)][:])
-                nc.vector.tensor_tensor(
-                    out=xa[r][:, c, :, :],
-                    in0=banks[("a", r)][:],
-                    in1=b1_bc[:, wcols].rearrange("q (p t) -> q t p", t=4),
-                    op=ALU.add,
-                )
 
         regroup_w1("a", 0, "v")
         regroup_w1("b", 0, "s")
+        nc.vector.quantize_mx(out=hq[:].bitcast(FP8X4), scales=hs[:], in_=gh[:])
+        quantise_w1("a", 0)
         for x, r in enumerate(T_CHUNKS):
             nc.vector.tensor_reduce(
                 out=adj_t[:, x, :], in_=ps_e[:, x, :].rearrange("p (g i) -> p i g", i=NODES), axis=AX.X, op=ALU.add
@@ -250,27 +266,36 @@ def tile_simplegnn_pa_t_kernel(tc, h, adj_mask, w1a, w1b, b1, w2, b2, gamma, bet
         for u in range(2):
             for x in range(2):
                 mask_rotation(x, u, "v")
-        nc.vector.quantize_mx(out=hq[:].bitcast(FP8X4), scales=hs[:], in_=gh[:])
-        quantise_w1("a", 0)
-        regroup_w1("a", 1, "v")
         quantise_w1("b", 0)
-        banks0 = first_layer(0)
-        regroup_w1("b", 1, "v")
+        banks0 = {}
+        first_layer_t(0, banks0)
+        first_layer_a(0, banks0)
+        regroup_w1("a", 1, "v")
+        regroup_w1("b", 1, "s")
         quantise_w1("a", 1)
-        first_layer_out(0, banks0)
+        first_layer_out_t(0, banks0)
         quantise_w1("b", 1)
-        banks1 = first_layer(1)
+        banks1 = {}
+        first_layer_t(1, banks1)
+        first_layer_out_a(0, banks0)
+        first_layer_a(1, banks1)
+        first_layer_out_t(1, banks1)
+        first_layer_out_a(1, banks1)
+        acc = const.tile([P, CHUNKS, D], F32)
+
+        def start_acc():
+            for r in range(CHUNKS):
+                nc.vector.scalar_tensor_tensor(
+                    out=acc[:, r, :], in0=b2_bc[:], scalar=deg16[:, r : r + 1], in1=h_sb[:, r, :],
+                    op0=ALU.mult, op1=ALU.add,
+                )
 
         w2q = const.tile([P, 2, D], U32, align_bytes=64)
         w2s = const.tile([P, 2, D], U8, align_bytes=64)
 
-        acc = const.tile([P, CHUNKS, D], F32)
-        for r in range(CHUNKS):
-            t1 = stage.tile([P, D], F32, tag="t1")
-            nc.gpsimd.tensor_scalar(
-                out=t1[:], in0=b2_bc[:], scalar1=deg16[:, r : r + 1], scalar2=0.0, op0=ALU.mult, op1=ALU.add
-            )
-            nc.gpsimd.tensor_tensor(out=acc[:, r, :], in0=t1[:], in1=h_sb[:, r, :], op=ALU.add)
+        for u in range(2, 4):
+            for x in range(2):
+                mask_rotation(x, u, "g")
         g2 = {}
         for c in range(2):
             g2[c] = const.tile([P, 2048], BF16, name="g2%d" % c, align_bytes=64)
@@ -280,10 +305,11 @@ def tile_simplegnn_pa_t_kernel(tc, h, adj_mask, w1a, w1b, b1, w2, b2, gamma, bet
                 scalar1=1.0, scalar2=0.0, op0=ALU.mult, op1=ALU.add,
             )
 
-        for u in range(2, NODES):
+        for u in range(4, NODES):
             for x in range(2):
                 mask_rotation(x, u, "g")
 
+        a_seq = list(range(NODES)) + [None]
         t_seq = ["za"] + list(range(NODES))
         rounds = len(t_seq)
         z = {}
@@ -295,37 +321,57 @@ def tile_simplegnn_pa_t_kernel(tc, h, adj_mask, w1a, w1b, b1, w2, b2, gamma, bet
             for c in range(2):
                 z[(k, c)] = zpool.tile([P, 4 * ROWS], BF16, tag="z", name="z%d" % c, align_bytes=64)
 
-        def sums_on_tensor(k, c, banks):
+        def sums_on_tensor(k, banks):
             tu = t_seq[k]
             for x, r in enumerate(T_CHUNKS):
-                banks[(c, r)] = pre_pool.tile([P, 4, P], F32, tag="pre", name="pre%d%d" % (c, r))
+                banks[(1, r)] = pre_pool.tile([P, 4, P], F32, tag="pre", name="pre1%d" % r)
                 for t in range(4):
                     if tu == "za":
-                        nc.tensor.transpose(banks[(c, r)][:, t, :], xa[r][:, c, t, :], ident[:])
+                        nc.tensor.transpose(banks[(1, r)][:, t, :], xa[r][:, 1, t, :], ident[:])
                     else:
                         nc.tensor.matmul(
-                            out=banks[(c, r)][:, t, :], lhsT=xb[r][:, c, t, :], rhs=protm[:, x, tu, :],
+                            out=banks[(1, r)][:, t, :], lhsT=xb[r][:, 1, t, :], rhs=protm[:, x, tu, :],
                             is_transpose=True, start=True, stop=False,
                         )
                         nc.tensor.matmul(
-                            out=banks[(c, r)][:, t, :], lhsT=xa[r][:, c, t, :], rhs=ident[:],
+                            out=banks[(1, r)][:, t, :], lhsT=xa[r][:, 1, t, :], rhs=ident[:],
                             is_transpose=True, start=False, stop=True,
                         )
+            if tu != "za":
+                for x, r in enumerate(T_CHUNKS):
+                    banks[(0, r)] = pre_pool.tile([P, 4, P], F32, tag="pre", name="pre0%d" % r)
+                    for t in range(4):
+                        nc.tensor.transpose(banks[(0, r)][:, t, :], xb[r][:, 0, t, :], protm[:, x, tu, :])
 
-        def relu_from_psum(k, c, banks):
+        def relu_from_psum(k, banks):
             for r in T_CHUNKS:
                 nc.scalar.activation(
-                    out=z[(k, c)][:, 4 * P * r : 4 * P * (r + 1)].rearrange("p (r t) -> p r t", t=4),
-                    in_=banks[(c, r)][:].rearrange("p t r -> p r t"),
+                    out=z[(k, 1)][:, 4 * P * r : 4 * P * (r + 1)].rearrange("p (r t) -> p r t", t=4),
+                    in_=banks[(1, r)][:].rearrange("p t r -> p r t"),
                     func=ACT.Relu,
                 )
+
+        def sums_from_psum(k, banks):
+            if t_seq[k] == "za":
+                nc.scalar.activation(
+                    out=z[(k, 0)][:, 4 * N_A : 4 * ROWS], in_=at_sb[:].rearrange("p r t -> p (r t)"), func=ACT.Relu
+                )
+                return
+            for r in T_CHUNKS:
+                nc.vector.tensor_tensor(
+                    out=z[(k, 0)][:, 4 * P * r : 4 * P * (r + 1)].rearrange("p (r t) -> p r t", t=4),
+                    in0=banks[(0, r)][:].rearrange("p t r -> p r t"),
+                    in1=at_sb[:, P * r - N_A : P * r - N_A + P, :],
+                    op=ALU.add,
+                )
+            nc.scalar.activation(out=z[(k, 0)][:, 4 * N_A : 4 * ROWS], in_=z[(k, 0)][:, 4 * N_A : 4 * ROWS], func=ACT.Relu)
 
         def sums_on_vector(k, c):
             nc.vector.tensor_tensor(
                 out=z[(k, c)][:, 0 : 4 * N_A].rearrange("p (g i t) -> p g i t", i=NODES, t=4),
                 in0=a_sb[:, c, :, :].rearrange("p (g i) t -> p g i t", i=NODES),
                 in1=b_sb[:, c, :, :]
-                .rearrange("p (g j) t -> p g j t", j=NODES)[:, :, k, :]
+                .rearrange("p (g j) t -> p g j t", j=NODES)[:, :, a_seq[k], :]
                 .unsqueeze(2)
                 .to_broadcast([P, N_A // NODES, NODES, 4]),
                 op=ALU.add,
@@ -340,7 +386,7 @@ def tile_simplegnn_pa_t_kernel(tc, h, adj_mask, w1a, w1b, b1, w2, b2, gamma, bet
         def quantise_z(k, c):
             zq[(k, c)] = zpool.tile([P, ROWS], U32, tag="zq", name="zq%d" % c, align_bytes=64)
             zs[(k, c)] = zpool.tile([P, ROWS], U8, tag="zs", name="zs%d" % c, align_bytes=64)
-            lo = 0 if k < NODES else N_A
+            lo = N_A if a_seq[k] is None else 0
             nc.vector.quantize_mx(
                 out=zq[(k, c)][:, lo:ROWS].bitcast(FP8X4), scales=zs[(k, c)][:, lo:ROWS], in_=z[(k, c)][:, 4 * lo : 4 * ROWS]
             )
@@ -421,59 +467,53 @@ def tile_simplegnn_pa_t_kernel(tc, h, adj_mask, w1a, w1b, b1, w2, b2, gamma, bet
             )
             nc.sync.dma_start(out=out_flat[P * r : P * r + P, :], in_=y[r][:])
 
-        new_z(0)
-        sums_on_vector(0, 0)
-        relu_in_place(0, 0, "s")
-        first_layer_out(1, banks1)
+        def prepare(k, banks):
+            new_z(k)
+            relu_from_psum(k, banks)
+            if a_seq[k] is not None:
+                for c in range(2):
+                    sums_on_vector(k, c)
+                    relu_in_place(k, c, "s")
+            sums_from_psum(k, banks)
+
+        def ln_apply(r):
+            ln_centre_vector(r)
+            ln_rstd(r)
+            ln_finish_vector(r)
+
         pre_next = {}
-        sums_on_tensor(0, 0, pre_next)
-        sums_on_tensor(0, 1, pre_next)
-        relu_from_psum(0, 0, pre_next)
-        sums_on_vector(0, 1)
-        relu_in_place(0, 1, "s")
-        relu_from_psum(0, 1, pre_next)
+        sums_on_tensor(0, pre_next)
+        start_acc()
+        prepare(0, pre_next)
 
         for k in range(rounds):
             more = k + 1 < rounds
             ms = {}
             pre_next = {}
             if more:
-                sums_on_tensor(k + 1, 0, pre_next)
-            quantise_z(k, 0)
+                sums_on_tensor(k + 1, pre_next)
             quantise_z(k, 1)
+            quantise_z(k, 0)
             if k == 0:
                 for c in range(2):
                     nc.vector.quantize_mx(out=w2q[:, c, :].bitcast(FP8X4), scales=w2s[:, c, :], in_=g2[c][:])
-            if k < NODES:
+            if a_seq[k] is not None:
                 second_layer_a(k, ms)
-            if more:
-                sums_on_tensor(k + 1, 1, pre_next)
             second_layer_t(k, ms)
             if more:
-                new_z(k + 1)
-                relu_from_psum(k + 1, 0, pre_next)
-                if k + 1 < NODES:
-                    sums_on_vector(k + 1, 0)
-                    relu_in_place(k + 1, 0, "s")
-                    sums_on_vector(k + 1, 1)
-                relu_from_psum(k + 1, 1, pre_next)
-            if k < NODES:
-                add_scaled(A_CHUNKS[0], ms[A_CHUNKS[0]][:], mask16[:, A_CHUNKS[0], k : k + 1])
-                if k + 1 < NODES:
-                    relu_in_place(k + 1, 1, "v")
-                add_scaled(A_CHUNKS[1], ms[A_CHUNKS[1]][:], mask16[:, A_CHUNKS[1], k : k + 1])
-            if k == 0:
-                for r in T_CHUNKS:
-                    add_scaled(r, ms[r][:], degm1[:, r : r + 1])
+                prepare(k + 1, pre_next)
+                for r in A_CHUNKS:
+                    add_scaled(r, ms[r][:], mask16[:, r, a_seq[k] : a_seq[k] + 1])
+                if t_seq[k] == "za":
+                    for r in T_CHUNKS:
+                        add_scaled(r, ms[r][:], degm1[:, r : r + 1])
+
         for r in A_CHUNKS:
             ln_stats(r)
         for r in A_CHUNKS:
-            ln_rstd(r)
-            ln_apply_gpsimd(r)
+            ln_apply(r)
         for r in T_CHUNKS:
             add_scaled(r, g_t[r][:], 1.0 / NODES)
             ln_stats(r)
         for r in T_CHUNKS:
-            ln_centre_vector(r)
-            ln_rstd(r)
-            ln_finish_vector(r)
+            ln_apply(r)

@@ -23,7 +23,8 @@ FLOPS = 2 * ROWS * D * F * 2 + 2 * ROWS * NODES * F * D
 A_CHUNKS = (0, 1)
 T_CHUNKS = (2, 3)
 N_A = 256
-ZA_AT = 8
+V_SLOTS = ((2, 0),)
+T_SLOTS = ((2, 1), (3, 1), (3, 0))
 
 
 def tile_simplegnn_pa_t_kernel(tc, h, adj_mask, w1a, w1b, b1, w2, b2, gamma, beta, out):
@@ -50,8 +51,6 @@ def tile_simplegnn_pa_t_kernel(tc, h, adj_mask, w1a, w1b, b1, w2, b2, gamma, bet
             nc.sync.dma_start(out=b1_sb[:], in_=b1.rearrange("(c p t) -> p c t", c=2, p=P, t=4))
         h_sb = const.tile([P, CHUNKS, D], BF16)
         nc.sync.dma_start(out=h_sb[:], in_=h_flat.rearrange("(r p) d -> p r d", p=P))
-        b2_bc = const.tile([P, D], BF16)
-        nc.sync.dma_start(out=b2_bc[:], in_=b2.partition_broadcast(P))
         raw1 = {}
         for o in ("a", "b"):
             raw1[o] = const.tile([P, 4, F], BF16, name="raw1" + o)
@@ -67,6 +66,8 @@ def tile_simplegnn_pa_t_kernel(tc, h, adj_mask, w1a, w1b, b1, w2, b2, gamma, bet
         load_w1("b", 0)
         b1_bc = const.tile([P, F], BF16)
         nc.sync.dma_start(out=b1_bc[:], in_=b1.partition_broadcast(P))
+        b2_bc = const.tile([P, D], BF16)
+        nc.sync.dma_start(out=b2_bc[:], in_=b2.partition_broadcast(P))
         load_w1("a", 1)
         load_w1("b", 1)
         raw2 = const.tile([P, 2, 4, D], BF16)
@@ -163,7 +164,9 @@ def tile_simplegnn_pa_t_kernel(tc, h, adj_mask, w1a, w1b, b1, w2, b2, gamma, bet
 
         a_sb = const.tile([P, 2, N_A, 4], F32)
         b_sb = const.tile([P, 2, N_A, 4], F32)
-        at_sb = const.tile([P, ROWS - N_A, 4], F32)
+        at_sb = {}
+        for r, c in V_SLOTS:
+            at_sb[(r, c)] = const.tile([P, P, 4], F32, name="at%d%d" % (r, c))
         xa = {}
         xb = {}
         for r in T_CHUNKS:
@@ -186,9 +189,12 @@ def tile_simplegnn_pa_t_kernel(tc, h, adj_mask, w1a, w1b, b1, w2, b2, gamma, bet
                 hcols = slice(P * r, P * r + P)
                 banks[("a", r)] = m_pool.tile([P, 4, P], F32, tag="m", name="fxa%d" % r)
                 banks[("b", r)] = g_pool.tile([P, 4, P], F32, tag="g", name="fxb%d" % r)
-                if c == 0:
+                if (r, c) in V_SLOTS:
                     for t in range(4):
-                        mx_lone(banks[("a", r)][:, t, :], w1q["a"], w1s["a"], slice(P * t, P * t + P), hq, hs, hcols)
+                        mx_lone(
+                            banks[("a", r)][:, t, :], w1q["a"], w1s["a"], slice(512 * c + P * t, 512 * c + P * t + P),
+                            hq, hs, hcols,
+                        )
                 else:
                     mx_lone(
                         banks[("a", r)][:].rearrange("p t f -> p (t f)"), hq, hs, hcols,
@@ -212,9 +218,9 @@ def tile_simplegnn_pa_t_kernel(tc, h, adj_mask, w1a, w1b, b1, w2, b2, gamma, bet
         def first_layer_out_t(c, banks):
             for r in T_CHUNKS:
                 nc.scalar.copy(out=xb[r][:, c, :, :], in_=banks[("b", r)][:])
-                if c == 0:
+                if (r, c) in V_SLOTS:
                     nc.vector.tensor_tensor(
-                        out=at_sb[:, P * r - N_A : P * r - N_A + P, :],
+                        out=at_sb[(r, c)][:],
                         in0=banks[("a", r)][:].rearrange("p t r -> p r t"),
                         in1=b1f[:, c, :].unsqueeze(1).to_broadcast([P, P, 4]),
                         op=ALU.add,
@@ -323,48 +329,49 @@ def tile_simplegnn_pa_t_kernel(tc, h, adj_mask, w1a, w1b, b1, w2, b2, gamma, bet
 
         def sums_on_tensor(k, banks):
             tu = t_seq[k]
-            for x, r in enumerate(T_CHUNKS):
-                banks[(1, r)] = pre_pool.tile([P, 4, P], F32, tag="pre", name="pre1%d" % r)
+            for r, c in T_SLOTS:
+                x = T_CHUNKS.index(r)
+                banks[(c, r)] = pre_pool.tile([P, 4, P], F32, tag="pre", name="pre%d%d" % (c, r))
                 for t in range(4):
                     if tu == "za":
-                        nc.tensor.transpose(banks[(1, r)][:, t, :], xa[r][:, 1, t, :], ident[:])
+                        nc.tensor.transpose(banks[(c, r)][:, t, :], xa[r][:, c, t, :], ident[:])
                     else:
                         nc.tensor.matmul(
-                            out=banks[(1, r)][:, t, :], lhsT=xb[r][:, 1, t, :], rhs=protm[:, x, tu, :],
+                            out=banks[(c, r)][:, t, :], lhsT=xb[r][:, c, t, :], rhs=protm[:, x, tu, :],
                             is_transpose=True, start=True, stop=False,
                         )
                         nc.tensor.matmul(
-                            out=banks[(1, r)][:, t, :], lhsT=xa[r][:, 1, t, :], rhs=ident[:],
+                            out=banks[(c, r)][:, t, :], lhsT=xa[r][:, c, t, :], rhs=ident[:],
                             is_transpose=True, start=False, stop=True,
                         )
             if tu != "za":
-                for x, r in enumerate(T_CHUNKS):
-                    banks[(0, r)] = pre_pool.tile([P, 4, P], F32, tag="pre", name="pre0%d" % r)
+                for r, c in V_SLOTS:
+                    x = T_CHUNKS.index(r)
+                    banks[(c, r)] = pre_pool.tile([P, 4, P], F32, tag="pre", name="pre%d%d" % (c, r))
                     for t in range(4):
-                        nc.tensor.transpose(banks[(0, r)][:, t, :], xb[r][:, 0, t, :], protm[:, x, tu, :])
+                        nc.tensor.transpose(banks[(c, r)][:, t, :], xb[r][:, c, t, :], protm[:, x, tu, :])
 
         def relu_from_psum(k, banks):
-            for r in T_CHUNKS:
+            for r, c in T_SLOTS:
                 nc.scalar.activation(
-                    out=z[(k, 1)][:, 4 * P * r : 4 * P * (r + 1)].rearrange("p (r t) -> p r t", t=4),
-                    in_=banks[(1, r)][:].rearrange("p t r -> p r t"),
+                    out=z[(k, c)][:, 4 * P * r : 4 * P * (r + 1)].rearrange("p (r t) -> p r t", t=4),
+                    in_=banks[(c, r)][:].rearrange("p t r -> p r t"),
                     func=ACT.Relu,
                 )
 
         def sums_from_psum(k, banks):
-            if t_seq[k] == "za":
-                nc.scalar.activation(
-                    out=z[(k, 0)][:, 4 * N_A : 4 * ROWS], in_=at_sb[:].rearrange("p r t -> p (r t)"), func=ACT.Relu
-                )
-                return
-            for r in T_CHUNKS:
-                nc.vector.tensor_tensor(
-                    out=z[(k, 0)][:, 4 * P * r : 4 * P * (r + 1)].rearrange("p (r t) -> p r t", t=4),
-                    in0=banks[(0, r)][:].rearrange("p t r -> p r t"),
-                    in1=at_sb[:, P * r - N_A : P * r - N_A + P, :],
-                    op=ALU.add,
-                )
-            nc.scalar.activation(out=z[(k, 0)][:, 4 * N_A : 4 * ROWS], in_=z[(k, 0)][:, 4 * N_A : 4 * ROWS], func=ACT.Relu)
+            for r, c in V_SLOTS:
+                part = z[(k, c)][:, 4 * P * r : 4 * P * (r + 1)]
+                if t_seq[k] == "za":
+                    nc.scalar.activation(out=part, in_=at_sb[(r, c)][:].rearrange("p r t -> p (r t)"), func=ACT.Relu)
+                else:
+                    nc.vector.tensor_tensor(
+                        out=part.rearrange("p (r t) -> p r t", t=4),
+                        in0=banks[(c, r)][:].rearrange("p t r -> p r t"),
+                        in1=at_sb[(r, c)][:],
+                        op=ALU.add,
+                    )
+                    nc.scalar.activation(out=part, in_=part, func=ACT.Relu)
 
         def sums_on_vector(k, c):
             nc.vector.tensor_tensor(

@@ -53,12 +53,13 @@ def tile_simplegnn_pa_t_kernel(tc, h, adj_mask, w1a, w1b, b1, w2, b2, gamma, bet
         nc.sync.dma_start(out=h_sb[:], in_=h_flat.rearrange("(r p) d -> p r d", p=P))
         raw1 = {}
         for o in ("a", "b"):
-            raw1[o] = const.tile([P, 4, F], BF16, name="raw1" + o)
+            for c in range(2):
+                raw1[(o, c)] = const.tile([P, 4, 512], BF16, name="raw1%s%d" % (o, c))
 
         def load_w1(o, c):
             for u in range(2):
                 nc.sync.dma_start(
-                    out=raw1[o][:, 2 * u : 2 * u + 2, 512 * c : 512 * c + 512],
+                    out=raw1[(o, c)][:, 2 * u : 2 * u + 2, :],
                     in_=w1[o][256 * u : 256 * u + 256, 512 * c : 512 * c + 512].rearrange("(q e) f -> q e f", e=2),
                 )
 
@@ -152,7 +153,7 @@ def tile_simplegnn_pa_t_kernel(tc, h, adj_mask, w1a, w1b, b1, w2, b2, gamma, bet
 
         def regroup_w1(o, c, eng):
             dst = g1[(o, c)][:].rearrange("q (t p k) -> q p k t", t=4, p=P, k=4)
-            src = raw1[o][:, :, 512 * c : 512 * c + 512].rearrange("q k (p t) -> q p k t", t=4)
+            src = raw1[(o, c)][:].rearrange("q k (p t) -> q p k t", t=4)
             if eng == "v":
                 nc.vector.tensor_copy(out=dst, in_=src)
             else:
@@ -265,9 +266,7 @@ def tile_simplegnn_pa_t_kernel(tc, h, adj_mask, w1a, w1b, b1, w2, b2, gamma, bet
             if eng == "v":
                 nc.vector.tensor_scalar_mul(out=dst, in0=src, scalar1=mt[:, x, u : u + 1])
             else:
-                nc.gpsimd.tensor_scalar(
-                    out=dst, in0=src, scalar1=mt[:, x, u : u + 1], scalar2=0.0, op0=ALU.mult, op1=ALU.add
-                )
+                nc.scalar.activation(out=dst, in_=src, func=ACT.Copy, scale=mt[:, x, u : u + 1])
 
         for u in range(2):
             for x in range(2):
@@ -299,21 +298,15 @@ def tile_simplegnn_pa_t_kernel(tc, h, adj_mask, w1a, w1b, b1, w2, b2, gamma, bet
         w2q = const.tile([P, 2, D], U32, align_bytes=64)
         w2s = const.tile([P, 2, D], U8, align_bytes=64)
 
-        for u in range(2, 4):
-            for x in range(2):
-                mask_rotation(x, u, "g")
         g2 = {}
         for c in range(2):
             g2[c] = const.tile([P, 2048], BF16, name="g2%d" % c, align_bytes=64)
-            nc.gpsimd.tensor_scalar(
-                out=g2[c][:].rearrange("p (m i t) -> p m t i", i=4, t=4),
-                in0=raw2[:, c, :, :].rearrange("p t (m i) -> p m t i", i=4),
-                scalar1=1.0, scalar2=0.0, op0=ALU.mult, op1=ALU.add,
-            )
-
-        for u in range(4, NODES):
-            for x in range(2):
-                mask_rotation(x, u, "g")
+            dst = g2[c][:].rearrange("p (m i t) -> p m t i", i=4, t=4)
+            src = raw2[:, c, :, :].rearrange("p t (m i) -> p m t i", i=4)
+            if c == 0:
+                nc.vector.tensor_copy(out=dst, in_=src)
+            else:
+                nc.scalar.copy(out=dst, in_=src)
 
         a_seq = list(range(NODES)) + [None]
         t_seq = ["za"] + list(range(NODES))
@@ -514,6 +507,9 @@ def tile_simplegnn_pa_t_kernel(tc, h, adj_mask, w1a, w1b, b1, w2, b2, gamma, bet
                 if t_seq[k] == "za":
                     for r in T_CHUNKS:
                         add_scaled(r, ms[r][:], degm1[:, r : r + 1])
+                if k + 2 < NODES:
+                    for x in range(2):
+                        mask_rotation(x, k + 2, "s")
 
         for r in A_CHUNKS:
             ln_stats(r)

@@ -23,8 +23,7 @@ FLOPS = 2 * ROWS * D * F * 2 + 2 * ROWS * NODES * F * D
 A_CHUNKS = (0, 1)
 T_CHUNKS = (2, 3)
 N_A = 256
-V_SLOTS = ((2, 0),)
-T_SLOTS = ((2, 1), (3, 1), (3, 0))
+LEAD = 2
 
 
 def tile_simplegnn_pa_t_kernel(tc, h, adj_mask, w1a, w1b, b1, w2, b2, gamma, beta, out):
@@ -36,19 +35,17 @@ def tile_simplegnn_pa_t_kernel(tc, h, adj_mask, w1a, w1b, b1, w2, b2, gamma, bet
 
     with ExitStack() as ctx:
         const = ctx.enter_context(tc.tile_pool(name="const", bufs=1))
-        stage = ctx.enter_context(tc.tile_pool(name="stage", bufs=2))
-        zpool = ctx.enter_context(tc.tile_pool(name="zpool", bufs=4))
+        zpool = ctx.enter_context(tc.tile_pool(name="zpool", bufs=8))
         small = ctx.enter_context(tc.tile_pool(name="small", bufs=4))
-        pre_pool = ctx.enter_context(tc.psum_pool(name="pre", bufs=4))
-        m_pool = ctx.enter_context(tc.psum_pool(name="m", bufs=2))
+        w_pool = ctx.enter_context(tc.psum_pool(name="w", bufs=6))
         g_pool = ctx.enter_context(tc.psum_pool(name="g", bufs=2))
         ctx.enter_context(tc.manual_schedule())
+        ctx.enter_context(nc.allow_low_precision(reason="zeros and ones: sums with at most one one are exact in bfloat16"))
 
         mask_sb = const.tile([P, CHUNKS, NODES], BF16)
         b1_sb = const.tile([P, 2, 4], BF16)
         with nc.allow_non_contiguous_dma(reason="small bias and mask tables"):
             nc.sync.dma_start(out=mask_sb[:], in_=adj_flat.rearrange("(r p) j -> p r j", p=P))
-            nc.sync.dma_start(out=b1_sb[:], in_=b1.rearrange("(c p t) -> p c t", c=2, p=P, t=4))
         h_sb = const.tile([P, CHUNKS, D], BF16)
         nc.sync.dma_start(out=h_sb[:], in_=h_flat.rearrange("(r p) d -> p r d", p=P))
         raw1 = {}
@@ -67,12 +64,16 @@ def tile_simplegnn_pa_t_kernel(tc, h, adj_mask, w1a, w1b, b1, w2, b2, gamma, bet
         load_w1("b", 0)
         b1_bc = const.tile([P, F], BF16)
         nc.sync.dma_start(out=b1_bc[:], in_=b1.partition_broadcast(P))
-        b2_bc = const.tile([P, D], BF16)
-        nc.sync.dma_start(out=b2_bc[:], in_=b2.partition_broadcast(P))
         load_w1("a", 1)
         load_w1("b", 1)
-        raw2 = const.tile([P, 2, 4, D], BF16)
-        nc.sync.dma_start(out=raw2[:], in_=w2.rearrange("(c p t) n -> p c t n", c=2, p=P, t=4))
+        with nc.allow_non_contiguous_dma(reason="small bias table"):
+            nc.sync.dma_start(out=b1_sb[:], in_=b1.rearrange("(c p t) -> p c t", c=2, p=P, t=4))
+        raw2 = {}
+        for c in range(2):
+            raw2[c] = const.tile([P, 4, D], BF16, name="raw2%d" % c)
+            nc.sync.dma_start(out=raw2[c][:], in_=w2[512 * c : 512 * c + 512, :].rearrange("(p t) n -> p t n", t=4))
+        b2_bc = const.tile([P, D], BF16)
+        nc.sync.dma_start(out=b2_bc[:], in_=b2.partition_broadcast(P))
         gamma_bc = const.tile([P, D], BF16)
         beta_bc = const.tile([P, D], BF16)
         nc.sync.dma_start(out=gamma_bc[:], in_=gamma.partition_broadcast(P))
@@ -88,43 +89,40 @@ def tile_simplegnn_pa_t_kernel(tc, h, adj_mask, w1a, w1b, b1, w2, b2, gamma, bet
         ident_v = ident[:].rearrange("p (g i) -> p g i", i=NODES)
         nc.vector.tensor_copy(out=ident_d[:, :, 0:NODES], in_=ident_v)
         nc.vector.tensor_copy(out=ident_d[:, :, NODES : 2 * NODES], in_=ident_v)
-        i16d = const.tile([P, 2 * NODES], F32)
+        i16d = const.tile([P, 2 * NODES], BF16)
         nc.vector.tensor_reduce(
             out=i16d[:, 0:NODES], in_=ident[:].rearrange("p (g i) -> p i g", i=NODES), axis=AX.X, op=ALU.add
         )
         nc.vector.tensor_copy(out=i16d[:, NODES : 2 * NODES], in_=i16d[:, 0:NODES])
-        sel2 = const.tile([P, NODES, NODES], F32)
+        sel2 = const.tile([P, NODES, NODES], BF16)
         for u in range(NODES):
             nc.vector.tensor_copy(out=sel2[:, u, :], in_=i16d[:, u : u + NODES])
         bd8 = const.tile([P, 8], F32)
         nc.vector.tensor_reduce(out=bd8[:], in_=ident_v, axis=AX.X, op=ALU.add)
-        maskf = const.tile([P, CHUNKS, NODES], F32)
-        nc.vector.tensor_copy(out=maskf[:], in_=mask_sb[:])
-        mask16 = const.tile([P, CHUNKS, NODES], F32)
-        nc.vector.tensor_scalar_mul(out=mask16[:], in0=mask_sb[:], scalar1=1.0 / NODES)
-        deg16 = const.tile([P, CHUNKS], F32)
-        nc.vector.tensor_reduce(out=deg16[:], in_=mask16[:], axis=AX.X, op=ALU.add)
-        degm1 = const.tile([P, CHUNKS], F32)
-        nc.vector.tensor_scalar_add(out=degm1[:], in0=deg16[:], scalar1=-1.0)
-        b1f = const.tile([P, 2, 4], F32)
-        nc.vector.tensor_copy(out=b1f[:], in_=b1_sb[:])
         blk = const.tile([P, 2, 8, NODES], F32)
-        ps_e = pre_pool.tile([P, 2, P], F32, tag="pre")
-        adj_t = const.tile([P, 2, NODES], F32)
-        mt = const.tile([P, 2, NODES], F32)
+        ps_e = w_pool.tile([P, 2, P], F32, tag="w")
         for x, r in enumerate(T_CHUNKS):
             nc.vector.tensor_tensor(
                 out=blk[:, x, :, :],
                 in0=bd8[:].unsqueeze(2).to_broadcast([P, 8, NODES]),
-                in1=maskf[:, r, :].unsqueeze(1).to_broadcast([P, 8, NODES]),
+                in1=mask_sb[:, r, :].unsqueeze(1).to_broadcast([P, 8, NODES]),
                 op=ALU.mult,
             )
             nc.tensor.transpose(ps_e[:, x, :], blk[:, x, :, :].rearrange("p g j -> p (g j)"), ident[:])
 
+        def rotate_rows(dst, src):
+            prod = small.tile([P, 2, NODES, NODES], BF16, tag="prod")
+            for x in range(2):
+                nc.vector.tensor_tensor(
+                    out=prod[:, x, :, :], in0=sel2[:], in1=src[:, x, :].unsqueeze(1).to_broadcast([P, NODES, NODES]), op=ALU.mult
+                )
+            nc.vector.tensor_reduce(out=dst, in_=prod[:], axis=AX.X, op=ALU.add)
+
+
         gh = const.tile([P, 4 * ROWS], BF16, align_bytes=64)
         ghw = gh[:].bitcast(F32).rearrange("p (r u) -> p r u", u=2)
         for half in range(2):
-            ps_h = pre_pool.tile([P, 2, 2, P], F32, tag="pre")
+            ps_h = w_pool.tile([P, 2, 2, P], F32, tag="w")
             for l in range(2):
                 r = 2 * half + l
                 for u in range(2):
@@ -133,14 +131,26 @@ def tile_simplegnn_pa_t_kernel(tc, h, adj_mask, w1a, w1b, b1, w2, b2, gamma, bet
                     )
             for l in range(2):
                 r = 2 * half + l
-                dst = ghw[:, r * P : (r + 1) * P, :]
-                src = ps_h[:, l, :, :].rearrange("p u r -> p r u")
-                if half == 0:
-                    nc.vector.tensor_copy(out=dst, in_=src)
-                else:
-                    nc.scalar.copy(out=dst, in_=src)
+                nc.scalar.copy(out=ghw[:, r * P : (r + 1) * P, :], in_=ps_h[:, l, :, :].rearrange("p u r -> p r u"))
         hq = const.tile([P, ROWS], U32, align_bytes=64)
         hs = const.tile([P, ROWS], U8, align_bytes=64)
+
+        adj_t = const.tile([P, 2, NODES], BF16)
+        nc.vector.tensor_reduce(
+            out=adj_t[:], in_=ps_e[:].rearrange("p x (g i) -> p x i g", i=NODES), axis=AX.X, op=ALU.add
+        )
+        mt = const.tile([P, 2, NODES], F32)
+        rotate_rows(mt[:], adj_t[:])
+
+        move = const.tile([P, 2, NODES, P], F32)
+
+        def move_neighbours(u, eng):
+            for x in range(2):
+                dst = move[:, x, u, :].rearrange("p (g i) -> p g i", i=NODES)
+                if eng == "v":
+                    nc.vector.tensor_scalar_mul(out=dst, in0=ident_d[:, :, u : u + NODES], scalar1=mt[:, x, u : u + 1])
+                else:
+                    nc.scalar.activation(out=dst, in_=ident_d[:, :, u : u + NODES], func=ACT.Copy, scale=mt[:, x, u : u + 1])
 
         w1q = {}
         w1s = {}
@@ -151,9 +161,9 @@ def tile_simplegnn_pa_t_kernel(tc, h, adj_mask, w1a, w1b, b1, w2, b2, gamma, bet
             for c in range(2):
                 g1[(o, c)] = const.tile([P, 2048], BF16, name="g1%s%d" % (o, c), align_bytes=64)
 
-        def regroup_w1(o, c, eng):
-            dst = g1[(o, c)][:].rearrange("q (t p k) -> q p k t", t=4, p=P, k=4)
-            src = raw1[(o, c)][:].rearrange("q k (p t) -> q p k t", t=4)
+        def regroup_w1(o, c, eng, lo=0, hi=4):
+            dst = g1[(o, c)][:].rearrange("q (t p k) -> q t p k", t=4, p=P, k=4)[:, lo:hi, :, :].rearrange("q t p k -> q p k t")
+            src = raw1[(o, c)][:].rearrange("q k (p t) -> q p k t", t=4)[:, :, :, lo:hi]
             if eng == "v":
                 nc.vector.tensor_copy(out=dst, in_=src)
             else:
@@ -165,9 +175,6 @@ def tile_simplegnn_pa_t_kernel(tc, h, adj_mask, w1a, w1b, b1, w2, b2, gamma, bet
 
         a_sb = const.tile([P, 2, N_A, 4], F32)
         b_sb = const.tile([P, 2, N_A, 4], F32)
-        at_sb = {}
-        for r, c in V_SLOTS:
-            at_sb[(r, c)] = const.tile([P, P, 4], F32, name="at%d%d" % (r, c))
         xa = {}
         xb = {}
         for r in T_CHUNKS:
@@ -185,210 +192,152 @@ def tile_simplegnn_pa_t_kernel(tc, h, adj_mask, w1a, w1b, b1, w2, b2, gamma, bet
                 stop=True,
             )
 
-        def first_layer_t(c, banks):
+        banks = {}
+
+        def first_layer_t(o, c):
+            pool, tag = (w_pool, "w") if o == "a" else (g_pool, "g")
             for r in T_CHUNKS:
-                hcols = slice(P * r, P * r + P)
-                banks[("a", r)] = m_pool.tile([P, 4, P], F32, tag="m", name="fxa%d" % r)
-                banks[("b", r)] = g_pool.tile([P, 4, P], F32, tag="g", name="fxb%d" % r)
-                if (r, c) in V_SLOTS:
-                    for t in range(4):
-                        mx_lone(
-                            banks[("a", r)][:, t, :], w1q["a"], w1s["a"], slice(512 * c + P * t, 512 * c + P * t + P),
-                            hq, hs, hcols,
-                        )
-                else:
-                    mx_lone(
-                        banks[("a", r)][:].rearrange("p t f -> p (t f)"), hq, hs, hcols,
-                        w1q["a"], w1s["a"], slice(512 * c, 512 * c + 512),
-                    )
+                banks[(o, r, c)] = pool.tile([P, 4, P], F32, tag=tag, name="fx%s%d%d" % (o, r, c))
                 mx_lone(
-                    banks[("b", r)][:].rearrange("p t f -> p (t f)"), hq, hs, hcols,
-                    w1q["b"], w1s["b"], slice(512 * c, 512 * c + 512),
+                    banks[(o, r, c)][:].rearrange("p t f -> p (t f)"), hq, hs, slice(P * r, P * r + P),
+                    w1q[o], w1s[o], slice(512 * c, 512 * c + 512),
                 )
 
-        def first_layer_a(c, banks):
-            for r in A_CHUNKS:
-                for o in ("a", "b"):
-                    banks[(o, r)] = pre_pool.tile([P, 4, P], F32, tag="pre", name="fl%s%d" % (o, r))
-                    for t in range(4):
-                        mx_lone(
-                            banks[(o, r)][:, t, :], w1q[o], w1s[o], slice(512 * c + P * t, 512 * c + P * t + P),
-                            hq, hs, slice(P * r, P * r + P),
-                        )
-
-        def first_layer_out_t(c, banks):
+        def first_layer_out_t(o, c):
             for r in T_CHUNKS:
-                nc.scalar.copy(out=xb[r][:, c, :, :], in_=banks[("b", r)][:])
-                if (r, c) in V_SLOTS:
-                    nc.vector.tensor_tensor(
-                        out=at_sb[(r, c)][:],
-                        in0=banks[("a", r)][:].rearrange("p t r -> p r t"),
-                        in1=b1f[:, c, :].unsqueeze(1).to_broadcast([P, P, 4]),
-                        op=ALU.add,
-                    )
+                if o == "b":
+                    nc.scalar.copy(out=xb[r][:, c, :, :], in_=banks[(o, r, c)][:])
                 else:
                     nc.vector.tensor_tensor(
                         out=xa[r][:, c, :, :],
-                        in0=banks[("a", r)][:],
+                        in0=banks[(o, r, c)][:],
                         in1=b1_bc[:, 512 * c : 512 * c + 512].rearrange("q (p t) -> q t p", t=4),
                         op=ALU.add,
                     )
 
-        def first_layer_out_a(c, banks):
+        def first_layer_a(c):
+            for r in A_CHUNKS:
+                for o, pool, tag in (("a", w_pool, "w"), ("b", w_pool, "w")):
+                    banks[(o, r, c)] = pool.tile([P, 4, P], F32, tag=tag, name="fl%s%d%d" % (o, r, c))
+                    for t in range(4):
+                        mx_lone(
+                            banks[(o, r, c)][:, t, :], w1q[o], w1s[o], slice(512 * c + P * t, 512 * c + P * t + P),
+                            hq, hs, slice(P * r, P * r + P),
+                        )
+
+        def first_layer_out_a(c):
             for r in A_CHUNKS:
                 rows = slice(P * r, P * r + P)
-                nc.scalar.copy(out=a_sb[:, c, rows, :], in_=banks[("a", r)][:].rearrange("p t r -> p r t"))
+                nc.scalar.copy(out=a_sb[:, c, rows, :], in_=banks[("a", r, c)][:].rearrange("p t r -> p r t"))
                 nc.vector.tensor_tensor(
                     out=b_sb[:, c, rows, :],
-                    in0=banks[("b", r)][:].rearrange("p t r -> p r t"),
+                    in0=banks[("b", r, c)][:].rearrange("p t r -> p r t"),
                     in1=b1f[:, c, :].unsqueeze(1).to_broadcast([P, P, 4]),
                     op=ALU.add,
                 )
 
-        regroup_w1("a", 0, "v")
-        regroup_w1("b", 0, "s")
-        nc.vector.quantize_mx(out=hq[:].bitcast(FP8X4), scales=hs[:], in_=gh[:])
-        quantise_w1("a", 0)
-        for x, r in enumerate(T_CHUNKS):
-            nc.vector.tensor_reduce(
-                out=adj_t[:, x, :], in_=ps_e[:, x, :].rearrange("p (g i) -> p i g", i=NODES), axis=AX.X, op=ALU.add
-            )
-            prod = small.tile([P, NODES, NODES], F32, tag="prod")
-            nc.vector.tensor_tensor(
-                out=prod[:], in0=sel2[:], in1=adj_t[:, x, :].unsqueeze(1).to_broadcast([P, NODES, NODES]), op=ALU.mult
-            )
-            nc.vector.tensor_reduce(out=mt[:, x, :], in_=prod[:], axis=AX.X, op=ALU.add)
-        protm = const.tile([P, 2, NODES, P], F32)
-
-        def mask_rotation(x, u, eng):
-            dst = protm[:, x, u, :].rearrange("p (g i) -> p g i", i=NODES)
-            src = ident_d[:, :, u : u + NODES]
-            if eng == "v":
-                nc.vector.tensor_scalar_mul(out=dst, in0=src, scalar1=mt[:, x, u : u + 1])
-            else:
-                nc.scalar.activation(out=dst, in_=src, func=ACT.Copy, scale=mt[:, x, u : u + 1])
-
-        for u in range(2):
-            for x in range(2):
-                mask_rotation(x, u, "v")
-        quantise_w1("b", 0)
-        banks0 = {}
-        first_layer_t(0, banks0)
-        first_layer_a(0, banks0)
-        regroup_w1("a", 1, "v")
-        regroup_w1("b", 1, "s")
-        quantise_w1("a", 1)
-        first_layer_out_t(0, banks0)
-        quantise_w1("b", 1)
-        banks1 = {}
-        first_layer_t(1, banks1)
-        first_layer_out_a(0, banks0)
-        first_layer_a(1, banks1)
-        first_layer_out_t(1, banks1)
-        first_layer_out_a(1, banks1)
-        acc = const.tile([P, CHUNKS, D], F32)
-
-        def start_acc():
-            for r in range(CHUNKS):
-                nc.vector.scalar_tensor_tensor(
-                    out=acc[:, r, :], in0=b2_bc[:], scalar=deg16[:, r : r + 1], in1=h_sb[:, r, :],
-                    op0=ALU.mult, op1=ALU.add,
-                )
-
         w2q = const.tile([P, 2, D], U32, align_bytes=64)
         w2s = const.tile([P, 2, D], U8, align_bytes=64)
-
         g2 = {}
         for c in range(2):
             g2[c] = const.tile([P, 2048], BF16, name="g2%d" % c, align_bytes=64)
-            dst = g2[c][:].rearrange("p (m i t) -> p m t i", i=4, t=4)
-            src = raw2[:, c, :, :].rearrange("p t (m i) -> p m t i", i=4)
-            if c == 0:
-                nc.vector.tensor_copy(out=dst, in_=src)
-            else:
-                nc.scalar.copy(out=dst, in_=src)
 
-        a_seq = list(range(NODES)) + [None]
-        t_seq = ["za"] + list(range(NODES))
-        rounds = len(t_seq)
+        def regroup_w2(c, eng):
+            dst = g2[c][:].rearrange("p (m i t) -> p m t i", i=4, t=4)
+            srcv = raw2[c][:].rearrange("p t (m i) -> p m t i", i=4)
+            if eng == "v":
+                nc.vector.tensor_copy(out=dst, in_=srcv)
+            elif eng == "s":
+                nc.scalar.copy(out=dst, in_=srcv)
+            else:
+                nc.gpsimd.tensor_scalar(out=dst, in0=srcv, scalar1=1.0, scalar2=0.0, op0=ALU.mult, op1=ALU.add)
+
+        def quantise_w2(c):
+            nc.vector.quantize_mx(out=w2q[:, c, :].bitcast(FP8X4), scales=w2s[:, c, :], in_=g2[c][:])
+
+        acc = const.tile([P, CHUNKS, D], F32)
+        mask16 = const.tile([P, CHUNKS, NODES], F32)
+        deg16 = const.tile([P, CHUNKS], F32)
+        degm1 = const.tile([P, CHUNKS], F32)
+
+        def mask_scalars():
+            nc.vector.tensor_scalar_mul(out=mask16[:], in0=mask_sb[:], scalar1=1.0 / NODES)
+            nc.vector.tensor_reduce(out=deg16[:], in_=mask16[:], axis=AX.X, op=ALU.add)
+            nc.vector.tensor_scalar_add(out=degm1[:], in0=deg16[:], scalar1=-1.0)
+
+        rounds = NODES + max(1, LEAD)
         z = {}
         zq = {}
         zs = {}
         g_t = {}
+        self_t = {}
+        T_SLOTS = ((2, 0), (3, 0), (2, 1), (3, 1))
 
-        def new_z(k):
-            for c in range(2):
-                z[(k, c)] = zpool.tile([P, 4 * ROWS], BF16, tag="z", name="z%d" % c, align_bytes=64)
+        def t_unit(k):
+            return k - 1 if k <= NODES else None
 
-        def sums_on_tensor(k, banks):
-            tu = t_seq[k]
-            for r, c in T_SLOTS:
-                x = T_CHUNKS.index(r)
-                banks[(c, r)] = pre_pool.tile([P, 4, P], F32, tag="pre", name="pre%d%d" % (c, r))
+        def a_unit(k):
+            return k - LEAD if k >= LEAD else None
+
+        def new_z(k, c):
+            z[(k, c)] = zpool.tile([P, 4 * ROWS], BF16, tag="z", name="z%d" % c, align_bytes=64)
+
+        pre = {}
+
+        def sums_on_tensor(k, c):
+            tu = t_unit(k)
+            if tu is None:
+                return
+            for x, r in enumerate(T_CHUNKS):
+                pre[(c, r)] = w_pool.tile([P, 4, P], F32, tag="w", name="pre%d%d" % (c, r))
                 for t in range(4):
-                    if tu == "za":
-                        nc.tensor.transpose(banks[(c, r)][:, t, :], xa[r][:, c, t, :], ident[:])
-                    else:
-                        nc.tensor.matmul(
-                            out=banks[(c, r)][:, t, :], lhsT=xb[r][:, c, t, :], rhs=protm[:, x, tu, :],
-                            is_transpose=True, start=True, stop=False,
-                        )
-                        nc.tensor.matmul(
-                            out=banks[(c, r)][:, t, :], lhsT=xa[r][:, c, t, :], rhs=ident[:],
-                            is_transpose=True, start=False, stop=True,
-                        )
-            if tu != "za":
-                for r, c in V_SLOTS:
-                    x = T_CHUNKS.index(r)
-                    banks[(c, r)] = pre_pool.tile([P, 4, P], F32, tag="pre", name="pre%d%d" % (c, r))
-                    for t in range(4):
-                        nc.tensor.transpose(banks[(c, r)][:, t, :], xb[r][:, c, t, :], protm[:, x, tu, :])
+                    if tu < 0:
+                        nc.tensor.transpose(pre[(c, r)][:, t, :], xa[r][:, c, t, :], ident[:])
+                        continue
+                    nc.tensor.matmul(
+                        out=pre[(c, r)][:, t, :], lhsT=xb[r][:, c, t, :], rhs=move[:, x, tu, :],
+                        is_transpose=True, start=True, stop=False,
+                    )
+                    nc.tensor.matmul(
+                        out=pre[(c, r)][:, t, :], lhsT=xa[r][:, c, t, :], rhs=ident[:],
+                        is_transpose=True, start=False, stop=True,
+                    )
 
-        def relu_from_psum(k, banks):
-            for r, c in T_SLOTS:
+        def relu_from_psum(k, c):
+            if t_unit(k) is None:
+                return
+            for r in T_CHUNKS:
                 nc.scalar.activation(
                     out=z[(k, c)][:, 4 * P * r : 4 * P * (r + 1)].rearrange("p (r t) -> p r t", t=4),
-                    in_=banks[(c, r)][:].rearrange("p t r -> p r t"),
+                    in_=pre[(c, r)][:].rearrange("p t r -> p r t"),
                     func=ACT.Relu,
                 )
 
-        def sums_from_psum(k, banks):
-            for r, c in V_SLOTS:
-                part = z[(k, c)][:, 4 * P * r : 4 * P * (r + 1)]
-                if t_seq[k] == "za":
-                    nc.scalar.activation(out=part, in_=at_sb[(r, c)][:].rearrange("p r t -> p (r t)"), func=ACT.Relu)
-                else:
-                    nc.vector.tensor_tensor(
-                        out=part.rearrange("p (r t) -> p r t", t=4),
-                        in0=banks[(c, r)][:].rearrange("p t r -> p r t"),
-                        in1=at_sb[(r, c)][:],
-                        op=ALU.add,
-                    )
-                    nc.scalar.activation(out=part, in_=part, func=ACT.Relu)
-
         def sums_on_vector(k, c):
+            au = a_unit(k)
+            if au is None:
+                return
             nc.vector.tensor_tensor(
                 out=z[(k, c)][:, 0 : 4 * N_A].rearrange("p (g i t) -> p g i t", i=NODES, t=4),
                 in0=a_sb[:, c, :, :].rearrange("p (g i) t -> p g i t", i=NODES),
                 in1=b_sb[:, c, :, :]
-                .rearrange("p (g j) t -> p g j t", j=NODES)[:, :, a_seq[k], :]
+                .rearrange("p (g j) t -> p g j t", j=NODES)[:, :, au, :]
                 .unsqueeze(2)
                 .to_broadcast([P, N_A // NODES, NODES, 4]),
                 op=ALU.add,
             )
 
-        def relu_in_place(k, c, eng):
-            if eng == "s":
+        def relu_in_place(k, c):
+            if a_unit(k) is not None:
                 nc.scalar.activation(out=z[(k, c)][:, 0 : 4 * N_A], in_=z[(k, c)][:, 0 : 4 * N_A], func=ACT.Relu)
-            else:
-                nc.vector.tensor_scalar_max(out=z[(k, c)][:, 0 : 4 * N_A], in0=z[(k, c)][:, 0 : 4 * N_A], scalar1=0.0)
 
         def quantise_z(k, c):
             zq[(k, c)] = zpool.tile([P, ROWS], U32, tag="zq", name="zq%d" % c, align_bytes=64)
             zs[(k, c)] = zpool.tile([P, ROWS], U8, tag="zs", name="zs%d" % c, align_bytes=64)
-            lo = N_A if a_seq[k] is None else 0
+            lo = N_A if a_unit(k) is None else 0
+            hi = N_A if t_unit(k) is None else ROWS
             nc.vector.quantize_mx(
-                out=zq[(k, c)][:, lo:ROWS].bitcast(FP8X4), scales=zs[(k, c)][:, lo:ROWS], in_=z[(k, c)][:, 4 * lo : 4 * ROWS]
+                out=zq[(k, c)][:, lo:hi].bitcast(FP8X4), scales=zs[(k, c)][:, lo:hi], in_=z[(k, c)][:, 4 * lo : 4 * hi]
             )
 
         def mx_pass(dst, k, c, r, start, stop):
@@ -403,120 +352,162 @@ def tile_simplegnn_pa_t_kernel(tc, h, adj_mask, w1a, w1b, b1, w2, b2, gamma, bet
                 stop=stop,
             )
 
-        def second_layer_a(k, ms):
+        ms = {}
+
+        def second_layer_a(k):
+            if a_unit(k) is None:
+                return
             for r in A_CHUNKS:
-                ms[r] = m_pool.tile([P, D], F32, tag="m", name="m%d" % r)
+                ms[(k, r)] = w_pool.tile([P, D], F32, tag="w", name="m%d" % r)
                 for c in range(2):
-                    mx_pass(ms[r][:], k, c, r, c == 0, c == 1)
+                    mx_pass(ms[(k, r)][:], k, c, r, c == 0, c == 1)
 
-        def second_layer_t(k, ms):
-            tu = t_seq[k]
+        def second_layer_t(k):
+            tu = t_unit(k)
+            if tu is None:
+                return
             for r in T_CHUNKS:
-                if tu == "za":
-                    ms[r] = g_pool.tile([P, D], F32, tag="g", name="mz%d" % r)
+                if tu < 0:
+                    self_t[r] = w_pool.tile([P, D], F32, tag="w", name="self%d" % r)
                     for c in range(2):
-                        mx_pass(ms[r][:], k, c, r, c == 0, c == 1)
-                else:
-                    if tu == 0:
-                        g_t[r] = g_pool.tile([P, D], F32, tag="g", name="gt%d" % r)
-                    for c in range(2):
-                        mx_pass(g_t[r][:], k, c, r, tu == 0 and c == 0, tu == NODES - 1 and c == 1)
+                        mx_pass(self_t[r][:], k, c, r, c == 0, c == 1)
+                    continue
+                if tu == 0:
+                    g_t[r] = g_pool.tile([P, D], F32, tag="g", name="gt%d" % r)
+                for c in range(2):
+                    mx_pass(g_t[r][:], k, c, r, tu == 0 and c == 0, tu == NODES - 1 and c == 1)
 
-        def add_scaled(r, src, factor):
+        sums = {}
+
+        def add_scaled(r, src, factor, first, last):
+            kw = {}
+            if last:
+                sums[r] = small.tile([P, 1], F32, tag="sum", name="sum%d" % r)
+                kw["accum_out"] = sums[r][:]
             nc.vector.scalar_tensor_tensor(
-                out=acc[:, r, :], in0=src, scalar=factor, in1=acc[:, r, :], op0=ALU.mult, op1=ALU.add
+                out=acc[:, r, :], in0=src, scalar=factor, in1=h_sb[:, r, :] if first else acc[:, r, :],
+                op0=ALU.mult, op1=ALU.add, **kw
             )
 
-        mv = {}
-        rstd = {}
+        def add_messages(k):
+            au = a_unit(k)
+            if au is None:
+                return
+            for r in A_CHUNKS:
+                add_scaled(r, ms[(k, r)][:], mask16[:, r, au : au + 1], au == 0, au == NODES - 1)
+
+        negmu = {}
         sd = {}
         y = {}
 
         def ln_stats(r):
-            stats = small.tile([P, 6], F32, tag="stats")
-            nc.vector.bn_stats(out=stats[:], in_=acc[:, r, :])
-            mv[r] = small.tile([P, 2], F32, tag="mv", name="mv%d" % r)
-            nc.vector.bn_aggr(out=mv[r][:], in_=stats[:])
-            ve = small.tile([P, 1], F32, tag="ve")
-            nc.vector.tensor_scalar_add(out=ve[:], in0=mv[r][:, 1:2], scalar1=EPS)
+            negmu[r] = small.tile([P, 1], F32, tag="negmu", name="negmu%d" % r)
+            nc.vector.tensor_scalar_mul(out=negmu[r][:], in0=sums[r][:], scalar1=-1.0 / D)
+            y[r] = small.tile([P, D], F32, tag="y", name="y%d" % r)
+            sq = small.tile([P, 1], F32, tag="sq", name="sq%d" % r)
+            nc.scalar.activation(out=y[r][:], in_=acc[:, r, :], func=ACT.Square, bias=negmu[r][:], accum_out=sq[:])
             sd[r] = small.tile([P, 1], F32, tag="sd", name="sd%d" % r)
-            nc.scalar.sqrt(out=sd[r][:], in_=ve[:])
+            nc.scalar.activation(out=sd[r][:], in_=sq[:], func=ACT.Sqrt, scale=1.0 / D, bias=EPS)
 
-        def ln_rstd(r):
-            rstd[r] = small.tile([P, 1], F32, tag="rstd", name="rstd%d" % r)
-            nc.vector.reciprocal(out=rstd[r][:], in_=sd[r][:])
-
-        def ln_apply_gpsimd(r):
-            y[r] = small.tile([P, D], F32, tag="y", name="y%d" % r)
-            nc.gpsimd.tensor_scalar(
-                out=y[r][:], in0=acc[:, r, :], scalar1=mv[r][:, 0:1], scalar2=rstd[r][:], op0=ALU.subtract, op1=ALU.mult
-            )
-            nc.gpsimd.tensor_tensor(out=y[r][:], in0=y[r][:], in1=gamma_bc[:], op=ALU.mult)
-            nc.gpsimd.tensor_tensor(out=y[r][:], in0=y[r][:], in1=beta_bc[:], op=ALU.add)
-            nc.sync.dma_start(out=out_flat[P * r : P * r + P, :], in_=y[r][:])
-
-        def ln_centre_vector(r):
-            y[r] = small.tile([P, D], F32, tag="y", name="y%d" % r)
+        def ln_centre(r):
             nc.vector.scalar_tensor_tensor(
-                out=y[r][:], in0=acc[:, r, :], scalar=mv[r][:, 0:1], in1=gamma_bc[:], op0=ALU.subtract, op1=ALU.mult
+                out=acc[:, r, :], in0=acc[:, r, :], scalar=negmu[r][:], in1=gamma_bc[:], op0=ALU.add, op1=ALU.mult
             )
 
-        def ln_finish_vector(r):
+        def ln_finish(r):
+            rstd = small.tile([P, 1], F32, tag="rstd", name="rstd%d" % r)
+            nc.vector.reciprocal(out=rstd[:], in_=sd[r][:])
+            y2 = small.tile([P, D], F32, tag="y2", name="y2%d" % r)
             nc.vector.scalar_tensor_tensor(
-                out=y[r][:], in0=y[r][:], scalar=rstd[r][:], in1=beta_bc[:], op0=ALU.mult, op1=ALU.add
+                out=y2[:], in0=acc[:, r, :], scalar=rstd[:], in1=beta_bc[:], op0=ALU.mult, op1=ALU.add
             )
-            nc.sync.dma_start(out=out_flat[P * r : P * r + P, :], in_=y[r][:])
+            nc.sync.dma_start(out=out_flat[P * r : P * r + P, :], in_=y2[:])
 
-        def prepare(k, banks):
-            new_z(k)
-            relu_from_psum(k, banks)
-            if a_seq[k] is not None:
-                for c in range(2):
-                    sums_on_vector(k, c)
-                    relu_in_place(k, c, "s")
-            sums_from_psum(k, banks)
-
-        def ln_apply(r):
-            ln_centre_vector(r)
-            ln_rstd(r)
-            ln_finish_vector(r)
-
-        pre_next = {}
-        sums_on_tensor(0, pre_next)
-        start_acc()
-        prepare(0, pre_next)
-
+        b1f = const.tile([P, 2, 4], F32)
+        for o in ("a", "b"):
+            regroup_w1(o, 0, "v", 0, 3)
+            regroup_w1(o, 0, "s", 3, 4)
+            if o == "a":
+                nc.vector.quantize_mx(out=hq[:].bitcast(FP8X4), scales=hs[:], in_=gh[:])
+                quantise_w1("a", 0)
+                first_layer_t("a", 0)
+        quantise_w1("b", 0)
+        first_layer_out_t("a", 0)
+        first_layer_t("b", 0)
+        regroup_w1("a", 1, "s", 2, 4)
+        new_z(0, 0)
+        sums_on_tensor(0, 0)
+        first_layer_out_t("b", 0)
+        regroup_w1("b", 1, "s", 2, 4)
+        relu_from_psum(0, 0)
+        regroup_w1("a", 1, "v", 0, 2)
+        quantise_w1("a", 1)
+        first_layer_a(0)
+        first_layer_t("a", 1)
+        regroup_w1("b", 1, "v", 0, 2)
+        quantise_w1("b", 1)
+        first_layer_t("b", 1)
+        first_layer_out_t("a", 1)
+        nc.vector.tensor_copy(out=b1f[:], in_=b1_sb[:])
+        first_layer_out_a(0)
+        first_layer_out_t("b", 1)
+        move_neighbours(0, "v")
+        new_z(0, 1)
+        sums_on_tensor(0, 1)
+        new_z(1, 0)
+        sums_on_tensor(1, 0)
+        relu_from_psum(0, 1)
+        relu_from_psum(1, 0)
+        first_layer_a(1)
+        regroup_w2(0, "v")
+        first_layer_out_a(1)
+        regroup_w2(1, "s")
+        mask_scalars()
+        quantise_w2(0)
+        move_neighbours(1, "s")
+        move_neighbours(2, "s")
+        sums_on_vector(1, 0)
+        relu_in_place(1, 0)
+        new_z(1, 1)
+        sums_on_vector(1, 1)
+        for c in range(2):
+            quantise_z(0, c)
+        quantise_w2(1)
+        new_z(2, 0)
+        sums_on_vector(2, 0)
         for k in range(rounds):
             more = k + 1 < rounds
-            ms = {}
-            pre_next = {}
-            if more:
-                sums_on_tensor(k + 1, pre_next)
-            quantise_z(k, 1)
-            quantise_z(k, 0)
+            for kk, c in ((k + 1, 1), (k + 2, 0)):
+                if kk < rounds:
+                    sums_on_tensor(kk, c)
+                    relu_from_psum(kk, c)
+                    relu_in_place(kk, c)
+            for kk, c in ((k + 2, 1), (k + 3, 0)):
+                if kk < rounds:
+                    new_z(kk, c)
+                    sums_on_vector(kk, c)
+            second_layer_a(k)
+            second_layer_t(k)
+            if k + 3 < NODES:
+                move_neighbours(k + 3, "s")
             if k == 0:
-                for c in range(2):
-                    nc.vector.quantize_mx(out=w2q[:, c, :].bitcast(FP8X4), scales=w2s[:, c, :], in_=g2[c][:])
-            if a_seq[k] is not None:
-                second_layer_a(k, ms)
-            second_layer_t(k, ms)
+                for r in T_CHUNKS:
+                    add_scaled(r, self_t[r][:], degm1[:, r : r + 1], True, False)
+            if 8 <= k < 8 + CHUNKS:
+                add_scaled(k - 8, b2_bc[:], deg16[:, k - 8 : k - 7], False, False)
+            add_messages(k)
             if more:
-                prepare(k + 1, pre_next)
-                for r in A_CHUNKS:
-                    add_scaled(r, ms[r][:], mask16[:, r, a_seq[k] : a_seq[k] + 1])
-                if t_seq[k] == "za":
-                    for r in T_CHUNKS:
-                        add_scaled(r, ms[r][:], degm1[:, r : r + 1])
-                if k + 2 < NODES:
-                    for x in range(2):
-                        mask_rotation(x, k + 2, "s")
-
+                for c in range(2):
+                    quantise_z(k + 1, c)
+            if t_unit(k) == NODES - 1:
+                for r in T_CHUNKS:
+                    add_scaled(r, g_t[r][:], 1.0 / NODES, False, True)
+                    ln_stats(r)
+                for r in T_CHUNKS:
+                    ln_centre(r)
+                    ln_finish(r)
         for r in A_CHUNKS:
             ln_stats(r)
         for r in A_CHUNKS:
-            ln_apply(r)
-        for r in T_CHUNKS:
-            add_scaled(r, g_t[r][:], 1.0 / NODES)
-            ln_stats(r)
-        for r in T_CHUNKS:
-            ln_apply(r)
+            ln_centre(r)
+            ln_finish(r)

@@ -35,7 +35,7 @@ def tile_simplegnn_pa_t_kernel(tc, h, adj_mask, w1a, w1b, b1, w2, b2, gamma, bet
 
     with ExitStack() as ctx:
         const = ctx.enter_context(tc.tile_pool(name="const", bufs=1))
-        zpool = ctx.enter_context(tc.tile_pool(name="zpool", bufs=8))
+        zpool = ctx.enter_context(tc.tile_pool(name="zpool", bufs=4))
         small = ctx.enter_context(tc.tile_pool(name="small", bufs=4))
         w_pool = ctx.enter_context(tc.psum_pool(name="w", bufs=6))
         g_pool = ctx.enter_context(tc.psum_pool(name="g", bufs=2))
@@ -280,7 +280,7 @@ def tile_simplegnn_pa_t_kernel(tc, h, adj_mask, w1a, w1b, b1, w2, b2, gamma, bet
             return k - LEAD if k >= LEAD else None
 
         def new_z(k, c):
-            z[(k, c)] = zpool.tile([P, 4 * ROWS], BF16, tag="z", name="z%d" % c, align_bytes=64)
+            z[(k, c)] = zpool.tile([P, 4 * ROWS], BF16, tag="z%d" % c, name="z%d" % c, align_bytes=64)
 
         pre = {}
 
@@ -332,8 +332,8 @@ def tile_simplegnn_pa_t_kernel(tc, h, adj_mask, w1a, w1b, b1, w2, b2, gamma, bet
                 nc.scalar.activation(out=z[(k, c)][:, 0 : 4 * N_A], in_=z[(k, c)][:, 0 : 4 * N_A], func=ACT.Relu)
 
         def quantise_z(k, c):
-            zq[(k, c)] = zpool.tile([P, ROWS], U32, tag="zq", name="zq%d" % c, align_bytes=64)
-            zs[(k, c)] = zpool.tile([P, ROWS], U8, tag="zs", name="zs%d" % c, align_bytes=64)
+            zq[(k, c)] = zpool.tile([P, ROWS], U32, tag="zq%d" % c, name="zq%d" % c, align_bytes=64)
+            zs[(k, c)] = zpool.tile([P, ROWS], U8, tag="zs%d" % c, name="zs%d" % c, align_bytes=64)
             lo = N_A if a_unit(k) is None else 0
             hi = N_A if t_unit(k) is None else ROWS
             nc.vector.quantize_mx(
@@ -403,23 +403,24 @@ def tile_simplegnn_pa_t_kernel(tc, h, adj_mask, w1a, w1b, b1, w2, b2, gamma, bet
         def ln_stats(r):
             negmu[r] = small.tile([P, 1], F32, tag="negmu", name="negmu%d" % r)
             nc.vector.tensor_scalar_mul(out=negmu[r][:], in0=sums[r][:], scalar1=-1.0 / D)
-            y[r] = small.tile([P, D], F32, tag="y", name="y%d" % r)
+            junk = small.tile([P, D], F32, tag="junk", name="junk", bufs=2)
             sq = small.tile([P, 1], F32, tag="sq", name="sq%d" % r)
-            nc.scalar.activation(out=y[r][:], in_=acc[:, r, :], func=ACT.Square, bias=negmu[r][:], accum_out=sq[:])
+            nc.scalar.activation(out=junk[:], in_=acc[:, r, :], func=ACT.Square, bias=negmu[r][:], accum_out=sq[:])
             sd[r] = small.tile([P, 1], F32, tag="sd", name="sd%d" % r)
             nc.scalar.activation(out=sd[r][:], in_=sq[:], func=ACT.Sqrt, scale=1.0 / D, bias=EPS)
 
         def ln_centre(r):
+            y[r] = small.tile([P, D], F32, tag="y", name="y%d" % r, bufs=2)
             nc.vector.scalar_tensor_tensor(
-                out=acc[:, r, :], in0=acc[:, r, :], scalar=negmu[r][:], in1=gamma_bc[:], op0=ALU.add, op1=ALU.mult
+                out=y[r][:], in0=acc[:, r, :], scalar=negmu[r][:], in1=gamma_bc[:], op0=ALU.add, op1=ALU.mult
             )
 
         def ln_finish(r):
             rstd = small.tile([P, 1], F32, tag="rstd", name="rstd%d" % r)
             nc.vector.reciprocal(out=rstd[:], in_=sd[r][:])
-            y2 = small.tile([P, D], F32, tag="y2", name="y2%d" % r)
+            y2 = small.tile([P, D], F32, tag="y2", name="y2%d" % r, bufs=2)
             nc.vector.scalar_tensor_tensor(
-                out=y2[:], in0=acc[:, r, :], scalar=rstd[:], in1=beta_bc[:], op0=ALU.mult, op1=ALU.add
+                out=y2[:], in0=y[r][:], scalar=rstd[:], in1=beta_bc[:], op0=ALU.mult, op1=ALU.add
             )
             nc.sync.dma_start(out=out_flat[P * r : P * r + P, :], in_=y2[:])
 
@@ -459,55 +460,92 @@ def tile_simplegnn_pa_t_kernel(tc, h, adj_mask, w1a, w1b, b1, w2, b2, gamma, bet
         relu_from_psum(0, 1)
         relu_from_psum(1, 0)
         first_layer_a(1)
+        new_z(1, 1)
+        sums_on_tensor(1, 1)
+        move_neighbours(1, "v")
+        move_neighbours(2, "v")
         regroup_w2(0, "v")
         first_layer_out_a(1)
+        relu_from_psum(1, 1)
         regroup_w2(1, "s")
         mask_scalars()
         quantise_w2(0)
-        move_neighbours(1, "s")
-        move_neighbours(2, "s")
-        sums_on_vector(1, 0)
-        relu_in_place(1, 0)
-        new_z(1, 1)
-        sums_on_vector(1, 1)
-        for c in range(2):
-            quantise_z(0, c)
-        quantise_w2(1)
-        new_z(2, 0)
+        for k in (2, 3):
+            for c in range(2):
+                new_z(k, c)
         sums_on_vector(2, 0)
-        for k in range(rounds):
-            more = k + 1 < rounds
-            for kk, c in ((k + 1, 1), (k + 2, 0)):
-                if kk < rounds:
-                    sums_on_tensor(kk, c)
-                    relu_from_psum(kk, c)
-                    relu_in_place(kk, c)
-            for kk, c in ((k + 2, 1), (k + 3, 0)):
-                if kk < rounds:
-                    new_z(kk, c)
-                    sums_on_vector(kk, c)
-            second_layer_a(k)
-            second_layer_t(k)
-            if k + 3 < NODES:
-                move_neighbours(k + 3, "s")
-            if k == 0:
-                for r in T_CHUNKS:
-                    add_scaled(r, self_t[r][:], degm1[:, r : r + 1], True, False)
-            if 8 <= k < 8 + CHUNKS:
-                add_scaled(k - 8, b2_bc[:], deg16[:, k - 8 : k - 7], False, False)
-            add_messages(k)
-            if more:
+        sums_on_vector(2, 1)
+        for k in range(2):
+            for c in range(2):
+                quantise_z(k, c)
+        quantise_w2(1)
+        move_neighbours(3, "v")
+        move_neighbours(4, "v")
+        sums_on_vector(3, 0)
+        sums_on_vector(3, 1)
+        def finish_t():
+            for r in T_CHUNKS:
+                add_scaled(r, g_t[r][:], 1.0 / NODES, False, True)
+                ln_stats(r)
+            for r in T_CHUNKS:
+                ln_centre(r)
+            for r in T_CHUNKS:
+                ln_finish(r)
+
+        for k0 in range(0, rounds, 2):
+            pair = [k for k in (k0, k0 + 1) if k < rounds]
+            ahead = [k for k in (k0 + 2, k0 + 3) if k < rounds]
+            for k in ahead:
                 for c in range(2):
-                    quantise_z(k + 1, c)
-            if t_unit(k) == NODES - 1:
-                for r in T_CHUNKS:
-                    add_scaled(r, g_t[r][:], 1.0 / NODES, False, True)
-                    ln_stats(r)
-                for r in T_CHUNKS:
-                    ln_centre(r)
-                    ln_finish(r)
+                    sums_on_tensor(k, c)
+                    relu_from_psum(k, c)
+            for k in ahead:
+                for c in range(2):
+                    relu_in_place(k, c)
+            last_t = any([t_unit(k) == NODES - 1 for k in pair])
+            for k in pair:
+                second_layer_t(k)
+                second_layer_a(k)
+            for k in ahead:
+                if k + 3 < NODES:
+                    move_neighbours(k + 3, "s")
+            for c in range(2):
+                if k0 + 4 < rounds:
+                    new_z(k0 + 4, c)
+                    sums_on_vector(k0 + 4, c)
+            for k in (k0,):
+                if k == 0:
+                    for r in T_CHUNKS:
+                        add_scaled(r, self_t[r][:], degm1[:, r : r + 1], True, False)
+                if 8 <= k < 8 + CHUNKS:
+                    add_scaled(k - 8, b2_bc[:], deg16[:, k - 8 : k - 7], False, False)
+                if t_unit(k) == NODES - 1:
+                    finish_t()
+                if k < rounds:
+                    add_messages(k)
+            for c in range(2):
+                if k0 + 2 < rounds:
+                    quantise_z(k0 + 2, c)
+            for k in (k0 + 1,):
+                if k == 0:
+                    for r in T_CHUNKS:
+                        add_scaled(r, self_t[r][:], degm1[:, r : r + 1], True, False)
+                if 8 <= k < 8 + CHUNKS:
+                    add_scaled(k - 8, b2_bc[:], deg16[:, k - 8 : k - 7], False, False)
+                if t_unit(k) == NODES - 1:
+                    finish_t()
+                if k < rounds:
+                    add_messages(k)
+            for c in range(2):
+                if k0 + 3 < rounds:
+                    quantise_z(k0 + 3, c)
+            for c in range(2):
+                if k0 + 5 < rounds:
+                    new_z(k0 + 5, c)
+                    sums_on_vector(k0 + 5, c)
         for r in A_CHUNKS:
             ln_stats(r)
         for r in A_CHUNKS:
             ln_centre(r)
+        for r in A_CHUNKS:
             ln_finish(r)

@@ -42,10 +42,12 @@ def tile_simplegnn_pa_t_kernel(tc, h, adj_mask, w1a, w1b, b1, w2, b2, gamma, bet
         ctx.enter_context(tc.manual_schedule())
         ctx.enter_context(nc.allow_low_precision(reason="zeros and ones: sums with at most one one are exact in bfloat16"))
 
+        b1_row = const.tile([P, F], BF16)
+        nc.gpsimd.memset(b1_row[:], 0.0)
+        nc.sync.dma_start(out=b1_row[0:1, :], in_=b1.unsqueeze(0))
         mask_sb = const.tile([P, CHUNKS, NODES], BF16)
-        b1_sb = const.tile([P, 2, 4], BF16)
-        with nc.allow_non_contiguous_dma(reason="small bias and mask tables"):
-            nc.sync.dma_start(out=mask_sb[:], in_=adj_flat.rearrange("(r p) j -> p r j", p=P))
+        with nc.allow_non_contiguous_dma(reason="small mask table"):
+            nc.scalar.dma_start(out=mask_sb[:], in_=adj_flat.rearrange("(r p) j -> p r j", p=P))
         h_sb = const.tile([P, CHUNKS, D], BF16)
         nc.sync.dma_start(out=h_sb[:], in_=h_flat.rearrange("(r p) d -> p r d", p=P))
         raw1 = {}
@@ -62,12 +64,8 @@ def tile_simplegnn_pa_t_kernel(tc, h, adj_mask, w1a, w1b, b1, w2, b2, gamma, bet
 
         load_w1("a", 0)
         load_w1("b", 0)
-        b1_bc = const.tile([P, F], BF16)
-        nc.sync.dma_start(out=b1_bc[:], in_=b1.partition_broadcast(P))
         load_w1("a", 1)
         load_w1("b", 1)
-        with nc.allow_non_contiguous_dma(reason="small bias table"):
-            nc.sync.dma_start(out=b1_sb[:], in_=b1.rearrange("(c p t) -> p c t", c=2, p=P, t=4))
         raw2 = {}
         for c in range(2):
             raw2[c] = const.tile([P, 4, D], BF16, name="raw2%d" % c)
@@ -85,6 +83,21 @@ def tile_simplegnn_pa_t_kernel(tc, h, adj_mask, w1a, w1b, b1, w2, b2, gamma, bet
         nc.scalar.sqrt(out=warm2[:], in_=warm[:])
         ident = const.tile([P, P], F32)
         make_identity(nc, ident[:])
+        ones = const.tile([P, P], BF16)
+        nc.vector.memset(ones[:], 1.0)
+        b1_bc = const.tile([P, F], BF16)
+        b1f = const.tile([P, 2, 4], F32)
+        ps_f = w_pool.tile([P, 2, 4], F32, tag="w")
+        for c in range(2):
+            ps_b = w_pool.tile([P, 512], F32, tag="w")
+            nc.tensor.matmul(out=ps_b[:], lhsT=ones[:], rhs=b1_row[:, 512 * c : 512 * c + 512], start=True, stop=True)
+            nc.scalar.copy(out=b1_bc[:, 512 * c : 512 * c + 512], in_=ps_b[:])
+            for t in range(4):
+                nc.tensor.matmul(
+                    out=ps_f[:, c, t : t + 1], lhsT=b1_row[:, 512 * c + t : 512 * c + 512 : 4], rhs=ones[:, 0:1],
+                    start=True, stop=True,
+                )
+        nc.scalar.copy(out=b1f[:], in_=ps_f[:])
         ident_d = const.tile([P, 8, 2 * NODES], F32)
         ident_v = ident[:].rearrange("p (g i) -> p g i", i=NODES)
         nc.vector.tensor_copy(out=ident_d[:, :, 0:NODES], in_=ident_v)
@@ -424,7 +437,6 @@ def tile_simplegnn_pa_t_kernel(tc, h, adj_mask, w1a, w1b, b1, w2, b2, gamma, bet
             )
             nc.sync.dma_start(out=out_flat[P * r : P * r + P, :], in_=y2[:])
 
-        b1f = const.tile([P, 2, 4], F32)
         for o in ("a", "b"):
             regroup_w1(o, 0, "v", 0, 3)
             regroup_w1(o, 0, "s", 3, 4)
@@ -449,7 +461,6 @@ def tile_simplegnn_pa_t_kernel(tc, h, adj_mask, w1a, w1b, b1, w2, b2, gamma, bet
         quantise_w1("b", 1)
         first_layer_t("b", 1)
         first_layer_out_t("a", 1)
-        nc.vector.tensor_copy(out=b1f[:], in_=b1_sb[:])
         first_layer_out_a(0)
         first_layer_out_t("b", 1)
         move_neighbours(0, "v")

@@ -37,13 +37,14 @@ def tile_simplegnn_pa_t_kernel(tc, h, adj_mask, w1a, w1b, b1, w2, b2, gamma, bet
         const = ctx.enter_context(tc.tile_pool(name="const", bufs=1))
         zpool = ctx.enter_context(tc.tile_pool(name="zpool", bufs=4))
         small = ctx.enter_context(tc.tile_pool(name="small", bufs=4))
+        movepool = ctx.enter_context(tc.tile_pool(name="move", bufs=8))
         w_pool = ctx.enter_context(tc.psum_pool(name="w", bufs=6))
         g_pool = ctx.enter_context(tc.psum_pool(name="g", bufs=2))
         ctx.enter_context(tc.manual_schedule())
         ctx.enter_context(nc.allow_low_precision(reason="zeros and ones: sums with at most one one are exact in bfloat16"))
 
         b1_row = const.tile([P, F], BF16)
-        nc.gpsimd.memset(b1_row[:], 0.0)
+        nc.vector.memset(b1_row[:], 0.0)
         nc.sync.dma_start(out=b1_row[0:1, :], in_=b1.unsqueeze(0))
         mask_sb = const.tile([P, CHUNKS, NODES], BF16)
         with nc.allow_non_contiguous_dma(reason="small mask table"):
@@ -155,11 +156,12 @@ def tile_simplegnn_pa_t_kernel(tc, h, adj_mask, w1a, w1b, b1, w2, b2, gamma, bet
         mt = const.tile([P, 2, NODES], F32)
         rotate_rows(mt[:], adj_t[:])
 
-        move = const.tile([P, 2, NODES, P], F32)
+        move = {}
 
         def move_neighbours(u, eng):
+            move[u] = movepool.tile([P, 2, P], F32, tag="move", name="move%d" % u)
             for x in range(2):
-                dst = move[:, x, u, :].rearrange("p (g i) -> p g i", i=NODES)
+                dst = move[u][:, x, :].rearrange("p (g i) -> p g i", i=NODES)
                 if eng == "v":
                     nc.vector.tensor_scalar_mul(out=dst, in0=ident_d[:, :, u : u + NODES], scalar1=mt[:, x, u : u + 1])
                 else:
@@ -293,7 +295,7 @@ def tile_simplegnn_pa_t_kernel(tc, h, adj_mask, w1a, w1b, b1, w2, b2, gamma, bet
             return k - LEAD if k >= LEAD else None
 
         def new_z(k, c):
-            z[(k, c)] = zpool.tile([P, 4 * ROWS], BF16, tag="z%d" % c, name="z%d" % c, align_bytes=64)
+            z[(k, c)] = zpool.tile([P, 4 * ROWS], BF16, tag="z%d" % c, name="z%d" % c, align_bytes=64, bufs=4)
 
         pre = {}
 
@@ -308,7 +310,7 @@ def tile_simplegnn_pa_t_kernel(tc, h, adj_mask, w1a, w1b, b1, w2, b2, gamma, bet
                         nc.tensor.transpose(pre[(c, r)][:, t, :], xa[r][:, c, t, :], ident[:])
                         continue
                     nc.tensor.matmul(
-                        out=pre[(c, r)][:, t, :], lhsT=xb[r][:, c, t, :], rhs=move[:, x, tu, :],
+                        out=pre[(c, r)][:, t, :], lhsT=xb[r][:, c, t, :], rhs=move[tu][:, x, :],
                         is_transpose=True, start=True, stop=False,
                     )
                     nc.tensor.matmul(
@@ -345,8 +347,8 @@ def tile_simplegnn_pa_t_kernel(tc, h, adj_mask, w1a, w1b, b1, w2, b2, gamma, bet
                 nc.scalar.activation(out=z[(k, c)][:, 0 : 4 * N_A], in_=z[(k, c)][:, 0 : 4 * N_A], func=ACT.Relu)
 
         def quantise_z(k, c):
-            zq[(k, c)] = zpool.tile([P, ROWS], U32, tag="zq%d" % c, name="zq%d" % c, align_bytes=64)
-            zs[(k, c)] = zpool.tile([P, ROWS], U8, tag="zs%d" % c, name="zs%d" % c, align_bytes=64)
+            zq[(k, c)] = zpool.tile([P, ROWS], U32, tag="zq%d" % c, name="zq%d" % c, align_bytes=64, bufs=6)
+            zs[(k, c)] = zpool.tile([P, ROWS], U8, tag="zs%d" % c, name="zs%d" % c, align_bytes=64, bufs=6)
             lo = N_A if a_unit(k) is None else 0
             hi = N_A if t_unit(k) is None else ROWS
             nc.vector.quantize_mx(
@@ -423,19 +425,32 @@ def tile_simplegnn_pa_t_kernel(tc, h, adj_mask, w1a, w1b, b1, w2, b2, gamma, bet
             nc.scalar.activation(out=sd[r][:], in_=sq[:], func=ACT.Sqrt, scale=1.0 / D, bias=EPS)
 
         def ln_centre(r):
-            y[r] = small.tile([P, D], F32, tag="y", name="y%d" % r, bufs=2)
+            y[r] = small.tile([P, D], F32, tag="y", name="y%d" % r, bufs=4)
             nc.vector.scalar_tensor_tensor(
                 out=y[r][:], in0=acc[:, r, :], scalar=negmu[r][:], in1=gamma_bc[:], op0=ALU.add, op1=ALU.mult
             )
 
-        def ln_finish(r):
+        def ln_aside(r):
             rstd = small.tile([P, 1], F32, tag="rstd", name="rstd%d" % r)
             nc.vector.reciprocal(out=rstd[:], in_=sd[r][:])
-            y2 = small.tile([P, D], F32, tag="y2", name="y2%d" % r, bufs=2)
-            nc.vector.scalar_tensor_tensor(
-                out=y2[:], in0=y[r][:], scalar=rstd[:], in1=beta_bc[:], op0=ALU.mult, op1=ALU.add
-            )
-            nc.sync.dma_start(out=out_flat[P * r : P * r + P, :], in_=y2[:])
+            shift = small.tile([P, 1], F32, tag="shift", name="shift%d" % r)
+            nc.vector.tensor_scalar_mul(out=shift[:], in0=negmu[r][:], scalar1=rstd[:])
+            y[r] = small.tile([P, D], F32, tag="y", name="y%d" % r, bufs=4)
+            nc.scalar.activation(out=y[r][:], in_=acc[:, r, :], func=ACT.Identity, scale=rstd[:], bias=shift[:])
+            nc.gpsimd.tensor_tensor(out=y[r][:], in0=y[r][:], in1=gamma_bc[:], op=ALU.mult)
+            nc.gpsimd.tensor_tensor(out=y[r][:], in0=y[r][:], in1=beta_bc[:], op=ALU.add)
+            nc.gpsimd.dma_start(out=out_flat[P * r : P * r + P, :], in_=y[r][:])
+
+        def ln_finish(r, width=D):
+            rstd = small.tile([P, 1], F32, tag="rstd", name="rstd%d" % r)
+            nc.vector.reciprocal(out=rstd[:], in_=sd[r][:])
+            y2 = small.tile([P, D], F32, tag="y2", name="y2%d" % r, bufs=4)
+            for lo in range(0, D, width):
+                cols = slice(lo, lo + width)
+                nc.vector.scalar_tensor_tensor(
+                    out=y2[:, cols], in0=y[r][:, cols], scalar=rstd[:], in1=beta_bc[:, cols], op0=ALU.mult, op1=ALU.add
+                )
+                nc.sync.dma_start(out=out_flat[P * r : P * r + P, cols], in_=y2[:, cols])
 
         for o in ("a", "b"):
             regroup_w1(o, 0, "v", 0, 3)
@@ -476,16 +491,21 @@ def tile_simplegnn_pa_t_kernel(tc, h, adj_mask, w1a, w1b, b1, w2, b2, gamma, bet
         move_neighbours(1, "v")
         move_neighbours(2, "v")
         regroup_w2(0, "v")
+        regroup_w2(1, "v")
         first_layer_out_a(1)
         relu_from_psum(1, 1)
-        regroup_w2(1, "s")
         mask_scalars()
         quantise_w2(0)
-        for k in (2, 3):
+        for k in (2, 3, 4, 5):
             for c in range(2):
                 new_z(k, c)
+        for c in range(2):
+            sums_on_tensor(2, c)
+            relu_from_psum(2, c)
         sums_on_vector(2, 0)
         sums_on_vector(2, 1)
+        for c in range(2):
+            relu_in_place(2, c)
         for k in range(2):
             for c in range(2):
                 quantise_z(k, c)
@@ -494,37 +514,37 @@ def tile_simplegnn_pa_t_kernel(tc, h, adj_mask, w1a, w1b, b1, w2, b2, gamma, bet
         move_neighbours(4, "v")
         sums_on_vector(3, 0)
         sums_on_vector(3, 1)
+        for c in range(2):
+            quantise_z(2, c)
+        for k in (4, 5):
+            for c in range(2):
+                sums_on_vector(k, c)
         def finish_t():
             for r in T_CHUNKS:
                 add_scaled(r, g_t[r][:], 1.0 / NODES, False, True)
                 ln_stats(r)
-            for r in T_CHUNKS:
-                ln_centre(r)
-            for r in T_CHUNKS:
-                ln_finish(r)
 
-        for k0 in range(0, rounds, 2):
-            pair = [k for k in (k0, k0 + 1) if k < rounds]
-            ahead = [k for k in (k0 + 2, k0 + 3) if k < rounds]
+        for k0 in range(0, rounds, 3):
+            pair = [k for k in range(k0, k0 + 3) if k < rounds]
+            ahead = [k for k in range(k0 + 3, k0 + 6) if k < rounds]
             for k in ahead:
                 for c in range(2):
                     sums_on_tensor(k, c)
                     relu_from_psum(k, c)
+                if k + 2 < NODES:
+                    move_neighbours(k + 2, "s")
             for k in ahead:
                 for c in range(2):
                     relu_in_place(k, c)
-            last_t = any([t_unit(k) == NODES - 1 for k in pair])
             for k in pair:
                 second_layer_t(k)
                 second_layer_a(k)
-            for k in ahead:
-                if k + 3 < NODES:
-                    move_neighbours(k + 3, "s")
-            for c in range(2):
-                if k0 + 4 < rounds:
-                    new_z(k0 + 4, c)
-                    sums_on_vector(k0 + 4, c)
-            for k in (k0,):
+            for n, k in enumerate(pair):
+                for kk in [k0 + 6 + n]:
+                    if kk < rounds and n == 0:
+                        for c in range(2):
+                            new_z(kk, c)
+                            sums_on_vector(kk, c)
                 if k == 0:
                     for r in T_CHUNKS:
                         add_scaled(r, self_t[r][:], degm1[:, r : r + 1], True, False)
@@ -532,28 +552,20 @@ def tile_simplegnn_pa_t_kernel(tc, h, adj_mask, w1a, w1b, b1, w2, b2, gamma, bet
                     add_scaled(k - 8, b2_bc[:], deg16[:, k - 8 : k - 7], False, False)
                 if t_unit(k) == NODES - 1:
                     finish_t()
-                if k < rounds:
-                    add_messages(k)
-            for c in range(2):
-                if k0 + 2 < rounds:
-                    quantise_z(k0 + 2, c)
-            for k in (k0 + 1,):
-                if k == 0:
-                    for r in T_CHUNKS:
-                        add_scaled(r, self_t[r][:], degm1[:, r : r + 1], True, False)
-                if 8 <= k < 8 + CHUNKS:
-                    add_scaled(k - 8, b2_bc[:], deg16[:, k - 8 : k - 7], False, False)
+                add_messages(k)
                 if t_unit(k) == NODES - 1:
-                    finish_t()
-                if k < rounds:
-                    add_messages(k)
-            for c in range(2):
-                if k0 + 3 < rounds:
-                    quantise_z(k0 + 3, c)
-            for c in range(2):
-                if k0 + 5 < rounds:
-                    new_z(k0 + 5, c)
-                    sums_on_vector(k0 + 5, c)
+                    ln_aside(T_CHUNKS[0])
+                    ln_centre(T_CHUNKS[1])
+                    ln_finish(T_CHUNKS[1])
+                if k + 3 < rounds:
+                    for c in range(2):
+                        quantise_z(k + 3, c)
+            if True:
+                for kk in range(k0 + 6 + 1, k0 + 9):
+                    if kk < rounds:
+                        for c in range(2):
+                            new_z(kk, c)
+                            sums_on_vector(kk, c)
         for r in A_CHUNKS:
             ln_stats(r)
         for r in A_CHUNKS:

@@ -44,11 +44,33 @@ def tile_simplegnn_pa_t_kernel(tc, h, adj_mask, w1a, w1b, b1, w2, b2, gamma, bet
         ctx.enter_context(nc.allow_low_precision(reason="zeros and ones: sums with at most one one are exact in bfloat16"))
 
         b1_row = const.tile([P, F], BF16)
-        nc.vector.memset(b1_row[:], 0.0)
-        nc.sync.dma_start(out=b1_row[0:1, :], in_=b1.unsqueeze(0))
+        warm = const.tile([P, 1], F32)
+        nc.vector.memset(warm[:], 1.0)
+        warm2 = const.tile([P, 1], F32)
+        nc.scalar.sqrt(out=warm2[:], in_=warm[:])
+        ident = const.tile([P, P], F32)
+        make_identity(nc, ident[:])
+        ones = const.tile([P, P], BF16)
+        nc.vector.memset(ones[:], 1.0)
+        ident_d = const.tile([P, 8, 2 * NODES], F32)
+        ident_v = ident[:].rearrange("p (g i) -> p g i", i=NODES)
+        nc.vector.tensor_copy(out=ident_d[:, :, 0:NODES], in_=ident_v)
+        nc.vector.tensor_copy(out=ident_d[:, :, NODES : 2 * NODES], in_=ident_v)
+        i16d = const.tile([P, 2 * NODES], BF16)
+        nc.vector.tensor_reduce(
+            out=i16d[:, 0:NODES], in_=ident[:].rearrange("p (g i) -> p i g", i=NODES), axis=AX.X, op=ALU.add
+        )
+        nc.vector.tensor_copy(out=i16d[:, NODES : 2 * NODES], in_=i16d[:, 0:NODES])
+        sel2 = const.tile([P, NODES, NODES], BF16)
+        for u in range(NODES):
+            nc.vector.tensor_copy(out=sel2[:, u, :], in_=i16d[:, u : u + NODES])
+        bd8 = const.tile([P, 8], F32)
+        nc.vector.tensor_reduce(out=bd8[:], in_=ident_v, axis=AX.X, op=ALU.add)
+        nc.vector.memset(b1_row[:].bitcast(F32), 0.0)
+
         mask_sb = const.tile([P, CHUNKS, NODES], BF16)
         with nc.allow_non_contiguous_dma(reason="small mask table"):
-            nc.scalar.dma_start(out=mask_sb[:], in_=adj_flat.rearrange("(r p) j -> p r j", p=P))
+            nc.sync.dma_start(out=mask_sb[:], in_=adj_flat.rearrange("(r p) j -> p r j", p=P))
         h_sb = const.tile([P, CHUNKS, D], BF16)
         nc.sync.dma_start(out=h_sb[:], in_=h_flat.rearrange("(r p) d -> p r d", p=P))
         raw1 = {}
@@ -65,6 +87,7 @@ def tile_simplegnn_pa_t_kernel(tc, h, adj_mask, w1a, w1b, b1, w2, b2, gamma, bet
 
         load_w1("a", 0)
         load_w1("b", 0)
+        nc.sync.dma_start(out=b1_row[0:1, :], in_=b1.unsqueeze(0))
         load_w1("a", 1)
         load_w1("b", 1)
         raw2 = {}
@@ -78,41 +101,6 @@ def tile_simplegnn_pa_t_kernel(tc, h, adj_mask, w1a, w1b, b1, w2, b2, gamma, bet
         nc.sync.dma_start(out=gamma_bc[:], in_=gamma.partition_broadcast(P))
         nc.sync.dma_start(out=beta_bc[:], in_=beta.partition_broadcast(P))
 
-        warm = const.tile([P, 1], F32)
-        nc.vector.memset(warm[:], 1.0)
-        warm2 = const.tile([P, 1], F32)
-        nc.scalar.sqrt(out=warm2[:], in_=warm[:])
-        ident = const.tile([P, P], F32)
-        make_identity(nc, ident[:])
-        ones = const.tile([P, P], BF16)
-        nc.vector.memset(ones[:], 1.0)
-        b1_bc = const.tile([P, F], BF16)
-        b1f = const.tile([P, 2, 4], F32)
-        ps_f = w_pool.tile([P, 2, 4], F32, tag="w")
-        for c in range(2):
-            ps_b = w_pool.tile([P, 512], F32, tag="w")
-            nc.tensor.matmul(out=ps_b[:], lhsT=ones[:], rhs=b1_row[:, 512 * c : 512 * c + 512], start=True, stop=True)
-            nc.scalar.copy(out=b1_bc[:, 512 * c : 512 * c + 512], in_=ps_b[:])
-            for t in range(4):
-                nc.tensor.matmul(
-                    out=ps_f[:, c, t : t + 1], lhsT=b1_row[:, 512 * c + t : 512 * c + 512 : 4], rhs=ones[:, 0:1],
-                    start=True, stop=True,
-                )
-        nc.scalar.copy(out=b1f[:], in_=ps_f[:])
-        ident_d = const.tile([P, 8, 2 * NODES], F32)
-        ident_v = ident[:].rearrange("p (g i) -> p g i", i=NODES)
-        nc.vector.tensor_copy(out=ident_d[:, :, 0:NODES], in_=ident_v)
-        nc.vector.tensor_copy(out=ident_d[:, :, NODES : 2 * NODES], in_=ident_v)
-        i16d = const.tile([P, 2 * NODES], BF16)
-        nc.vector.tensor_reduce(
-            out=i16d[:, 0:NODES], in_=ident[:].rearrange("p (g i) -> p i g", i=NODES), axis=AX.X, op=ALU.add
-        )
-        nc.vector.tensor_copy(out=i16d[:, NODES : 2 * NODES], in_=i16d[:, 0:NODES])
-        sel2 = const.tile([P, NODES, NODES], BF16)
-        for u in range(NODES):
-            nc.vector.tensor_copy(out=sel2[:, u, :], in_=i16d[:, u : u + NODES])
-        bd8 = const.tile([P, 8], F32)
-        nc.vector.tensor_reduce(out=bd8[:], in_=ident_v, axis=AX.X, op=ALU.add)
         blk = const.tile([P, 2, 8, NODES], F32)
         ps_e = w_pool.tile([P, 2, P], F32, tag="w")
         for x, r in enumerate(T_CHUNKS):
@@ -146,6 +134,25 @@ def tile_simplegnn_pa_t_kernel(tc, h, adj_mask, w1a, w1b, b1, w2, b2, gamma, bet
             for l in range(2):
                 r = 2 * half + l
                 nc.scalar.copy(out=ghw[:, r * P : (r + 1) * P, :], in_=ps_h[:, l, :, :].rearrange("p u r -> p r u"))
+        b1_bc = const.tile([P, F], BF16)
+        b1f = const.tile([P, 2, 4], F32)
+        ps_f = w_pool.tile([P, 2, 4], F32, tag="w")
+        ps_bs = []
+        for c in range(2):
+            ps_b = g_pool.tile([P, 512], F32, tag="g", name="ps_b%d" % c)
+            nc.tensor.matmul(out=ps_b[:], lhsT=ones[:], rhs=b1_row[:, 512 * c : 512 * c + 512], start=True, stop=True)
+            ps_bs.append(ps_b)
+            for t in range(4):
+                nc.tensor.matmul(
+                    out=ps_f[:, c, t : t + 1], lhsT=b1_row[:, 512 * c + t : 512 * c + 512 : 4], rhs=ones[:, 0:1],
+                    start=True, stop=True,
+                )
+
+        def spread_b1():
+            for c in range(2):
+                nc.scalar.copy(out=b1_bc[:, 512 * c : 512 * c + 512], in_=ps_bs[c][:])
+            nc.scalar.copy(out=b1f[:], in_=ps_f[:])
+
         hq = const.tile([P, ROWS], U32, align_bytes=64)
         hs = const.tile([P, ROWS], U8, align_bytes=64)
 
@@ -251,8 +258,8 @@ def tile_simplegnn_pa_t_kernel(tc, h, adj_mask, w1a, w1b, b1, w2, b2, gamma, bet
                     op=ALU.add,
                 )
 
-        w2q = const.tile([P, 2, D], U32, align_bytes=64)
-        w2s = const.tile([P, 2, D], U8, align_bytes=64)
+        w2q = const.tile([P, 2, D], U32, align_bytes=256)
+        w2s = const.tile([P, 2, D], U8, align_bytes=256)
         g2 = {}
         for c in range(2):
             g2[c] = const.tile([P, 2048], BF16, name="g2%d" % c, align_bytes=64)
@@ -347,8 +354,8 @@ def tile_simplegnn_pa_t_kernel(tc, h, adj_mask, w1a, w1b, b1, w2, b2, gamma, bet
                 nc.scalar.activation(out=z[(k, c)][:, 0 : 4 * N_A], in_=z[(k, c)][:, 0 : 4 * N_A], func=ACT.Relu)
 
         def quantise_z(k, c):
-            zq[(k, c)] = zpool.tile([P, ROWS], U32, tag="zq%d" % c, name="zq%d" % c, align_bytes=64, bufs=6)
-            zs[(k, c)] = zpool.tile([P, ROWS], U8, tag="zs%d" % c, name="zs%d" % c, align_bytes=64, bufs=6)
+            zq[(k, c)] = zpool.tile([P, ROWS], U32, tag="zq%d" % c, name="zq%d" % c, align_bytes=256, bufs=6)
+            zs[(k, c)] = zpool.tile([P, ROWS], U8, tag="zs%d" % c, name="zs%d" % c, align_bytes=256, bufs=6)
             lo = N_A if a_unit(k) is None else 0
             hi = N_A if t_unit(k) is None else ROWS
             nc.vector.quantize_mx(
@@ -459,6 +466,7 @@ def tile_simplegnn_pa_t_kernel(tc, h, adj_mask, w1a, w1b, b1, w2, b2, gamma, bet
                 nc.vector.quantize_mx(out=hq[:].bitcast(FP8X4), scales=hs[:], in_=gh[:])
                 quantise_w1("a", 0)
                 first_layer_t("a", 0)
+        spread_b1()
         quantise_w1("b", 0)
         first_layer_out_t("a", 0)
         first_layer_t("b", 0)
@@ -540,14 +548,14 @@ def tile_simplegnn_pa_t_kernel(tc, h, adj_mask, w1a, w1b, b1, w2, b2, gamma, bet
                 second_layer_t(k)
                 second_layer_a(k)
             for n, k in enumerate(pair):
+                if k == 0:
+                    for r in T_CHUNKS:
+                        add_scaled(r, self_t[r][:], degm1[:, r : r + 1], True, False)
                 for kk in [k0 + 6 + n]:
                     if kk < rounds and n == 0:
                         for c in range(2):
                             new_z(kk, c)
                             sums_on_vector(kk, c)
-                if k == 0:
-                    for r in T_CHUNKS:
-                        add_scaled(r, self_t[r][:], degm1[:, r : r + 1], True, False)
                 if 8 <= k < 8 + CHUNKS:
                     add_scaled(k - 8, b2_bc[:], deg16[:, k - 8 : k - 7], False, False)
                 if t_unit(k) == NODES - 1:

@@ -91,15 +91,19 @@ def tile_simplegnn_pa_t_kernel(tc, h, adj_mask, w1a, w1b, b1, w2, b2, gamma, bet
         load_w1("a", 1)
         load_w1("b", 1)
         raw2 = {}
-        for c in range(2):
+
+        def load_w2(c):
             raw2[c] = const.tile([P, 4, D], BF16, name="raw2%d" % c)
             nc.sync.dma_start(out=raw2[c][:], in_=w2[512 * c : 512 * c + 512, :].rearrange("(p t) n -> p t n", t=4))
+
+        load_w2(0)
         b2_bc = const.tile([P, D], BF16)
         nc.sync.dma_start(out=b2_bc[:], in_=b2.partition_broadcast(P))
         gamma_bc = const.tile([P, D], BF16)
         beta_bc = const.tile([P, D], BF16)
         nc.sync.dma_start(out=gamma_bc[:], in_=gamma.partition_broadcast(P))
         nc.sync.dma_start(out=beta_bc[:], in_=beta.partition_broadcast(P))
+        load_w2(1)
 
         blk = const.tile([P, 2, 8, NODES], F32)
         ps_e = w_pool.tile([P, 2, P], F32, tag="w")
@@ -301,8 +305,10 @@ def tile_simplegnn_pa_t_kernel(tc, h, adj_mask, w1a, w1b, b1, w2, b2, gamma, bet
         def a_unit(k):
             return k - LEAD if k >= LEAD else None
 
-        def new_z(k, c):
-            z[(k, c)] = zpool.tile([P, 4 * ROWS], BF16, tag="z%d" % c, name="z%d" % c, align_bytes=64, bufs=4)
+        QUARTER = 4 * N_A
+
+        def new_z(k):
+            z[k] = zpool.tile([P, 4 * QUARTER], BF16, tag="z", name="z%d" % k, align_bytes=64, bufs=4)
 
         pre = {}
 
@@ -328,46 +334,54 @@ def tile_simplegnn_pa_t_kernel(tc, h, adj_mask, w1a, w1b, b1, w2, b2, gamma, bet
         def relu_from_psum(k, c):
             if t_unit(k) is None:
                 return
-            for r in T_CHUNKS:
+            for x, r in enumerate(T_CHUNKS):
+                start = (2 + c) * QUARTER + 4 * P * x
                 nc.scalar.activation(
-                    out=z[(k, c)][:, 4 * P * r : 4 * P * (r + 1)].rearrange("p (r t) -> p r t", t=4),
+                    out=z[k][:, start : start + 4 * P].rearrange("p (r t) -> p r t", t=4),
                     in_=pre[(c, r)][:].rearrange("p t r -> p r t"),
                     func=ACT.Relu,
                 )
 
-        def sums_on_vector(k, c):
+        def sums_on_vector(k):
             au = a_unit(k)
             if au is None:
                 return
+            graphs = 2 * N_A // NODES
             nc.vector.tensor_tensor(
-                out=z[(k, c)][:, 0 : 4 * N_A].rearrange("p (g i t) -> p g i t", i=NODES, t=4),
-                in0=a_sb[:, c, :, :].rearrange("p (g i) t -> p g i t", i=NODES),
-                in1=b_sb[:, c, :, :]
-                .rearrange("p (g j) t -> p g j t", j=NODES)[:, :, au, :]
+                out=z[k][:, 0 : 2 * QUARTER].rearrange("p (g i t) -> p g i t", i=NODES, t=4),
+                in0=a_sb[:].rearrange("p c (g i) t -> p (c g) i t", i=NODES),
+                in1=b_sb[:]
+                .rearrange("p c (g j) t -> p (c g) j t", j=NODES)[:, :, au, :]
                 .unsqueeze(2)
-                .to_broadcast([P, N_A // NODES, NODES, 4]),
+                .to_broadcast([P, graphs, NODES, 4]),
                 op=ALU.add,
             )
 
-        def relu_in_place(k, c):
+        def relu_in_place(k):
             if a_unit(k) is not None:
-                nc.scalar.activation(out=z[(k, c)][:, 0 : 4 * N_A], in_=z[(k, c)][:, 0 : 4 * N_A], func=ACT.Relu)
+                part = z[k][:, 0 : 2 * QUARTER]
+                if k == LEAD:
+                    nc.vector.tensor_scalar_max(out=part, in0=part, scalar1=0.0)
+                else:
+                    nc.scalar.activation(out=part, in_=part, func=ACT.Relu)
 
-        def quantise_z(k, c):
-            zq[(k, c)] = zpool.tile([P, ROWS], U32, tag="zq%d" % c, name="zq%d" % c, align_bytes=256, bufs=6)
-            zs[(k, c)] = zpool.tile([P, ROWS], U8, tag="zs%d" % c, name="zs%d" % c, align_bytes=256, bufs=6)
-            lo = N_A if a_unit(k) is None else 0
-            hi = N_A if t_unit(k) is None else ROWS
+        def quantise_z(k):
+            zq[k] = zpool.tile([P, QUARTER], U32, tag="zq", name="zq%d" % k, align_bytes=256, bufs=6)
+            zs[k] = zpool.tile([P, QUARTER], U8, tag="zs", name="zs%d" % k, align_bytes=256, bufs=6)
+            lo = QUARTER // 2 if a_unit(k) is None else 0
+            hi = QUARTER // 2 if t_unit(k) is None else QUARTER
             nc.vector.quantize_mx(
-                out=zq[(k, c)][:, lo:hi].bitcast(FP8X4), scales=zs[(k, c)][:, lo:hi], in_=z[(k, c)][:, 4 * lo : 4 * hi]
+                out=zq[k][:, lo:hi].bitcast(FP8X4), scales=zs[k][:, lo:hi], in_=z[k][:, 4 * lo : 4 * hi]
             )
 
         def mx_pass(dst, k, c, r, start, stop):
-            cols = slice(P * r, P * r + P)
+            route, x = divmod(r, 2)
+            first = (2 * route + c) * N_A + P * x
+            cols = slice(first, first + P)
             nc.tensor.matmul_mx(
                 out=dst,
-                lhsT=zq[(k, c)][:, cols].bitcast(FP8X4),
-                lhsT_scale=zs[(k, c)][:, cols],
+                lhsT=zq[k][:, cols].bitcast(FP8X4),
+                lhsT_scale=zs[k][:, cols],
                 rhs=w2q[:, c, :].bitcast(FP8X4),
                 rhs_scale=w2s[:, c, :],
                 start=start,
@@ -471,7 +485,7 @@ def tile_simplegnn_pa_t_kernel(tc, h, adj_mask, w1a, w1b, b1, w2, b2, gamma, bet
         first_layer_out_t("a", 0)
         first_layer_t("b", 0)
         regroup_w1("a", 1, "s", 2, 4)
-        new_z(0, 0)
+        new_z(0)
         sums_on_tensor(0, 0)
         first_layer_out_t("b", 0)
         regroup_w1("b", 1, "s", 2, 4)
@@ -487,46 +501,36 @@ def tile_simplegnn_pa_t_kernel(tc, h, adj_mask, w1a, w1b, b1, w2, b2, gamma, bet
         first_layer_out_a(0)
         first_layer_out_t("b", 1)
         move_neighbours(0, "v")
-        new_z(0, 1)
         sums_on_tensor(0, 1)
-        new_z(1, 0)
+        new_z(1)
         sums_on_tensor(1, 0)
         relu_from_psum(0, 1)
         relu_from_psum(1, 0)
         first_layer_a(1)
-        new_z(1, 1)
         sums_on_tensor(1, 1)
         move_neighbours(1, "v")
         move_neighbours(2, "v")
         regroup_w2(0, "v")
-        regroup_w2(1, "v")
+        regroup_w2(1, "g")
         first_layer_out_a(1)
         relu_from_psum(1, 1)
         mask_scalars()
         quantise_w2(0)
         for k in (2, 3, 4, 5):
-            for c in range(2):
-                new_z(k, c)
+            new_z(k)
         for c in range(2):
             sums_on_tensor(2, c)
             relu_from_psum(2, c)
-        sums_on_vector(2, 0)
-        sums_on_vector(2, 1)
-        for c in range(2):
-            relu_in_place(2, c)
+            move_neighbours(3 + c, "s")
+        sums_on_vector(2)
+        relu_in_place(2)
         for k in range(2):
-            for c in range(2):
-                quantise_z(k, c)
+            quantise_z(k)
         quantise_w2(1)
-        move_neighbours(3, "v")
-        move_neighbours(4, "v")
-        sums_on_vector(3, 0)
-        sums_on_vector(3, 1)
-        for c in range(2):
-            quantise_z(2, c)
+        sums_on_vector(3)
+        quantise_z(2)
         for k in (4, 5):
-            for c in range(2):
-                sums_on_vector(k, c)
+            sums_on_vector(k)
         def finish_t():
             for r in T_CHUNKS:
                 add_scaled(r, g_t[r][:], 1.0 / NODES, False, True)
@@ -542,8 +546,7 @@ def tile_simplegnn_pa_t_kernel(tc, h, adj_mask, w1a, w1b, b1, w2, b2, gamma, bet
                 if k + 2 < NODES:
                     move_neighbours(k + 2, "s")
             for k in ahead:
-                for c in range(2):
-                    relu_in_place(k, c)
+                relu_in_place(k)
             for k in pair:
                 second_layer_t(k)
                 second_layer_a(k)
@@ -551,11 +554,9 @@ def tile_simplegnn_pa_t_kernel(tc, h, adj_mask, w1a, w1b, b1, w2, b2, gamma, bet
                 if k == 0:
                     for r in T_CHUNKS:
                         add_scaled(r, self_t[r][:], degm1[:, r : r + 1], True, False)
-                for kk in [k0 + 6 + n]:
-                    if kk < rounds and n == 0:
-                        for c in range(2):
-                            new_z(kk, c)
-                            sums_on_vector(kk, c)
+                if n == 0 and k + 6 < rounds:
+                    new_z(k + 6)
+                    sums_on_vector(k + 6)
                 if 8 <= k < 8 + CHUNKS:
                     add_scaled(k - 8, b2_bc[:], deg16[:, k - 8 : k - 7], False, False)
                 if t_unit(k) == NODES - 1:
@@ -565,15 +566,15 @@ def tile_simplegnn_pa_t_kernel(tc, h, adj_mask, w1a, w1b, b1, w2, b2, gamma, bet
                     ln_aside(T_CHUNKS[0])
                     ln_centre(T_CHUNKS[1])
                     ln_finish(T_CHUNKS[1])
-                if k + 3 < rounds:
-                    for c in range(2):
-                        quantise_z(k + 3, c)
-            if True:
-                for kk in range(k0 + 6 + 1, k0 + 9):
-                    if kk < rounds:
-                        for c in range(2):
-                            new_z(kk, c)
-                            sums_on_vector(kk, c)
+                if 0 < k0 < rounds - 3:
+                    quantise_z(k + 3)
+            if k0 == 0:
+                for k in ahead:
+                    quantise_z(k)
+            for k in range(k0 + 7, k0 + 9):
+                if k < rounds:
+                    new_z(k)
+                    sums_on_vector(k)
         for r in A_CHUNKS:
             ln_stats(r)
         for r in A_CHUNKS:

@@ -50,6 +50,7 @@ def tile_simplegnn_pa_t_kernel(tc, h, adj_mask, w1a, w1b, b1, w2, b2, gamma, bet
         nc.scalar.sqrt(out=warm2[:], in_=warm[:])
         ident = const.tile([P, P], F32)
         make_identity(nc, ident[:])
+        nc.gpsimd.memset(b1_row[:].bitcast(F32), 0.0)
         ones = const.tile([P, P], BF16)
         nc.vector.memset(ones[:], 1.0)
         ident_d = const.tile([P, 8, 2 * NODES], F32)
@@ -66,7 +67,6 @@ def tile_simplegnn_pa_t_kernel(tc, h, adj_mask, w1a, w1b, b1, w2, b2, gamma, bet
             nc.vector.tensor_copy(out=sel2[:, u, :], in_=i16d[:, u : u + NODES])
         bd8 = const.tile([P, 8], F32)
         nc.vector.tensor_reduce(out=bd8[:], in_=ident_v, axis=AX.X, op=ALU.add)
-        nc.vector.memset(b1_row[:].bitcast(F32), 0.0)
 
         mask_sb = const.tile([P, CHUNKS, NODES], BF16)
         with nc.allow_non_contiguous_dma(reason="small mask table"):
@@ -497,25 +497,25 @@ def tile_simplegnn_pa_t_kernel(tc, h, adj_mask, w1a, w1b, b1, w2, b2, gamma, bet
         regroup_w1("b", 1, "v", 0, 2)
         quantise_w1("b", 1)
         first_layer_t("b", 1)
-        first_layer_out_t("a", 1)
-        first_layer_out_a(0)
-        first_layer_out_t("b", 1)
         move_neighbours(0, "v")
-        sums_on_tensor(0, 1)
+        first_layer_out_a(0)
+        first_layer_out_t("a", 1)
+        first_layer_out_t("b", 1)
         new_z(1)
         sums_on_tensor(1, 0)
-        relu_from_psum(0, 1)
+        sums_on_tensor(0, 1)
         relu_from_psum(1, 0)
+        relu_from_psum(0, 1)
         first_layer_a(1)
         sums_on_tensor(1, 1)
         move_neighbours(1, "v")
         move_neighbours(2, "v")
         regroup_w2(0, "v")
         regroup_w2(1, "g")
-        first_layer_out_a(1)
-        relu_from_psum(1, 1)
         mask_scalars()
         quantise_w2(0)
+        first_layer_out_a(1)
+        relu_from_psum(1, 1)
         for k in (2, 3, 4, 5):
             new_z(k)
         for c in range(2):

from contextlib import ExitStack

import concourse.mybir as mybir
from concourse.masks import make_identity

F32 = mybir.dt.float32
BF16 = mybir.dt.bfloat16
U32 = mybir.dt.uint32
U8 = mybir.dt.uint8
FP8X4 = mybir.dt.float8_e4m3fn_x4
ALU = mybir.AluOpType
ACT = mybir.ActivationFunctionType
AX = mybir.AxisListType

P = 128
NODES = 16
D = 512
F = 1024
ROWS = 512
CHUNKS = 4
EPS = 1e-5
FLOPS = 2 * ROWS * D * F * 2 + 2 * ROWS * NODES * F * D
A_CHUNKS = (0, 1)
T_CHUNKS = (2, 3)
N_A = 256
LEAD = 2


def tile_simplegnn_pa_t_kernel(tc, h, adj_mask, w1a, w1b, b1, w2, b2, gamma, beta, out):
    nc = tc.nc
    h_flat = h.flatten_outer_dims()
    adj_flat = adj_mask.flatten_outer_dims()
    out_flat = out.flatten_outer_dims()
    w1 = {"a": w1a, "b": w1b}

    with ExitStack() as ctx:
        const = ctx.enter_context(tc.tile_pool(name="const", bufs=1))
        zpool = ctx.enter_context(tc.tile_pool(name="zpool", bufs=4))
        small = ctx.enter_context(tc.tile_pool(name="small", bufs=4))
        movepool = ctx.enter_context(tc.tile_pool(name="move", bufs=8))
        w_pool = ctx.enter_context(tc.psum_pool(name="w", bufs=6))
        g_pool = ctx.enter_context(tc.psum_pool(name="g", bufs=2))
        ctx.enter_context(tc.manual_schedule())
        ctx.enter_context(nc.allow_low_precision(reason="zeros and ones: sums with at most one one are exact in bfloat16"))

        b1_row = const.tile([P, F], BF16)
        warm = const.tile([P, 1], F32)
        nc.vector.memset(warm[:], 1.0)
        warm2 = const.tile([P, 1], F32)
        nc.scalar.sqrt(out=warm2[:], in_=warm[:])
        ident = const.tile([P, P], F32)
        make_identity(nc, ident[:])
        nc.gpsimd.memset(b1_row[:].bitcast(F32), 0.0)
        ones = const.tile([P, P], BF16)
        nc.vector.memset(ones[:], 1.0)
        ident_d = const.tile([P, 8, 2 * NODES], F32)
        ident_v = ident[:].rearrange("p (g i) -> p g i", i=NODES)
        nc.vector.tensor_copy(out=ident_d[:, :, 0:NODES], in_=ident_v)
        nc.vector.tensor_copy(out=ident_d[:, :, NODES : 2 * NODES], in_=ident_v)
        i16d = const.tile([P, 2 * NODES], BF16)
        nc.vector.tensor_reduce(
            out=i16d[:, 0:NODES], in_=ident[:].rearrange("p (g i) -> p i g", i=NODES), axis=AX.X, op=ALU.add
        )
        nc.vector.tensor_copy(out=i16d[:, NODES : 2 * NODES], in_=i16d[:, 0:NODES])
        sel2 = const.tile([P, NODES, NODES], BF16)
        for u in range(NODES):
            nc.vector.tensor_copy(out=sel2[:, u, :], in_=i16d[:, u : u + NODES])
        bd8 = const.tile([P, 8], F32)
        nc.vector.tensor_reduce(out=bd8[:], in_=ident_v, axis=AX.X, op=ALU.add)

        mask_sb = const.tile([P, CHUNKS, NODES], BF16)
        with nc.allow_non_contiguous_dma(reason="small mask table"):
            nc.sync.dma_start(out=mask_sb[:], in_=adj_flat.rearrange("(r p) j -> p r j", p=P))
        h_sb = const.tile([P, CHUNKS, D], BF16)
        nc.sync.dma_start(out=h_sb[:], in_=h_flat.rearrange("(r p) d -> p r d", p=P))
        raw1 = {}
        for o in ("a", "b"):
            for c in range(2):
                raw1[(o, c)] = const.tile([P, 4, 512], BF16, name="raw1%s%d" % (o, c))

        def load_w1(o, c):
            for u in range(2):
                nc.sync.dma_start(
                    out=raw1[(o, c)][:, 2 * u : 2 * u + 2, :],
                    in_=w1[o][256 * u : 256 * u + 256, 512 * c : 512 * c + 512].rearrange("(q e) f -> q e f", e=2),
                )

        load_w1("a", 0)
        load_w1("b", 0)
        nc.sync.dma_start(out=b1_row[0:1, :], in_=b1.unsqueeze(0))
        load_w1("a", 1)
        load_w1("b", 1)
        raw2 = {}

        def load_w2(c):
            raw2[c] = const.tile([P, 4, D], BF16, name="raw2%d" % c)
            nc.sync.dma_start(out=raw2[c][:], in_=w2[512 * c : 512 * c + 512, :].rearrange("(p t) n -> p t n", t=4))

        load_w2(0)
        b2_bc = const.tile([P, D], BF16)
        nc.sync.dma_start(out=b2_bc[:], in_=b2.partition_broadcast(P))
        gamma_bc = const.tile([P, D], BF16)
        beta_bc = const.tile([P, D], BF16)
        nc.sync.dma_start(out=gamma_bc[:], in_=gamma.partition_broadcast(P))
        nc.sync.dma_start(out=beta_bc[:], in_=beta.partition_broadcast(P))
        load_w2(1)

        blk = const.tile([P, 2, 8, NODES], F32)
        ps_e = w_pool.tile([P, 2, P], F32, tag="w")
        for x, r in enumerate(T_CHUNKS):
            nc.vector.tensor_tensor(
                out=blk[:, x, :, :],
                in0=bd8[:].unsqueeze(2).to_broadcast([P, 8, NODES]),
                in1=mask_sb[:, r, :].unsqueeze(1).to_broadcast([P, 8, NODES]),
                op=ALU.mult,
            )
            nc.tensor.transpose(ps_e[:, x, :], blk[:, x, :, :].rearrange("p g j -> p (g j)"), ident[:])

        def rotate_rows(dst, src):
            prod = small.tile([P, 2, NODES, NODES], BF16, tag="prod")
            for x in range(2):
                nc.vector.tensor_tensor(
                    out=prod[:, x, :, :], in0=sel2[:], in1=src[:, x, :].unsqueeze(1).to_broadcast([P, NODES, NODES]), op=ALU.mult
                )
            nc.vector.tensor_reduce(out=dst, in_=prod[:], axis=AX.X, op=ALU.add)


        gh = const.tile([P, 4 * ROWS], BF16, align_bytes=64)
        ghw = gh[:].bitcast(F32).rearrange("p (r u) -> p r u", u=2)
        for half in range(2):
            ps_h = w_pool.tile([P, 2, 2, P], F32, tag="w")
            for l in range(2):
                r = 2 * half + l
                for u in range(2):
                    nc.tensor.transpose(
                        ps_h[:, l, u, :], h_sb[:, r, :].bitcast(F32)[:, u * P : (u + 1) * P], ident[:]
                    )
            for l in range(2):
                r = 2 * half + l
                nc.scalar.copy(out=ghw[:, r * P : (r + 1) * P, :], in_=ps_h[:, l, :, :].rearrange("p u r -> p r u"))
        b1_bc = const.tile([P, F], BF16)
        b1f = const.tile([P, 2, 4], F32)
        ps_f = w_pool.tile([P, 2, 4], F32, tag="w")
        ps_bs = []
        for c in range(2):
            ps_b = g_pool.tile([P, 512], F32, tag="g", name="ps_b%d" % c)
            nc.tensor.matmul(out=ps_b[:], lhsT=ones[:], rhs=b1_row[:, 512 * c : 512 * c + 512], start=True, stop=True)
            ps_bs.append(ps_b)
            for t in range(4):
                nc.tensor.matmul(
                    out=ps_f[:, c, t : t + 1], lhsT=b1_row[:, 512 * c + t : 512 * c + 512 : 4], rhs=ones[:, 0:1],
                    start=True, stop=True,
                )

        def spread_b1():
            for c in range(2):
                nc.scalar.copy(out=b1_bc[:, 512 * c : 512 * c + 512], in_=ps_bs[c][:])
            nc.scalar.copy(out=b1f[:], in_=ps_f[:])

        hq = const.tile([P, ROWS], U32, align_bytes=64)
        hs = const.tile([P, ROWS], U8, align_bytes=64)

        adj_t = const.tile([P, 2, NODES], BF16)
        nc.vector.tensor_reduce(
            out=adj_t[:], in_=ps_e[:].rearrange("p x (g i) -> p x i g", i=NODES), axis=AX.X, op=ALU.add
        )
        mt = const.tile([P, 2, NODES], F32)
        rotate_rows(mt[:], adj_t[:])

        move = {}

        def move_neighbours(u, eng):
            move[u] = movepool.tile([P, 2, P], F32, tag="move", name="move%d" % u)
            for x in range(2):
                dst = move[u][:, x, :].rearrange("p (g i) -> p g i", i=NODES)
                if eng == "v":
                    nc.vector.tensor_scalar_mul(out=dst, in0=ident_d[:, :, u : u + NODES], scalar1=mt[:, x, u : u + 1])
                else:
                    nc.scalar.activation(out=dst, in_=ident_d[:, :, u : u + NODES], func=ACT.Copy, scale=mt[:, x, u : u + 1])

        w1q = {}
        w1s = {}
        g1 = {}
        for o in ("a", "b"):
            w1q[o] = const.tile([P, F], U32, name="w1q" + o, align_bytes=64)
            w1s[o] = const.tile([P, F], U8, name="w1s" + o, align_bytes=64)
            for c in range(2):
                g1[(o, c)] = const.tile([P, 2048], BF16, name="g1%s%d" % (o, c), align_bytes=64)

        def regroup_w1(o, c, eng, lo=0, hi=4):
            dst = g1[(o, c)][:].rearrange("q (t p k) -> q t p k", t=4, p=P, k=4)[:, lo:hi, :, :].rearrange("q t p k -> q p k t")
            src = raw1[(o, c)][:].rearrange("q k (p t) -> q p k t", t=4)[:, :, :, lo:hi]
            if eng == "v":
                nc.vector.tensor_copy(out=dst, in_=src)
            else:
                nc.scalar.copy(out=dst, in_=src)

        def quantise_w1(o, c):
            cols = slice(512 * c, 512 * c + 512)
            nc.vector.quantize_mx(out=w1q[o][:, cols].bitcast(FP8X4), scales=w1s[o][:, cols], in_=g1[(o, c)][:])

        a_sb = const.tile([P, 2, N_A, 4], F32)
        b_sb = const.tile([P, 2, N_A, 4], F32)
        xa = {}
        xb = {}
        for r in T_CHUNKS:
            xa[r] = const.tile([P, 2, 4, P], F32, name="xa%d" % r)
            xb[r] = const.tile([P, 2, 4, P], F32, name="xb%d" % r)

        def mx_lone(dst, lq, ls, lcols, rq, rs, rcols):
            nc.tensor.matmul_mx(
                out=dst,
                lhsT=lq[:, lcols].bitcast(FP8X4),
                lhsT_scale=ls[:, lcols],
                rhs=rq[:, rcols].bitcast(FP8X4),
                rhs_scale=rs[:, rcols],
                start=True,
                stop=True,
            )

        banks = {}

        def first_layer_t(o, c):
            pool, tag = (w_pool, "w") if o == "a" else (g_pool, "g")
            for r in T_CHUNKS:
                banks[(o, r, c)] = pool.tile([P, 4, P], F32, tag=tag, name="fx%s%d%d" % (o, r, c))
                mx_lone(
                    banks[(o, r, c)][:].rearrange("p t f -> p (t f)"), hq, hs, slice(P * r, P * r + P),
                    w1q[o], w1s[o], slice(512 * c, 512 * c + 512),
                )

        def first_layer_out_t(o, c):
            for r in T_CHUNKS:
                if o == "b":
                    nc.scalar.copy(out=xb[r][:, c, :, :], in_=banks[(o, r, c)][:])
                else:
                    nc.vector.tensor_tensor(
                        out=xa[r][:, c, :, :],
                        in0=banks[(o, r, c)][:],
                        in1=b1_bc[:, 512 * c : 512 * c + 512].rearrange("q (p t) -> q t p", t=4),
                        op=ALU.add,
                    )

        def first_layer_a(c):
            for r in A_CHUNKS:
                for o, pool, tag in (("a", w_pool, "w"), ("b", w_pool, "w")):
                    banks[(o, r, c)] = pool.tile([P, 4, P], F32, tag=tag, name="fl%s%d%d" % (o, r, c))
                    for t in range(4):
                        mx_lone(
                            banks[(o, r, c)][:, t, :], w1q[o], w1s[o], slice(512 * c + P * t, 512 * c + P * t + P),
                            hq, hs, slice(P * r, P * r + P),
                        )

        def first_layer_out_a(c):
            for r in A_CHUNKS:
                rows = slice(P * r, P * r + P)
                nc.scalar.copy(out=a_sb[:, c, rows, :], in_=banks[("a", r, c)][:].rearrange("p t r -> p r t"))
                nc.vector.tensor_tensor(
                    out=b_sb[:, c, rows, :],
                    in0=banks[("b", r, c)][:].rearrange("p t r -> p r t"),
                    in1=b1f[:, c, :].unsqueeze(1).to_broadcast([P, P, 4]),
                    op=ALU.add,
                )

        w2q = const.tile([P, 2, D], U32, align_bytes=256)
        w2s = const.tile([P, 2, D], U8, align_bytes=256)
        g2 = {}
        for c in range(2):
            g2[c] = const.tile([P, 2048], BF16, name="g2%d" % c, align_bytes=64)

        def regroup_w2(c, eng):
            dst = g2[c][:].rearrange("p (m i t) -> p m t i", i=4, t=4)
            srcv = raw2[c][:].rearrange("p t (m i) -> p m t i", i=4)
            if eng == "v":
                nc.vector.tensor_copy(out=dst, in_=srcv)
            elif eng == "s":
                nc.scalar.copy(out=dst, in_=srcv)
            else:
                nc.gpsimd.tensor_scalar(out=dst, in0=srcv, scalar1=1.0, scalar2=0.0, op0=ALU.mult, op1=ALU.add)

        def quantise_w2(c):
            nc.vector.quantize_mx(out=w2q[:, c, :].bitcast(FP8X4), scales=w2s[:, c, :], in_=g2[c][:])

        acc = const.tile([P, CHUNKS, D], F32)
        mask16 = const.tile([P, CHUNKS, NODES], F32)
        deg16 = const.tile([P, CHUNKS], F32)
        degm1 = const.tile([P, CHUNKS], F32)

        def mask_scalars():
            nc.vector.tensor_scalar_mul(out=mask16[:], in0=mask_sb[:], scalar1=1.0 / NODES)
            nc.vector.tensor_reduce(out=deg16[:], in_=mask16[:], axis=AX.X, op=ALU.add)
            nc.vector.tensor_scalar_add(out=degm1[:], in0=deg16[:], scalar1=-1.0)

        rounds = NODES + max(1, LEAD)
        z = {}
        zq = {}
        zs = {}
        g_t = {}
        self_t = {}
        T_SLOTS = ((2, 0), (3, 0), (2, 1), (3, 1))

        def t_unit(k):
            return k - 1 if k <= NODES else None

        def a_unit(k):
            return k - LEAD if k >= LEAD else None

        QUARTER = 4 * N_A

        def new_z(k):
            z[k] = zpool.tile([P, 4 * QUARTER], BF16, tag="z", name="z%d" % k, align_bytes=64, bufs=4)

        pre = {}

        def sums_on_tensor(k, c):
            tu = t_unit(k)
            if tu is None:
                return
            for x, r in enumerate(T_CHUNKS):
                pre[(c, r)] = w_pool.tile([P, 4, P], F32, tag="w", name="pre%d%d" % (c, r))
                for t in range(4):
                    if tu < 0:
                        nc.tensor.transpose(pre[(c, r)][:, t, :], xa[r][:, c, t, :], ident[:])
                        continue
                    nc.tensor.matmul(
                        out=pre[(c, r)][:, t, :], lhsT=xb[r][:, c, t, :], rhs=move[tu][:, x, :],
                        is_transpose=True, start=True, stop=False,
                    )
                    nc.tensor.matmul(
                        out=pre[(c, r)][:, t, :], lhsT=xa[r][:, c, t, :], rhs=ident[:],
                        is_transpose=True, start=False, stop=True,
                    )

        def relu_from_psum(k, c):
            if t_unit(k) is None:
                return
            for x, r in enumerate(T_CHUNKS):
                start = (2 + c) * QUARTER + 4 * P * x
                nc.scalar.activation(
                    out=z[k][:, start : start + 4 * P].rearrange("p (r t) -> p r t", t=4),
                    in_=pre[(c, r)][:].rearrange("p t r -> p r t"),
                    func=ACT.Relu,
                )

        def sums_on_vector(k):
            au = a_unit(k)
            if au is None:
                return
            graphs = 2 * N_A // NODES
            nc.vector.tensor_tensor(
                out=z[k][:, 0 : 2 * QUARTER].rearrange("p (g i t) -> p g i t", i=NODES, t=4),
                in0=a_sb[:].rearrange("p c (g i) t -> p (c g) i t", i=NODES),
                in1=b_sb[:]
                .rearrange("p c (g j) t -> p (c g) j t", j=NODES)[:, :, au, :]
                .unsqueeze(2)
                .to_broadcast([P, graphs, NODES, 4]),
                op=ALU.add,
            )

        def relu_in_place(k):
            if a_unit(k) is not None:
                part = z[k][:, 0 : 2 * QUARTER]
                if k == LEAD:
                    nc.vector.tensor_scalar_max(out=part, in0=part, scalar1=0.0)
                else:
                    nc.scalar.activation(out=part, in_=part, func=ACT.Relu)

        def quantise_z(k):
            zq[k] = zpool.tile([P, QUARTER], U32, tag="zq", name="zq%d" % k, align_bytes=256, bufs=6)
            zs[k] = zpool.tile([P, QUARTER], U8, tag="zs", name="zs%d" % k, align_bytes=256, bufs=6)
            lo = QUARTER // 2 if a_unit(k) is None else 0
            hi = QUARTER // 2 if t_unit(k) is None else QUARTER
            nc.vector.quantize_mx(
                out=zq[k][:, lo:hi].bitcast(FP8X4), scales=zs[k][:, lo:hi], in_=z[k][:, 4 * lo : 4 * hi]
            )

        def mx_pass(dst, k, c, r, start, stop):
            route, x = divmod(r, 2)
            first = (2 * route + c) * N_A + P * x
            cols = slice(first, first + P)
            nc.tensor.matmul_mx(
                out=dst,
                lhsT=zq[k][:, cols].bitcast(FP8X4),
                lhsT_scale=zs[k][:, cols],
                rhs=w2q[:, c, :].bitcast(FP8X4),
                rhs_scale=w2s[:, c, :],
                start=start,
                stop=stop,
            )

        ms = {}

        def second_layer_a(k):
            if a_unit(k) is None:
                return
            for r in A_CHUNKS:
                ms[(k, r)] = w_pool.tile([P, D], F32, tag="w", name="m%d" % r)
                for c in range(2):
                    mx_pass(ms[(k, r)][:], k, c, r, c == 0, c == 1)

        def second_layer_t(k):
            tu = t_unit(k)
            if tu is None:
                return
            for r in T_CHUNKS:
                if tu < 0:
                    self_t[r] = w_pool.tile([P, D], F32, tag="w", name="self%d" % r)
                    for c in range(2):
                        mx_pass(self_t[r][:], k, c, r, c == 0, c == 1)
                    continue
                if tu == 0:
                    g_t[r] = g_pool.tile([P, D], F32, tag="g", name="gt%d" % r)
                for c in range(2):
                    mx_pass(g_t[r][:], k, c, r, tu == 0 and c == 0, tu == NODES - 1 and c == 1)

        sums = {}

        def add_scaled(r, src, factor, first, last):
            kw = {}
            if last:
                sums[r] = small.tile([P, 1], F32, tag="sum", name="sum%d" % r)
                kw["accum_out"] = sums[r][:]
            nc.vector.scalar_tensor_tensor(
                out=acc[:, r, :], in0=src, scalar=factor, in1=h_sb[:, r, :] if first else acc[:, r, :],
                op0=ALU.mult, op1=ALU.add, **kw
            )

        def add_messages(k):
            au = a_unit(k)
            if au is None:
                return
            for r in A_CHUNKS:
                add_scaled(r, ms[(k, r)][:], mask16[:, r, au : au + 1], au == 0, au == NODES - 1)

        negmu = {}
        sd = {}
        y = {}

        def ln_stats(r):
            negmu[r] = small.tile([P, 1], F32, tag="negmu", name="negmu%d" % r)
            nc.vector.tensor_scalar_mul(out=negmu[r][:], in0=sums[r][:], scalar1=-1.0 / D)
            junk = small.tile([P, D], F32, tag="junk", name="junk", bufs=2)
            sq = small.tile([P, 1], F32, tag="sq", name="sq%d" % r)
            nc.scalar.activation(out=junk[:], in_=acc[:, r, :], func=ACT.Square, bias=negmu[r][:], accum_out=sq[:])
            sd[r] = small.tile([P, 1], F32, tag="sd", name="sd%d" % r)
            nc.scalar.activation(out=sd[r][:], in_=sq[:], func=ACT.Sqrt, scale=1.0 / D, bias=EPS)

        def ln_centre(r):
            y[r] = small.tile([P, D], F32, tag="y", name="y%d" % r, bufs=4)
            nc.vector.scalar_tensor_tensor(
                out=y[r][:], in0=acc[:, r, :], scalar=negmu[r][:], in1=gamma_bc[:], op0=ALU.add, op1=ALU.mult
            )

        def ln_aside(r):
            rstd = small.tile([P, 1], F32, tag="rstd", name="rstd%d" % r)
            nc.vector.reciprocal(out=rstd[:], in_=sd[r][:])
            shift = small.tile([P, 1], F32, tag="shift", name="shift%d" % r)
            nc.vector.tensor_scalar_mul(out=shift[:], in0=negmu[r][:], scalar1=rstd[:])
            y[r] = small.tile([P, D], F32, tag="y", name="y%d" % r, bufs=4)
            nc.scalar.activation(out=y[r][:], in_=acc[:, r, :], func=ACT.Identity, scale=rstd[:], bias=shift[:])
            nc.gpsimd.tensor_tensor(out=y[r][:], in0=y[r][:], in1=gamma_bc[:], op=ALU.mult)
            nc.gpsimd.tensor_tensor(out=y[r][:], in0=y[r][:], in1=beta_bc[:], op=ALU.add)
            nc.gpsimd.dma_start(out=out_flat[P * r : P * r + P, :], in_=y[r][:])

        def ln_finish(r, width=D):
            rstd = small.tile([P, 1], F32, tag="rstd", name="rstd%d" % r)
            nc.vector.reciprocal(out=rstd[:], in_=sd[r][:])
            y2 = small.tile([P, D], F32, tag="y2", name="y2%d" % r, bufs=4)
            for lo in range(0, D, width):
                cols = slice(lo, lo + width)
                nc.vector.scalar_tensor_tensor(
                    out=y2[:, cols], in0=y[r][:, cols], scalar=rstd[:], in1=beta_bc[:, cols], op0=ALU.mult, op1=ALU.add
                )
                nc.sync.dma_start(out=out_flat[P * r : P * r + P, cols], in_=y2[:, cols])

        for o in ("a", "b"):
            regroup_w1(o, 0, "v", 0, 3)
            regroup_w1(o, 0, "s", 3, 4)
            if o == "a":
                nc.vector.quantize_mx(out=hq[:].bitcast(FP8X4), scales=hs[:], in_=gh[:])
                quantise_w1("a", 0)
                first_layer_t("a", 0)
        spread_b1()
        quantise_w1("b", 0)
        first_layer_out_t("a", 0)
        first_layer_t("b", 0)
        regroup_w1("a", 1, "s", 2, 4)
        new_z(0)
        sums_on_tensor(0, 0)
        first_layer_out_t("b", 0)
        regroup_w1("b", 1, "s", 2, 4)
        relu_from_psum(0, 0)
        regroup_w1("a", 1, "v", 0, 2)
        quantise_w1("a", 1)
        first_layer_a(0)
        first_layer_t("a", 1)
        regroup_w1("b", 1, "v", 0, 2)
        quantise_w1("b", 1)
        first_layer_t("b", 1)
        move_neighbours(0, "v")
        first_layer_out_a(0)
        first_layer_out_t("a", 1)
        first_layer_out_t("b", 1)
        new_z(1)
        sums_on_tensor(1, 0)
        sums_on_tensor(0, 1)
        relu_from_psum(1, 0)
        relu_from_psum(0, 1)
        first_layer_a(1)
        sums_on_tensor(1, 1)
        move_neighbours(1, "v")
        move_neighbours(2, "v")
        regroup_w2(0, "v")
        regroup_w2(1, "g")
        mask_scalars()
        quantise_w2(0)
        first_layer_out_a(1)
        relu_from_psum(1, 1)
        for k in (2, 3, 4, 5):
            new_z(k)
        for c in range(2):
            sums_on_tensor(2, c)
            relu_from_psum(2, c)
            move_neighbours(3 + c, "s")
        sums_on_vector(2)
        relu_in_place(2)
        for k in range(2):
            quantise_z(k)
        quantise_w2(1)
        sums_on_vector(3)
        quantise_z(2)
        for k in (4, 5):
            sums_on_vector(k)
        def finish_t():
            for r in T_CHUNKS:
                add_scaled(r, g_t[r][:], 1.0 / NODES, False, True)
                ln_stats(r)

        for k0 in range(0, rounds, 3):
            pair = [k for k in range(k0, k0 + 3) if k < rounds]
            ahead = [k for k in range(k0 + 3, k0 + 6) if k < rounds]
            for k in ahead:
                for c in range(2):
                    sums_on_tensor(k, c)
                    relu_from_psum(k, c)
                if k + 2 < NODES:
                    move_neighbours(k + 2, "s")
            for k in ahead:
                relu_in_place(k)
            for k in pair:
                second_layer_t(k)
                second_layer_a(k)
            for n, k in enumerate(pair):
                if k == 0:
                    for r in T_CHUNKS:
                        add_scaled(r, self_t[r][:], degm1[:, r : r + 1], True, False)
                if n == 0 and k + 6 < rounds:
                    new_z(k + 6)
                    sums_on_vector(k + 6)
                if 8 <= k < 8 + CHUNKS:
                    add_scaled(k - 8, b2_bc[:], deg16[:, k - 8 : k - 7], False, False)
                if t_unit(k) == NODES - 1:
                    finish_t()
                add_messages(k)
                if t_unit(k) == NODES - 1:
                    ln_aside(T_CHUNKS[0])
                    ln_centre(T_CHUNKS[1])
                    ln_finish(T_CHUNKS[1])
                if 0 < k0 < rounds - 3:
                    quantise_z(k + 3)
            if k0 == 0:
                for k in ahead:
                    quantise_z(k)
            for k in range(k0 + 7, k0 + 9):
                if k < rounds:
                    new_z(k)
                    sums_on_vector(k)
        for r in A_CHUNKS:
            ln_stats(r)
        for r in A_CHUNKS:
            ln_centre(r)
        for r in A_CHUNKS:
            ln_finish(r)
